import numpy as np
import ml_dtypes


def mxq(x, axis, fmt="e4m3"):
    dtype, down = {"e4m3": (ml_dtypes.float8_e4m3fn, 7), "e5m2": (ml_dtypes.float8_e5m2, 14)}[fmt]
    v = np.moveaxis(np.asarray(x, np.float32).astype(ml_dtypes.bfloat16).astype(np.float64), axis, -1)
    blocks = v.reshape(v.shape[:-1] + (-1, 32))
    amax = np.abs(blocks).max(-1, keepdims=True)
    byte = np.maximum(np.where(amax > 0, np.frexp(amax)[1] - 1 + 127, 0) - down, 1)
    scale = np.exp2(byte - 127.0)
    codes = (blocks / scale).astype(np.float32).astype(dtype).astype(np.float64)
    return np.moveaxis((codes * scale).reshape(v.shape), -1, axis)


WIDE = False


def mx_kscale(k):
    if not WIDE:
        return np.ones(k)
    levels = np.array([10, -10, 5, -5, 0])
    a = np.random.permutation(np.resize(levels, k // 512 * 4)).reshape(k // 512, 4)
    idx = np.arange(k)
    return np.exp2(a[idx // 512, idx % 128 // 32])


BF16 = ml_dtypes.bfloat16


def bf(x):
    return np.asarray(x, np.float32).astype(BF16)


def f64(x):
    return np.asarray(x).astype(np.float64)


B, D, O1, O2, O3 = 4096, 768, 1024, 512, 128
EPS = 1e-5


def mish(v):
    return v * np.tanh(np.log(1.0 + np.exp(v)))


def sigmoid(v):
    return 1.0 / (1.0 + np.exp(-v))


def ln(u, g, b):
    mu = u.mean(-1, keepdims=True)
    var = np.square(u - mu).mean(-1, keepdims=True)
    return (u - mu) * (1.0 / np.sqrt(var + EPS)) * g + b


def setup_inputs():
    s = mx_kscale(O2)
    return {"h_dec1": bf(mish(np.random.standard_normal((B, O2))) * s),
            "D2": bf(np.random.standard_normal((O1, O2)) * 1.5 / np.sqrt(O2) / s),
            "g4": bf(1.0 + 0.1 * np.random.standard_normal(O1)),
            "b4": bf(0.1 * np.random.standard_normal(O1)),
            "D3": bf(np.random.standard_normal((D, O1)) * 1.5 / np.sqrt(O1)),
            "bo": bf(0.3 * np.random.standard_normal(D))}


def reference(h_dec1, D2, g4, b4, D3, bo):
    u = mxq(f64(h_dec1), 1, "e4m3") @ mxq(f64(D2), 1, "e4m3").T
    h = mish(ln(u, f64(g4), f64(b4)))
    return sigmoid((mxq(h, 1, "e4m3") @ mxq(f64(D3), 1, "e4m3").T) + f64(bo))

@@ -1,0 +1,398 @@
+from contextlib import ExitStack
+
+import concourse.mybir as mybir
+from concourse.masks import make_identity
+
+F32 = mybir.dt.float32
+BF16 = mybir.dt.bfloat16
+U32 = mybir.dt.uint32
+U8 = mybir.dt.uint8
+FP8X4 = mybir.dt.float8_e4m3fn_x4
+ALU = mybir.AluOpType
+FUNC = mybir.ActivationFunctionType
+
+P = 128
+PACK = 4
+ROWS, K_IN, HIDDEN, K_OUT = 4096, 512, 1024, 768
+EPS = 1e-5
+BANK = 512
+
+ROW_TILES = ROWS // P
+CHUNKS = HIDDEN // P
+PASSES = HIDDEN // (P * PACK)
+OUT_TILES = K_OUT // P
+PAIR = 2 * P
+X_PAIRS = ROWS // PAIR
+
+BATCH_TILES = (4, 8, 8, 8, 4)
+SHARED_ROUNDS = 2
+X_PER_STEP = 3
+X_AHEAD = 4
+D3_FIRST_STEP = 2
+TANH_AHEAD = 2
+QUANT_LAG, BIAS_LAG, OUT_LAG = 1, 2, 4
+LN_FLOOR = 2.0 ** -60
+
+FLOPS = 2 * ROWS * K_IN * HIDDEN + 2 * ROWS * HIDDEN * K_OUT
+
+
+def tile_autoencoder_pb_t_kernel(tc, h_dec1, D2, g4, b4, D3, bo, out):
+    nc = tc.nc
+    with ExitStack() as stack:
+        const = stack.enter_context(tc.tile_pool(name="const", bufs=1))
+        stage = stack.enter_context(tc.tile_pool(name="stage", bufs=4))
+        raws = stack.enter_context(tc.tile_pool(name="raws", bufs=9))
+        small = stack.enter_context(tc.tile_pool(name="small", bufs=4))
+        zpool = stack.enter_context(tc.tile_pool(name="zpool", bufs=3))
+        vpool = stack.enter_context(tc.tile_pool(name="vpool", bufs=18))
+        qpool = stack.enter_context(tc.tile_pool(name="qpool", bufs=10))
+        hpool = stack.enter_context(tc.tile_pool(name="hpool", bufs=3))
+        ypool = stack.enter_context(tc.tile_pool(name="ypool", bufs=5))
+        psum_u = stack.enter_context(tc.psum_pool(name="psum_u", bufs=4))
+        psum_turn = stack.enter_context(tc.psum_pool(name="psum_turn", bufs=2))
+        psum_o = stack.enter_context(tc.psum_pool(name="psum_o", bufs=1))
+        stack.enter_context(tc.manual_schedule())
+
+        ident_f32 = const.tile([P, P], F32)
+        make_identity(nc, ident_f32[:])
+        ident_bf16 = const.tile([P, P], BF16)
+        make_identity(nc, ident_bf16[:])
+        minus_half = const.tile([P, 1], F32)
+        nc.vector.memset(minus_half[:], -0.5)
+        ln_floor = const.tile([P, 1], F32)
+        nc.vector.memset(ln_floor[:], LN_FLOOR)
+        warm_in = const.tile([P, 1], F32)
+        nc.vector.memset(warm_in[:], 0.0)
+        warm_out = const.tile([P, 1], F32)
+        gb_rows = const.tile([P, P], BF16)
+        nc.vector.memset(gb_rows[:], 0.0)
+
+        def load_sigmoid_table():
+            nc.scalar.activation(out=warm_out[:], in_=warm_in[:], func=FUNC.Sigmoid)
+
+        load_sigmoid_table()
+
+        x_words = const.tile([P, ROWS], U32, align_bytes=64)
+        x_scales = const.tile([P, ROWS], U8, align_bytes=64)
+        d2_words = const.tile([P, HIDDEN], U32, align_bytes=64)
+        d2_scales = const.tile([P, HIDDEN], U8, align_bytes=64)
+        d3_words = const.tile([P, PASSES, K_OUT], U32, align_bytes=64)
+        d3_scales = const.tile([P, PASSES, K_OUT], U8, align_bytes=64)
+        bo_rows = const.tile([P, K_OUT], BF16)
+        gain_bias = const.tile([P, 2 * CHUNKS], F32)
+
+        def load_rows(src, n):
+            raw = raws.tile([P, 2 * K_IN], BF16, name="raw")
+            nc.sync.dma_start(
+                out=raw[:].rearrange("p (a k) -> p a k", a=2),
+                in_=src[PAIR * n : PAIR * (n + 1), :].rearrange("(a p) k -> p a k", p=P),
+            )
+            return raw
+
+        def turn_rows(raw):
+            words = raw[:].bitcast(F32)
+            turned = psum_turn.tile([P, 2, PAIR], F32, tag="bank", name="turned")
+            for u in range(2):
+                for a in range(2):
+                    first = (K_IN // 2) * a + P * u
+                    nc.tensor.transpose(
+                        out=turned[:, u, P * a : P * (a + 1)],
+                        in_=words[:, first : first + P],
+                        identity=ident_f32[:],
+                    )
+            grouped = stage.tile([P, PAIR * PACK], BF16, align_bytes=64, tag="grouped", name="grouped")
+            nc.scalar.copy(
+                out=grouped[:].bitcast(F32).rearrange("p (r u) -> p r u", u=2),
+                in_=turned[:].rearrange("p u r -> p r u"),
+            )
+            return grouped
+
+        def quantise_rows(grouped, words, scales):
+            nc.vector.quantize_mx(out=words.bitcast(FP8X4), scales=scales, in_=grouped[:])
+
+        x_raw = {}
+        x_grouped = {}
+
+        def load_x(n):
+            x_raw[n] = load_rows(h_dec1, n)
+
+        def turn_x(n):
+            x_grouped[n] = turn_rows(x_raw[n])
+
+        def quantise_x(n):
+            cols = slice(PAIR * n, PAIR * (n + 1))
+            quantise_rows(x_grouped[n], x_words[:, cols], x_scales[:, cols])
+
+        d3_raw = {}
+        d3_grouped = {}
+
+        def load_d3(d):
+            raw = raws.tile([P, HIDDEN], BF16, name="raw")
+            nc.sync.dma_start(out=raw[:], in_=D3[P * d : P * (d + 1), :])
+            d3_raw[d] = raw
+
+        def turn_d3(d):
+            turned = psum_turn.tile([P, CHUNKS, P], BF16, tag="bank", name="turned3")
+            for c in range(CHUNKS):
+                nc.tensor.transpose(
+                    out=turned[:, c, :],
+                    in_=d3_raw[d][:, P * c : P * (c + 1)],
+                    identity=ident_bf16[:],
+                )
+            grouped = stage.tile([P, PASSES, P, PACK], BF16, align_bytes=64, tag="grouped", name="grouped3")
+            nc.scalar.copy(out=grouped[:], in_=turned[:].rearrange("p (g t) r -> p g r t", t=PACK))
+            d3_grouped[d] = grouped
+
+        def quantise_d3(d):
+            cols = slice(P * d, P * (d + 1))
+            for g in range(PASSES):
+                nc.vector.quantize_mx(
+                    out=d3_words[:, g, cols].bitcast(FP8X4),
+                    scales=d3_scales[:, g, cols],
+                    in_=d3_grouped[d][:, g].rearrange("p r t -> p (r t)"),
+                )
+
+        u_banks = {}
+        moments = {}
+        z_tiles = {}
+        zt_banks = {}
+        v_tiles = {}
+        q_tiles = {}
+
+        def first_matmul(r):
+            cols = slice(P * r, P * (r + 1))
+            banks = []
+            for half in range(HIDDEN // BANK):
+                hid = slice(BANK * half, BANK * (half + 1))
+                u = psum_u.tile([P, BANK], F32, name="u")
+                nc.tensor.matmul_mx(
+                    out=u[:],
+                    lhsT=x_words[:, cols].bitcast(FP8X4),
+                    lhsT_scale=x_scales[:, cols],
+                    rhs=d2_words[:, hid].bitcast(FP8X4),
+                    rhs_scale=d2_scales[:, hid],
+                    start=True,
+                    stop=True,
+                )
+                banks.append(u)
+            u_banks[r] = banks
+
+        def row_statistics(r):
+            parts = small.tile([P, 2, 6], F32, name="parts")
+            for half in range(2):
+                nc.vector.bn_stats(out=parts[:, half, :], in_=u_banks[r][half][:])
+            mean_var = small.tile([P, 2], F32, name="mean_var")
+            nc.vector.bn_aggr(out=mean_var[:], in_=parts[:].rearrange("p a s -> p (a s)"))
+            var_eps = small.tile([P, 1], F32, name="var_eps")
+            nc.gpsimd.tensor_scalar_add(out=var_eps[:], in0=mean_var[:, 1:2], scalar1=EPS)
+            rstd = small.tile([P, 1], F32, name="rstd")
+            nc.gpsimd.tensor_tensor(out=rstd[:], in0=var_eps[:], in1=minus_half[:], op=ALU.pow)
+            moments[r] = (mean_var, rstd)
+
+        def normalise(r):
+            mean_var, rstd = moments[r]
+            z = zpool.tile([P, HIDDEN], F32, name="z")
+            for half in range(2):
+                nc.vector.tensor_scalar(
+                    out=z[:, BANK * half : BANK * (half + 1)],
+                    in0=u_banks[r][half][:],
+                    scalar1=mean_var[:, 0:1],
+                    scalar2=rstd[:],
+                    op0=ALU.subtract,
+                    op1=ALU.mult,
+                )
+            z_tiles[r] = z
+
+        def turn_hidden(r):
+            banks = []
+            for g in range(PASSES):
+                turned = psum_turn.tile([P, PACK, P], F32, tag="bank", name="zt")
+                for t in range(PACK):
+                    c = PACK * g + t
+                    nc.tensor.transpose(
+                        out=turned[:, t, :], in_=z_tiles[r][:, P * c : P * (c + 1)], identity=ident_f32[:],
+                    )
+                banks.append(turned)
+            zt_banks[r] = banks
+
+        def gain_and_bias(r, shared):
+            v = vpool.tile([P, CHUNKS, P], F32, name="v")
+            for g in range(PASSES):
+                turned = zt_banks[r][g]
+                for t in range(PACK):
+                    c = PACK * g + t
+                    gain = gain_bias[:, c : c + 1]
+                    bias = gain_bias[:, CHUNKS + c : CHUNKS + c + 1]
+                    if g == 0 or not shared:
+                        nc.vector.tensor_scalar(
+                            out=v[:, c, :], in0=turned[:, t, :], scalar1=gain, scalar2=bias,
+                            op0=ALU.mult, op1=ALU.add,
+                        )
+                    else:
+                        nc.scalar.activation(
+                            out=v[:, c, :], in_=turned[:, t, :], func=FUNC.Identity, bias=bias, scale=gain,
+                        )
+            v_tiles[r] = v
+
+        def prepare_inputs(s):
+            d = s - D3_FIRST_STEP
+            for n in range(1 + X_PER_STEP * (s - 1), 1 + X_PER_STEP * s):
+                if 1 <= n < X_PAIRS:
+                    quantise_x(n)
+            if 0 <= d - 1 < OUT_TILES:
+                quantise_d3(d - 1)
+            for n in range(1 + X_PER_STEP * s, 1 + X_PER_STEP * (s + 1)):
+                if n + X_AHEAD < X_PAIRS:
+                    load_x(n + X_AHEAD)
+                if n < X_PAIRS:
+                    turn_x(n)
+            if 0 <= d + 2 < OUT_TILES:
+                load_d3(d + 2)
+            if 0 <= d < OUT_TILES:
+                turn_d3(d)
+
+        def front_step(s, shared):
+            prepare_inputs(s)
+            if 0 <= s - 2 < ROW_TILES:
+                turn_hidden(s - 2)
+            if s < ROW_TILES:
+                row_statistics(s)
+            if 0 <= s - 1 < ROW_TILES:
+                normalise(s - 1)
+            if s + 1 < ROW_TILES:
+                first_matmul(s + 1)
+            if 0 <= s - 2 < ROW_TILES:
+                gain_and_bias(s - 2, shared)
+
+        def sigmoid_tile(r):
+            q = qpool.tile([P, CHUNKS, P], F32, name="q")
+            nc.scalar.activation(out=q[:], in_=v_tiles[r][:], func=FUNC.Sigmoid, scale=-1.0)
+            q_tiles[r] = q
+
+        def log_tile(r):
+            nc.scalar.activation(out=q_tiles[r][:], in_=q_tiles[r][:], func=FUNC.Ln, bias=ln_floor[:])
+
+        def tanh_tile(r):
+            nc.scalar.activation(out=q_tiles[r][:], in_=q_tiles[r][:], func=FUNC.Tanh, scale=-1.0)
+
+        h_bf16 = {}
+        h_words = {}
+        o_banks = {}
+        y_tiles = {}
+
+        def mish_product(r):
+            hb = hpool.tile([P, PASSES, P, PACK], BF16, align_bytes=64, name="hb")
+            for g in range(PASSES):
+                chunks = slice(PACK * g, PACK * (g + 1))
+                nc.gpsimd.tensor_tensor(
+                    out=hb[:, g].rearrange("p (c i) t -> p c t i", i=4),
+                    in0=v_tiles[r][:, chunks, :].rearrange("p t (c i) -> p c t i", i=4),
+                    in1=q_tiles[r][:, chunks, :].rearrange("p t (c i) -> p c t i", i=4),
+                    op=ALU.mult,
+                )
+            h_bf16[r] = hb
+
+        def quantise_hidden(r):
+            hw = hpool.tile([P, PASSES * P], U32, align_bytes=64, name="hw")
+            hs = hpool.tile([P, PASSES * P], U8, align_bytes=64, name="hs")
+            nc.vector.quantize_mx(
+                out=hw[:].bitcast(FP8X4), scales=hs[:], in_=h_bf16[r][:].rearrange("p g r t -> p (g r t)"),
+            )
+            h_words[r] = (hw, hs)
+
+        def second_matmul(r):
+            hw, hs = h_words[r]
+            wide = psum_o.tile([P, BANK], F32, name="wide")
+            narrow = psum_o.tile([P, K_OUT - BANK], F32, name="narrow")
+            for g in range(PASSES):
+                cols = slice(P * g, P * (g + 1))
+                for acc, lo, hi in ((wide, 0, BANK), (narrow, BANK, K_OUT)):
+                    nc.tensor.matmul_mx(
+                        out=acc[:],
+                        lhsT=hw[:, cols].bitcast(FP8X4),
+                        lhsT_scale=hs[:, cols],
+                        rhs=d3_words[:, g, lo:hi].bitcast(FP8X4),
+                        rhs_scale=d3_scales[:, g, lo:hi],
+                        start=(g == 0),
+                        stop=(g == PASSES - 1),
+                    )
+            o_banks[r] = (wide, narrow)
+
+        def add_bias(r):
+            wide, narrow = o_banks[r]
+            y = ypool.tile([P, K_OUT], F32, name="y")
+            nc.vector.tensor_tensor(out=y[:, 0:BANK], in0=wide[:], in1=bo_rows[:, 0:BANK], op=ALU.add)
+            nc.vector.tensor_tensor(out=y[:, BANK:K_OUT], in0=narrow[:], in1=bo_rows[:, BANK:K_OUT], op=ALU.add)
+            y_tiles[r] = y
+
+        def output_sigmoid(r):
+            y = y_tiles[r]
+            nc.scalar.activation(out=y[:], in_=y[:], func=FUNC.Sigmoid)
+            nc.sync.dma_start(out=out[P * r : P * (r + 1), :], in_=y[:])
+
+        def back_tick(r, last):
+            if r <= last:
+                mish_product(r)
+            if 0 <= r - QUANT_LAG <= last:
+                quantise_hidden(r - QUANT_LAG)
+            if 0 <= r - BIAS_LAG <= last:
+                add_bias(r - BIAS_LAG)
+            if 0 <= r - QUANT_LAG <= last:
+                second_matmul(r - QUANT_LAG)
+
+        d2_raw = [load_rows(D2, n) for n in range(HIDDEN // PAIR)]
+        load_x(0)
+        nc.scalar.dma_start(out=gb_rows[0:CHUNKS, :], in_=g4.rearrange("(c p) -> c p", p=P))
+        nc.scalar.dma_start(out=gb_rows[CHUNKS : 2 * CHUNKS, :], in_=b4.rearrange("(c p) -> c p", p=P))
+        nc.scalar.dma_start(out=bo_rows[:], in_=bo.partition_broadcast(P))
+        for n in range(HIDDEN // PAIR):
+            cols = slice(PAIR * n, PAIR * (n + 1))
+            quantise_rows(turn_rows(d2_raw[n]), d2_words[:, cols], d2_scales[:, cols])
+        turn_x(0)
+        quantise_x(0)
+        for n in range(1, 1 + X_AHEAD):
+            load_x(n)
+        first_matmul(0)
+        gb_turned = psum_turn.tile([P, P], BF16, tag="bank", name="gb_turned")
+        nc.tensor.transpose(out=gb_turned[:], in_=gb_rows[:], identity=ident_bf16[:])
+        nc.vector.tensor_copy(out=gain_bias[:], in_=gb_turned[:, 0 : 2 * CHUNKS])
+
+        n_batches = len(BATCH_TILES)
+        first_tile = [sum(BATCH_TILES[:i]) for i in range(n_batches)]
+        last_step = [first_tile[i] + BATCH_TILES[i] - 1 + 2 for i in range(n_batches)]
+
+        for i in range(n_batches + 2):
+            back, middle, front = i - 2, i - 1, i
+            n_back = BATCH_TILES[back] if back >= 0 else 0
+            n_middle = BATCH_TILES[middle] if 0 <= middle < n_batches else 0
+            steps = []
+            if front < n_batches:
+                steps = list(range(last_step[front - 1] + 1 if front > 0 else 0, last_step[front] + 1))
+            flush = OUT_LAG if back == n_batches - 1 else 0
+            ticks_1 = max(n_back + flush, n_middle)
+            ticks_2 = n_middle if i > 0 else len(steps)
+            ticks = ticks_1 + ticks_2
+
+            def front_steps_of_tick(tick):
+                for j in range(len(steps) * tick // ticks, len(steps) * (tick + 1) // ticks):
+                    front_step(steps[j], i < SHARED_ROUNDS)
+
+            load_sigmoid_table()
+            for t in range(min(TANH_AHEAD, n_back)):
+                tanh_tile(first_tile[back] + t)
+            for t in range(ticks_1):
+                if t + TANH_AHEAD < n_back:
+                    tanh_tile(first_tile[back] + t + TANH_AHEAD)
+                if n_back and t < n_back + flush:
+                    r = first_tile[back] + t
+                    back_tick(r, first_tile[back] + n_back - 1)
+                    if 0 <= r - OUT_LAG:
+                        output_sigmoid(r - OUT_LAG)
+                if t < n_middle:
+                    sigmoid_tile(first_tile[middle] + t)
+                front_steps_of_tick(t)
+
+            for t in range(ticks_2):
+                if t < n_middle:
+                    log_tile(first_tile[middle] + t)
+                front_steps_of_tick(ticks_1 + t)

@@ -24,13 +24,12 @@ OUT_TILES = K_OUT // P
 PAIR = 2 * P
 X_PAIRS = ROWS // PAIR
 
-BATCH_TILES = (4, 8, 8, 8, 4)
-SHARED_ROUNDS = 2
+BATCH_TILES = (4, 4, 4, 4, 4, 4, 4, 4)
+SHARED_ROUNDS = 1
 X_PER_STEP = 3
 X_AHEAD = 4
 D3_FIRST_STEP = 2
-TANH_AHEAD = 2
-QUANT_LAG, BIAS_LAG, OUT_LAG = 1, 2, 4
+QUANT_LAG, BIAS_LAG = 1, 2
 LN_FLOOR = 2.0 ** -60
 
 FLOPS = 2 * ROWS * K_IN * HIDDEN + 2 * ROWS * HIDDEN * K_OUT
@@ -45,9 +44,9 @@ def tile_autoencoder_pb_t_kernel(tc, h_dec1, D2, g4, b4, D3, bo, out):
         small = stack.enter_context(tc.tile_pool(name="small", bufs=4))
         zpool = stack.enter_context(tc.tile_pool(name="zpool", bufs=3))
         vpool = stack.enter_context(tc.tile_pool(name="vpool", bufs=18))
-        qpool = stack.enter_context(tc.tile_pool(name="qpool", bufs=10))
+        qpool = stack.enter_context(tc.tile_pool(name="qpool", bufs=12))
         hpool = stack.enter_context(tc.tile_pool(name="hpool", bufs=3))
-        ypool = stack.enter_context(tc.tile_pool(name="ypool", bufs=5))
+        ypool = stack.enter_context(tc.tile_pool(name="ypool", bufs=6))
         psum_u = stack.enter_context(tc.psum_pool(name="psum_u", bufs=4))
         psum_turn = stack.enter_context(tc.psum_pool(name="psum_turn", bufs=2))
         psum_o = stack.enter_context(tc.psum_pool(name="psum_o", bufs=1))
@@ -330,15 +329,23 @@ def tile_autoencoder_pb_t_kernel(tc, h_dec1, D2, g4, b4, D3, bo, out):
             nc.scalar.activation(out=y[:], in_=y[:], func=FUNC.Sigmoid)
             nc.sync.dma_start(out=out[P * r : P * (r + 1), :], in_=y[:])
 
-        def back_tick(r, last):
-            if r <= last:
+        progress = {"added": 0, "stored": 0}
+
+        def back_tick(r):
+            if r < ROW_TILES:
                 mish_product(r)
-            if 0 <= r - QUANT_LAG <= last:
+            if 0 <= r - QUANT_LAG < ROW_TILES:
                 quantise_hidden(r - QUANT_LAG)
-            if 0 <= r - BIAS_LAG <= last:
+            if 0 <= r - BIAS_LAG < ROW_TILES:
                 add_bias(r - BIAS_LAG)
-            if 0 <= r - QUANT_LAG <= last:
+                progress["added"] = r - BIAS_LAG + 1
+            if 0 <= r - QUANT_LAG < ROW_TILES:
                 second_matmul(r - QUANT_LAG)
+
+        def drain_outputs():
+            for r in range(progress["stored"], progress["added"]):
+                output_sigmoid(r)
+            progress["stored"] = progress["added"]
 
         d2_raw = [load_rows(D2, n) for n in range(HIDDEN // PAIR)]
         load_x(0)
@@ -368,31 +375,29 @@ def tile_autoencoder_pb_t_kernel(tc, h_dec1, D2, g4, b4, D3, bo, out):
             steps = []
             if front < n_batches:
                 steps = list(range(last_step[front - 1] + 1 if front > 0 else 0, last_step[front] + 1))
-            flush = OUT_LAG if back == n_batches - 1 else 0
-            ticks_1 = max(n_back + flush, n_middle)
-            ticks_2 = n_middle if i > 0 else len(steps)
-            ticks = ticks_1 + ticks_2
+            ticks_1 = max(n_back, n_middle)
+            clock = max(3 * ticks_1 + n_middle, 1)
 
-            def front_steps_of_tick(tick):
-                for j in range(len(steps) * tick // ticks, len(steps) * (tick + 1) // ticks):
+            def others(lo, hi):
+                for j in range(n_back * lo // clock, n_back * hi // clock):
+                    back_tick(first_tile[back] + j)
+                for j in range(len(steps) * lo // clock, len(steps) * hi // clock):
                     front_step(steps[j], i < SHARED_ROUNDS)
 
             load_sigmoid_table()
-            for t in range(min(TANH_AHEAD, n_back)):
-                tanh_tile(first_tile[back] + t)
             for t in range(ticks_1):
-                if t + TANH_AHEAD < n_back:
-                    tanh_tile(first_tile[back] + t + TANH_AHEAD)
-                if n_back and t < n_back + flush:
-                    r = first_tile[back] + t
-                    back_tick(r, first_tile[back] + n_back - 1)
-                    if 0 <= r - OUT_LAG:
-                        output_sigmoid(r - OUT_LAG)
+                drain_outputs()
+                if t < n_back:
+                    tanh_tile(first_tile[back] + t)
                 if t < n_middle:
                     sigmoid_tile(first_tile[middle] + t)
-                front_steps_of_tick(t)
+                others(3 * t, 3 * t + 3)
+            for t in range(n_middle):
+                log_tile(first_tile[middle] + t)
+                others(3 * ticks_1 + t, 3 * ticks_1 + t + 1)
+            if ticks_1 == 0:
+                others(0, 1)
 
-            for t in range(ticks_2):
-                if t < n_middle:
-                    log_tile(first_tile[middle] + t)
-                front_steps_of_tick(ticks_1 + t)
+        for r in range(ROW_TILES, ROW_TILES + BIAS_LAG):
+            back_tick(r)
+        drain_outputs()

@@ -29,7 +29,8 @@ SHARED_ROUNDS = 1
 X_PER_STEP = 3
 X_AHEAD = 4
 D3_FIRST_STEP = 2
-QUANT_LAG, BIAS_LAG = 1, 2
+TURN_LAG = 3
+QUANT_LAG, BIAS_LAG = 2, 3
 LN_FLOOR = 2.0 ** -60
 
 FLOPS = 2 * ROWS * K_IN * HIDDEN + 2 * ROWS * HIDDEN * K_OUT
@@ -42,14 +43,14 @@ def tile_autoencoder_pb_t_kernel(tc, h_dec1, D2, g4, b4, D3, bo, out):
         stage = stack.enter_context(tc.tile_pool(name="stage", bufs=4))
         raws = stack.enter_context(tc.tile_pool(name="raws", bufs=9))
         small = stack.enter_context(tc.tile_pool(name="small", bufs=4))
-        zpool = stack.enter_context(tc.tile_pool(name="zpool", bufs=3))
-        vpool = stack.enter_context(tc.tile_pool(name="vpool", bufs=18))
-        qpool = stack.enter_context(tc.tile_pool(name="qpool", bufs=12))
-        hpool = stack.enter_context(tc.tile_pool(name="hpool", bufs=3))
+        zpool = stack.enter_context(tc.tile_pool(name="zpool", bufs=5))
+        vpool = stack.enter_context(tc.tile_pool(name="vpool", bufs=7))
+        qpool = stack.enter_context(tc.tile_pool(name="qpool", bufs=5))
+        hpool = stack.enter_context(tc.tile_pool(name="hpool", bufs=4))
         ypool = stack.enter_context(tc.tile_pool(name="ypool", bufs=6))
         psum_u = stack.enter_context(tc.psum_pool(name="psum_u", bufs=4))
         psum_turn = stack.enter_context(tc.psum_pool(name="psum_turn", bufs=2))
-        psum_o = stack.enter_context(tc.psum_pool(name="psum_o", bufs=1))
+        psum_o = stack.enter_context(tc.psum_pool(name="psum_o", bufs=2))
         stack.enter_context(tc.manual_schedule())
 
         ident_f32 = const.tile([P, P], F32)
@@ -90,7 +91,7 @@ def tile_autoencoder_pb_t_kernel(tc, h_dec1, D2, g4, b4, D3, bo, out):
 
         def turn_rows(raw):
             words = raw[:].bitcast(F32)
-            turned = psum_turn.tile([P, 2, PAIR], F32, tag="bank", name="turned")
+            turned = psum_o.tile([P, 2, PAIR], F32, tag="bank", name="turned")
             for u in range(2):
                 for a in range(2):
                     first = (K_IN // 2) * a + P * u
@@ -131,7 +132,7 @@ def tile_autoencoder_pb_t_kernel(tc, h_dec1, D2, g4, b4, D3, bo, out):
             d3_raw[d] = raw
 
         def turn_d3(d):
-            turned = psum_turn.tile([P, CHUNKS, P], BF16, tag="bank", name="turned3")
+            turned = psum_o.tile([P, CHUNKS, P], BF16, tag="bank", name="turned3")
             for c in range(CHUNKS):
                 nc.tensor.transpose(
                     out=turned[:, c, :],
@@ -202,36 +203,40 @@ def tile_autoencoder_pb_t_kernel(tc, h_dec1, D2, g4, b4, D3, bo, out):
                 )
             z_tiles[r] = z
 
-        def turn_hidden(r):
+        def turn_hidden(n, g):
             banks = []
-            for g in range(PASSES):
-                turned = psum_turn.tile([P, PACK, P], F32, tag="bank", name="zt")
-                for t in range(PACK):
-                    c = PACK * g + t
-                    nc.tensor.transpose(
-                        out=turned[:, t, :], in_=z_tiles[r][:, P * c : P * (c + 1)], identity=ident_f32[:],
-                    )
+            for j in range(2):
+                turned = psum_turn.tile([P, 2, PAIR], F32, tag="bank", name="zt")
+                for e in range(2):
+                    c = PACK * g + 2 * j + e
+                    for a in range(2):
+                        nc.tensor.transpose(
+                            out=turned[:, e, P * a : P * (a + 1)],
+                            in_=z_tiles[2 * n + a][:, P * c : P * (c + 1)],
+                            identity=ident_f32[:],
+                        )
                 banks.append(turned)
-            zt_banks[r] = banks
+            zt_banks[(n, g)] = banks
 
-        def gain_and_bias(r, shared):
-            v = vpool.tile([P, CHUNKS, P], F32, name="v")
-            for g in range(PASSES):
-                turned = zt_banks[r][g]
-                for t in range(PACK):
-                    c = PACK * g + t
+        def gain_and_bias(n, g, shared):
+            if g == 0:
+                v = vpool.tile([P, CHUNKS, PAIR], F32, name="v")
+                v_tiles[n] = v
+            for j in range(2):
+                for e in range(2):
+                    c = PACK * g + 2 * j + e
                     gain = gain_bias[:, c : c + 1]
                     bias = gain_bias[:, CHUNKS + c : CHUNKS + c + 1]
-                    if g == 0 or not shared:
+                    if j == 0 or not shared:
                         nc.vector.tensor_scalar(
-                            out=v[:, c, :], in0=turned[:, t, :], scalar1=gain, scalar2=bias,
+                            out=v_tiles[n][:, c, :], in0=zt_banks[(n, g)][j][:, e, :], scalar1=gain, scalar2=bias,
                             op0=ALU.mult, op1=ALU.add,
                         )
                     else:
                         nc.scalar.activation(
-                            out=v[:, c, :], in_=turned[:, t, :], func=FUNC.Identity, bias=bias, scale=gain,
+                            out=v_tiles[n][:, c, :], in_=zt_banks[(n, g)][j][:, e, :], func=FUNC.Identity,
+                            bias=bias, scale=gain,
                         )
-            v_tiles[r] = v
 
         def prepare_inputs(s):
             d = s - D3_FIRST_STEP
@@ -252,27 +257,28 @@ def tile_autoencoder_pb_t_kernel(tc, h_dec1, D2, g4, b4, D3, bo, out):
 
         def front_step(s, shared):
             prepare_inputs(s)
-            if 0 <= s - 2 < ROW_TILES:
-                turn_hidden(s - 2)
+            m = s - TURN_LAG
+            if 0 <= m < ROW_TILES:
+                turn_hidden(m // 2, m % 2)
             if s < ROW_TILES:
                 row_statistics(s)
             if 0 <= s - 1 < ROW_TILES:
                 normalise(s - 1)
             if s + 1 < ROW_TILES:
                 first_matmul(s + 1)
-            if 0 <= s - 2 < ROW_TILES:
-                gain_and_bias(s - 2, shared)
+            if 0 <= m < ROW_TILES:
+                gain_and_bias(m // 2, m % 2, shared)
 
-        def sigmoid_tile(r):
-            q = qpool.tile([P, CHUNKS, P], F32, name="q")
-            nc.scalar.activation(out=q[:], in_=v_tiles[r][:], func=FUNC.Sigmoid, scale=-1.0)
-            q_tiles[r] = q
+        def sigmoid_pair(n):
+            q = qpool.tile([P, CHUNKS, PAIR], F32, name="q")
+            nc.scalar.activation(out=q[:], in_=v_tiles[n][:], func=FUNC.Sigmoid, scale=-1.0)
+            q_tiles[n] = q
 
-        def log_tile(r):
-            nc.scalar.activation(out=q_tiles[r][:], in_=q_tiles[r][:], func=FUNC.Ln, bias=ln_floor[:])
+        def log_pair(n):
+            nc.scalar.activation(out=q_tiles[n][:], in_=q_tiles[n][:], func=FUNC.Ln, bias=ln_floor[:])
 
-        def tanh_tile(r):
-            nc.scalar.activation(out=q_tiles[r][:], in_=q_tiles[r][:], func=FUNC.Tanh, scale=-1.0)
+        def tanh_pair(n):
+            nc.scalar.activation(out=q_tiles[n][:], in_=q_tiles[n][:], func=FUNC.Tanh, scale=-1.0)
 
         h_bf16 = {}
         h_words = {}
@@ -281,12 +287,14 @@ def tile_autoencoder_pb_t_kernel(tc, h_dec1, D2, g4, b4, D3, bo, out):
 
         def mish_product(r):
             hb = hpool.tile([P, PASSES, P, PACK], BF16, align_bytes=64, name="hb")
+            rows = slice(P * (r % 2), P * (r % 2) + P)
             for g in range(PASSES):
                 chunks = slice(PACK * g, PACK * (g + 1))
-                nc.gpsimd.tensor_tensor(
+                engine = nc.vector if g == 1 and r >= ROW_TILES - BATCH_TILES[-1] else nc.gpsimd
+                engine.tensor_tensor(
                     out=hb[:, g].rearrange("p (c i) t -> p c t i", i=4),
-                    in0=v_tiles[r][:, chunks, :].rearrange("p t (c i) -> p c t i", i=4),
-                    in1=q_tiles[r][:, chunks, :].rearrange("p t (c i) -> p c t i", i=4),
+                    in0=v_tiles[r // 2][:, chunks, rows].rearrange("p t (c i) -> p c t i", i=4),
+                    in1=q_tiles[r // 2][:, chunks, rows].rearrange("p t (c i) -> p c t i", i=4),
                     op=ALU.mult,
                 )
             h_bf16[r] = hb
@@ -301,8 +309,8 @@ def tile_autoencoder_pb_t_kernel(tc, h_dec1, D2, g4, b4, D3, bo, out):
 
         def second_matmul(r):
             hw, hs = h_words[r]
-            wide = psum_o.tile([P, BANK], F32, name="wide")
-            narrow = psum_o.tile([P, K_OUT - BANK], F32, name="narrow")
+            wide = psum_o.tile([P, BANK], F32, tag="bank", name="wide")
+            narrow = psum_o.tile([P, K_OUT - BANK], F32, tag="bank", name="narrow")
             for g in range(PASSES):
                 cols = slice(P * g, P * (g + 1))
                 for acc, lo, hi in ((wide, 0, BANK), (narrow, BANK, K_OUT)):
@@ -332,8 +340,6 @@ def tile_autoencoder_pb_t_kernel(tc, h_dec1, D2, g4, b4, D3, bo, out):
         progress = {"added": 0, "stored": 0}
 
         def back_tick(r):
-            if r < ROW_TILES:
-                mish_product(r)
             if 0 <= r - QUANT_LAG < ROW_TILES:
                 quantise_hidden(r - QUANT_LAG)
             if 0 <= r - BIAS_LAG < ROW_TILES:
@@ -341,6 +347,8 @@ def tile_autoencoder_pb_t_kernel(tc, h_dec1, D2, g4, b4, D3, bo, out):
                 progress["added"] = r - BIAS_LAG + 1
             if 0 <= r - QUANT_LAG < ROW_TILES:
                 second_matmul(r - QUANT_LAG)
+            if r < ROW_TILES:
+                mish_product(r)
 
         def drain_outputs():
             for r in range(progress["stored"], progress["added"]):
@@ -360,13 +368,13 @@ def tile_autoencoder_pb_t_kernel(tc, h_dec1, D2, g4, b4, D3, bo, out):
         for n in range(1, 1 + X_AHEAD):
             load_x(n)
         first_matmul(0)
-        gb_turned = psum_turn.tile([P, P], BF16, tag="bank", name="gb_turned")
+        gb_turned = psum_o.tile([P, P], BF16, tag="bank", name="gb_turned")
         nc.tensor.transpose(out=gb_turned[:], in_=gb_rows[:], identity=ident_bf16[:])
         nc.vector.tensor_copy(out=gain_bias[:], in_=gb_turned[:, 0 : 2 * CHUNKS])
 
         n_batches = len(BATCH_TILES)
         first_tile = [sum(BATCH_TILES[:i]) for i in range(n_batches)]
-        last_step = [first_tile[i] + BATCH_TILES[i] - 1 + 2 for i in range(n_batches)]
+        last_step = [first_tile[i] + BATCH_TILES[i] - 1 + TURN_LAG for i in range(n_batches)]
 
         for i in range(n_batches + 2):
             back, middle, front = i - 2, i - 1, i
@@ -375,8 +383,8 @@ def tile_autoencoder_pb_t_kernel(tc, h_dec1, D2, g4, b4, D3, bo, out):
             steps = []
             if front < n_batches:
                 steps = list(range(last_step[front - 1] + 1 if front > 0 else 0, last_step[front] + 1))
-            ticks_1 = max(n_back, n_middle)
-            clock = max(3 * ticks_1 + n_middle, 1)
+            ticks_1 = max(n_back, n_middle) // 2
+            clock = max(3 * ticks_1 + n_middle // 2, 1)
 
             def others(lo, hi):
                 for j in range(n_back * lo // clock, n_back * hi // clock):
@@ -387,17 +395,17 @@ def tile_autoencoder_pb_t_kernel(tc, h_dec1, D2, g4, b4, D3, bo, out):
             load_sigmoid_table()
             for t in range(ticks_1):
                 drain_outputs()
-                if t < n_back:
-                    tanh_tile(first_tile[back] + t)
-                if t < n_middle:
-                    sigmoid_tile(first_tile[middle] + t)
+                if 2 * t < n_back:
+                    tanh_pair(first_tile[back] // 2 + t)
+                if 2 * t < n_middle:
+                    sigmoid_pair(first_tile[middle] // 2 + t)
                 others(3 * t, 3 * t + 3)
-            for t in range(n_middle):
-                log_tile(first_tile[middle] + t)
+            for t in range(n_middle // 2):
+                log_pair(first_tile[middle] // 2 + t)
                 others(3 * ticks_1 + t, 3 * ticks_1 + t + 1)
             if ticks_1 == 0:
                 others(0, 1)
 
         for r in range(ROW_TILES, ROW_TILES + BIAS_LAG):
             back_tick(r)
-        drain_outputs()
+            drain_outputs()

@@ -20,17 +20,18 @@ BANK = 512
 ROW_TILES = ROWS // P
 CHUNKS = HIDDEN // P
 PASSES = HIDDEN // (P * PACK)
-OUT_TILES = K_OUT // P
 PAIR = 2 * P
 X_PAIRS = ROWS // PAIR
+D2_PAIRS = HIDDEN // PAIR
+D3_TILES = K_OUT // P
 
-BATCH_TILES = (4, 4, 4, 4, 4, 4, 4, 4)
-SHARED_ROUNDS = 1
-X_PER_STEP = 3
-X_AHEAD = 4
-D3_FIRST_STEP = 2
+BATCH = 4
+N_BATCHES = ROW_TILES // BATCH
 TURN_LAG = 3
 QUANT_LAG, BIAS_LAG = 2, 3
+N_PIECES = X_PAIRS + D3_TILES
+PIECES_PER_STEP = (N_PIECES - 1) // (TURN_LAG + BATCH)
+PIECES_AHEAD = 4
 LN_FLOOR = 2.0 ** -60
 
 FLOPS = 2 * ROWS * K_IN * HIDDEN + 2 * ROWS * HIDDEN * K_OUT
@@ -40,14 +41,14 @@ def tile_autoencoder_pb_t_kernel(tc, h_dec1, D2, g4, b4, D3, bo, out):
     nc = tc.nc
     with ExitStack() as stack:
         const = stack.enter_context(tc.tile_pool(name="const", bufs=1))
-        stage = stack.enter_context(tc.tile_pool(name="stage", bufs=4))
-        raws = stack.enter_context(tc.tile_pool(name="raws", bufs=9))
+        raws = stack.enter_context(tc.tile_pool(name="raws", bufs=D2_PAIRS + 1 + PIECES_AHEAD))
+        stage = stack.enter_context(tc.tile_pool(name="stage", bufs=PIECES_PER_STEP + 1))
         small = stack.enter_context(tc.tile_pool(name="small", bufs=4))
-        zpool = stack.enter_context(tc.tile_pool(name="zpool", bufs=5))
-        vpool = stack.enter_context(tc.tile_pool(name="vpool", bufs=7))
-        qpool = stack.enter_context(tc.tile_pool(name="qpool", bufs=5))
-        hpool = stack.enter_context(tc.tile_pool(name="hpool", bufs=4))
-        ypool = stack.enter_context(tc.tile_pool(name="ypool", bufs=6))
+        zpool = stack.enter_context(tc.tile_pool(name="zpool", bufs=TURN_LAG + 2))
+        vpool = stack.enter_context(tc.tile_pool(name="vpool", bufs=3 * BATCH // 2 + 1))
+        qpool = stack.enter_context(tc.tile_pool(name="qpool", bufs=2 * BATCH // 2 + 1))
+        hpool = stack.enter_context(tc.tile_pool(name="hpool", bufs=QUANT_LAG + 2))
+        ypool = stack.enter_context(tc.tile_pool(name="ypool", bufs=BATCH + 2))
         psum_u = stack.enter_context(tc.psum_pool(name="psum_u", bufs=4))
         psum_turn = stack.enter_context(tc.psum_pool(name="psum_turn", bufs=2))
         psum_o = stack.enter_context(tc.psum_pool(name="psum_o", bufs=2))
@@ -110,49 +111,57 @@ def tile_autoencoder_pb_t_kernel(tc, h_dec1, D2, g4, b4, D3, bo, out):
         def quantise_rows(grouped, words, scales):
             nc.vector.quantize_mx(out=words.bitcast(FP8X4), scales=scales, in_=grouped[:])
 
-        x_raw = {}
-        x_grouped = {}
-
-        def load_x(n):
-            x_raw[n] = load_rows(h_dec1, n)
-
-        def turn_x(n):
-            x_grouped[n] = turn_rows(x_raw[n])
-
-        def quantise_x(n):
-            cols = slice(PAIR * n, PAIR * (n + 1))
-            quantise_rows(x_grouped[n], x_words[:, cols], x_scales[:, cols])
-
-        d3_raw = {}
-        d3_grouped = {}
-
         def load_d3(d):
             raw = raws.tile([P, HIDDEN], BF16, name="raw")
             nc.sync.dma_start(out=raw[:], in_=D3[P * d : P * (d + 1), :])
-            d3_raw[d] = raw
+            return raw
 
-        def turn_d3(d):
+        def turn_d3(raw):
             turned = psum_o.tile([P, CHUNKS, P], BF16, tag="bank", name="turned3")
             for c in range(CHUNKS):
                 nc.tensor.transpose(
-                    out=turned[:, c, :],
-                    in_=d3_raw[d][:, P * c : P * (c + 1)],
-                    identity=ident_bf16[:],
+                    out=turned[:, c, :], in_=raw[:, P * c : P * (c + 1)], identity=ident_bf16[:]
                 )
             grouped = stage.tile([P, PASSES, P, PACK], BF16, align_bytes=64, tag="grouped", name="grouped3")
             nc.scalar.copy(out=grouped[:], in_=turned[:].rearrange("p (g t) r -> p g r t", t=PACK))
-            d3_grouped[d] = grouped
+            return grouped
 
-        def quantise_d3(d):
+        def quantise_d3(grouped, d):
             cols = slice(P * d, P * (d + 1))
             for g in range(PASSES):
                 nc.vector.quantize_mx(
                     out=d3_words[:, g, cols].bitcast(FP8X4),
                     scales=d3_scales[:, g, cols],
-                    in_=d3_grouped[d][:, g].rearrange("p r t -> p (r t)"),
+                    in_=grouped[:, g].rearrange("p r t -> p (r t)"),
                 )
 
+        piece_raw = {}
+        piece_grouped = {}
+
+        def load_piece(n):
+            piece_raw[n] = load_rows(h_dec1, n) if n < X_PAIRS else load_d3(n - X_PAIRS)
+
+        def turn_piece(n):
+            piece_grouped[n] = turn_rows(piece_raw[n]) if n < X_PAIRS else turn_d3(piece_raw[n])
+
+        def quantise_piece(n):
+            if n < X_PAIRS:
+                cols = slice(PAIR * n, PAIR * (n + 1))
+                quantise_rows(piece_grouped[n], x_words[:, cols], x_scales[:, cols])
+            else:
+                quantise_d3(piece_grouped[n], n - X_PAIRS)
+
+        def prepare_inputs(s):
+            first = 1 + PIECES_PER_STEP * s
+            for n in range(max(first - PIECES_PER_STEP, 1), min(first, N_PIECES)):
+                quantise_piece(n)
+            for n in range(first, min(first + PIECES_PER_STEP, N_PIECES)):
+                if n + PIECES_AHEAD < N_PIECES:
+                    load_piece(n + PIECES_AHEAD)
+                turn_piece(n)
+
         u_banks = {}
+        bank_stats = {}
         moments = {}
         z_tiles = {}
         zt_banks = {}
@@ -177,12 +186,15 @@ def tile_autoencoder_pb_t_kernel(tc, h_dec1, D2, g4, b4, D3, bo, out):
                 banks.append(u)
             u_banks[r] = banks
 
-        def row_statistics(r):
-            parts = small.tile([P, 2, 6], F32, name="parts")
+        def bank_statistics(r):
+            stats = small.tile([P, 2, 6], F32, name="stats")
             for half in range(2):
-                nc.vector.bn_stats(out=parts[:, half, :], in_=u_banks[r][half][:])
+                nc.vector.bn_stats(out=stats[:, half, :], in_=u_banks[r][half][:])
+            bank_stats[r] = stats
+
+        def row_moments(r):
             mean_var = small.tile([P, 2], F32, name="mean_var")
-            nc.vector.bn_aggr(out=mean_var[:], in_=parts[:].rearrange("p a s -> p (a s)"))
+            nc.vector.bn_aggr(out=mean_var[:], in_=bank_stats[r][:].rearrange("p a s -> p (a s)"))
             var_eps = small.tile([P, 1], F32, name="var_eps")
             nc.gpsimd.tensor_scalar_add(out=var_eps[:], in0=mean_var[:, 1:2], scalar1=EPS)
             rstd = small.tile([P, 1], F32, name="rstd")
@@ -218,56 +230,37 @@ def tile_autoencoder_pb_t_kernel(tc, h_dec1, D2, g4, b4, D3, bo, out):
                 banks.append(turned)
             zt_banks[(n, g)] = banks
 
-        def gain_and_bias(n, g, shared):
+        def gain_and_bias(n, g):
             if g == 0:
                 v = vpool.tile([P, CHUNKS, PAIR], F32, name="v")
                 v_tiles[n] = v
             for j in range(2):
                 for e in range(2):
                     c = PACK * g + 2 * j + e
-                    gain = gain_bias[:, c : c + 1]
-                    bias = gain_bias[:, CHUNKS + c : CHUNKS + c + 1]
-                    if j == 0 or not shared:
-                        nc.vector.tensor_scalar(
-                            out=v_tiles[n][:, c, :], in0=zt_banks[(n, g)][j][:, e, :], scalar1=gain, scalar2=bias,
-                            op0=ALU.mult, op1=ALU.add,
-                        )
-                    else:
-                        nc.scalar.activation(
-                            out=v_tiles[n][:, c, :], in_=zt_banks[(n, g)][j][:, e, :], func=FUNC.Identity,
-                            bias=bias, scale=gain,
-                        )
+                    nc.vector.tensor_scalar(
+                        out=v_tiles[n][:, c, :],
+                        in0=zt_banks[(n, g)][j][:, e, :],
+                        scalar1=gain_bias[:, c : c + 1],
+                        scalar2=gain_bias[:, CHUNKS + c : CHUNKS + c + 1],
+                        op0=ALU.mult,
+                        op1=ALU.add,
+                    )
 
-        def prepare_inputs(s):
-            d = s - D3_FIRST_STEP
-            for n in range(1 + X_PER_STEP * (s - 1), 1 + X_PER_STEP * s):
-                if 1 <= n < X_PAIRS:
-                    quantise_x(n)
-            if 0 <= d - 1 < OUT_TILES:
-                quantise_d3(d - 1)
-            for n in range(1 + X_PER_STEP * s, 1 + X_PER_STEP * (s + 1)):
-                if n + X_AHEAD < X_PAIRS:
-                    load_x(n + X_AHEAD)
-                if n < X_PAIRS:
-                    turn_x(n)
-            if 0 <= d + 2 < OUT_TILES:
-                load_d3(d + 2)
-            if 0 <= d < OUT_TILES:
-                turn_d3(d)
-
-        def front_step(s, shared):
+        def front_step(s):
             prepare_inputs(s)
             m = s - TURN_LAG
             if 0 <= m < ROW_TILES:
                 turn_hidden(m // 2, m % 2)
             if s < ROW_TILES:
-                row_statistics(s)
+                bank_statistics(s)
             if 0 <= s - 1 < ROW_TILES:
                 normalise(s - 1)
+            if s < ROW_TILES:
+                row_moments(s)
             if s + 1 < ROW_TILES:
                 first_matmul(s + 1)
             if 0 <= m < ROW_TILES:
-                gain_and_bias(m // 2, m % 2, shared)
+                gain_and_bias(m // 2, m % 2)
 
         def sigmoid_pair(n):
             q = qpool.tile([P, CHUNKS, PAIR], F32, name="q")
@@ -290,7 +283,7 @@ def tile_autoencoder_pb_t_kernel(tc, h_dec1, D2, g4, b4, D3, bo, out):
             rows = slice(P * (r % 2), P * (r % 2) + P)
             for g in range(PASSES):
                 chunks = slice(PACK * g, PACK * (g + 1))
-                engine = nc.vector if g == 1 and r >= ROW_TILES - BATCH_TILES[-1] else nc.gpsimd
+                engine = nc.vector if g == 1 and r >= ROW_TILES - BATCH else nc.gpsimd
                 engine.tensor_tensor(
                     out=hb[:, g].rearrange("p (c i) t -> p c t i", i=4),
                     in0=v_tiles[r // 2][:, chunks, rows].rearrange("p t (c i) -> p c t i", i=4),
@@ -332,80 +325,60 @@ def tile_autoencoder_pb_t_kernel(tc, h_dec1, D2, g4, b4, D3, bo, out):
             nc.vector.tensor_tensor(out=y[:, BANK:K_OUT], in0=narrow[:], in1=bo_rows[:, BANK:K_OUT], op=ALU.add)
             y_tiles[r] = y
 
-        def output_sigmoid(r):
-            y = y_tiles[r]
-            nc.scalar.activation(out=y[:], in_=y[:], func=FUNC.Sigmoid)
-            nc.sync.dma_start(out=out[P * r : P * (r + 1), :], in_=y[:])
-
-        progress = {"added": 0, "stored": 0}
-
         def back_tick(r):
             if 0 <= r - QUANT_LAG < ROW_TILES:
                 quantise_hidden(r - QUANT_LAG)
             if 0 <= r - BIAS_LAG < ROW_TILES:
                 add_bias(r - BIAS_LAG)
-                progress["added"] = r - BIAS_LAG + 1
             if 0 <= r - QUANT_LAG < ROW_TILES:
                 second_matmul(r - QUANT_LAG)
-            if r < ROW_TILES:
+            if 0 <= r < ROW_TILES:
                 mish_product(r)
 
-        def drain_outputs():
-            for r in range(progress["stored"], progress["added"]):
-                output_sigmoid(r)
-            progress["stored"] = progress["added"]
+        def output_sigmoids(first_tick, end_tick):
+            for r in range(max(first_tick - BIAS_LAG, 0), min(end_tick - BIAS_LAG, ROW_TILES)):
+                y = y_tiles[r]
+                nc.scalar.activation(out=y[:], in_=y[:], func=FUNC.Sigmoid)
+                nc.sync.dma_start(out=out[P * r : P * (r + 1), :], in_=y[:])
 
-        d2_raw = [load_rows(D2, n) for n in range(HIDDEN // PAIR)]
-        load_x(0)
+        d2_raw = [load_rows(D2, n) for n in range(D2_PAIRS)]
+        load_piece(0)
         nc.scalar.dma_start(out=gb_rows[0:CHUNKS, :], in_=g4.rearrange("(c p) -> c p", p=P))
         nc.scalar.dma_start(out=gb_rows[CHUNKS : 2 * CHUNKS, :], in_=b4.rearrange("(c p) -> c p", p=P))
         nc.scalar.dma_start(out=bo_rows[:], in_=bo.partition_broadcast(P))
-        for n in range(HIDDEN // PAIR):
+        for n in range(D2_PAIRS):
             cols = slice(PAIR * n, PAIR * (n + 1))
             quantise_rows(turn_rows(d2_raw[n]), d2_words[:, cols], d2_scales[:, cols])
-        turn_x(0)
-        quantise_x(0)
-        for n in range(1, 1 + X_AHEAD):
-            load_x(n)
+        turn_piece(0)
+        quantise_piece(0)
+        for n in range(1, 1 + PIECES_AHEAD):
+            load_piece(n)
         first_matmul(0)
         gb_turned = psum_o.tile([P, P], BF16, tag="bank", name="gb_turned")
         nc.tensor.transpose(out=gb_turned[:], in_=gb_rows[:], identity=ident_bf16[:])
         nc.vector.tensor_copy(out=gain_bias[:], in_=gb_turned[:, 0 : 2 * CHUNKS])
 
-        n_batches = len(BATCH_TILES)
-        first_tile = [sum(BATCH_TILES[:i]) for i in range(n_batches)]
-        last_step = [first_tile[i] + BATCH_TILES[i] - 1 + TURN_LAG for i in range(n_batches)]
+        def pairs(batch):
+            if 0 <= batch < N_BATCHES:
+                return range(BATCH * batch // 2, BATCH * (batch + 1) // 2)
+            return range(0)
 
-        for i in range(n_batches + 2):
-            back, middle, front = i - 2, i - 1, i
-            n_back = BATCH_TILES[back] if back >= 0 else 0
-            n_middle = BATCH_TILES[middle] if 0 <= middle < n_batches else 0
-            steps = []
-            if front < n_batches:
-                steps = list(range(last_step[front - 1] + 1 if front > 0 else 0, last_step[front] + 1))
-            ticks_1 = max(n_back, n_middle) // 2
-            clock = max(3 * ticks_1 + n_middle // 2, 1)
-
-            def others(lo, hi):
-                for j in range(n_back * lo // clock, n_back * hi // clock):
-                    back_tick(first_tile[back] + j)
-                for j in range(len(steps) * lo // clock, len(steps) * hi // clock):
-                    front_step(steps[j], i < SHARED_ROUNDS)
-
+        for s in range(TURN_LAG):
+            front_step(s)
+        for i in range(N_BATCHES + 2):
+            first_tick = BATCH * (i - 2)
             load_sigmoid_table()
-            for t in range(ticks_1):
-                drain_outputs()
-                if 2 * t < n_back:
-                    tanh_pair(first_tile[back] // 2 + t)
-                if 2 * t < n_middle:
-                    sigmoid_pair(first_tile[middle] // 2 + t)
-                others(3 * t, 3 * t + 3)
-            for t in range(n_middle // 2):
-                log_pair(first_tile[middle] // 2 + t)
-                others(3 * ticks_1 + t, 3 * ticks_1 + t + 1)
-            if ticks_1 == 0:
-                others(0, 1)
-
+            for n in pairs(i - 2):
+                tanh_pair(n)
+            output_sigmoids(first_tick - BATCH, first_tick)
+            for n in pairs(i - 1):
+                sigmoid_pair(n)
+            for n in pairs(i - 1):
+                log_pair(n)
+            for j in range(BATCH):
+                front_step(TURN_LAG + BATCH * i + j)
+                back_tick(first_tick + j)
+        output_sigmoids(ROW_TILES - BATCH, ROW_TILES)
         for r in range(ROW_TILES, ROW_TILES + BIAS_LAG):
             back_tick(r)
-            drain_outputs()
+            output_sigmoids(r, r + 1)

@@ -21,17 +21,31 @@ ROW_TILES = ROWS // P
 CHUNKS = HIDDEN // P
 PASSES = HIDDEN // (P * PACK)
 PAIR = 2 * P
-X_PAIRS = ROWS // PAIR
-D2_PAIRS = HIDDEN // PAIR
+PAIRS = ROWS // PAIR
+D2_PIECES = HIDDEN // PAIR
 D3_TILES = K_OUT // P
 
-BATCH = 4
-N_BATCHES = ROW_TILES // BATCH
-TURN_LAG = 3
-QUANT_LAG, BIAS_LAG = 2, 3
-N_PIECES = X_PAIRS + D3_TILES
-PIECES_PER_STEP = (N_PIECES - 1) // (TURN_LAG + BATCH)
-PIECES_AHEAD = 4
+BATCHES = (3, 2, 2, 2, 2, 2, 2, 1)
+D3_ON = "S"
+LAG = 8
+RATE = 1
+OUT_LESS = 0
+OFF = 0.5
+STAGE = 8
+RAWS = 8
+QUANTS = 1
+VBUFS = 6
+QBUFS = 5
+YBUFS = 10
+HBUFS = 4
+V_PROD = 0
+COPY_CYCLES = 3
+XS = 6
+X_LEAD = 2
+D3_FROM = 1
+S_GAIN = 2
+FIRST_GAIN = 1
+N_BATCHES = len(BATCHES)
 LN_FLOOR = 2.0 ** -60
 
 FLOPS = 2 * ROWS * K_IN * HIDDEN + 2 * ROWS * HIDDEN * K_OUT
@@ -41,14 +55,15 @@ def tile_autoencoder_pb_t_kernel(tc, h_dec1, D2, g4, b4, D3, bo, out):
     nc = tc.nc
     with ExitStack() as stack:
         const = stack.enter_context(tc.tile_pool(name="const", bufs=1))
-        raws = stack.enter_context(tc.tile_pool(name="raws", bufs=D2_PAIRS + 1 + PIECES_AHEAD))
-        stage = stack.enter_context(tc.tile_pool(name="stage", bufs=PIECES_PER_STEP + 1))
+        raws = stack.enter_context(tc.tile_pool(name="raws", bufs=RAWS))
+        stage = stack.enter_context(tc.tile_pool(name="stage", bufs=STAGE))
         small = stack.enter_context(tc.tile_pool(name="small", bufs=4))
-        zpool = stack.enter_context(tc.tile_pool(name="zpool", bufs=TURN_LAG + 2))
-        vpool = stack.enter_context(tc.tile_pool(name="vpool", bufs=3 * BATCH // 2 + 1))
-        qpool = stack.enter_context(tc.tile_pool(name="qpool", bufs=2 * BATCH // 2 + 1))
-        hpool = stack.enter_context(tc.tile_pool(name="hpool", bufs=QUANT_LAG + 2))
-        ypool = stack.enter_context(tc.tile_pool(name="ypool", bufs=BATCH + 2))
+        zpool = stack.enter_context(tc.tile_pool(name="zpool", bufs=4))
+        vpool = stack.enter_context(tc.tile_pool(name="vpool", bufs=VBUFS))
+        qpool = stack.enter_context(tc.tile_pool(name="qpool", bufs=QBUFS))
+        hpool = stack.enter_context(tc.tile_pool(name="hpool", bufs=HBUFS))
+        wpool = stack.enter_context(tc.tile_pool(name="wpool", bufs=2))
+        ypool = stack.enter_context(tc.tile_pool(name="ypool", bufs=YBUFS))
         psum_u = stack.enter_context(tc.psum_pool(name="psum_u", bufs=4))
         psum_turn = stack.enter_context(tc.psum_pool(name="psum_turn", bufs=2))
         psum_o = stack.enter_context(tc.psum_pool(name="psum_o", bufs=2))
@@ -58,7 +73,7 @@ def tile_autoencoder_pb_t_kernel(tc, h_dec1, D2, g4, b4, D3, bo, out):
         make_identity(nc, ident_f32[:])
         ident_bf16 = const.tile([P, P], BF16)
         make_identity(nc, ident_bf16[:])
-        minus_half = const.tile([P, 1], F32)
+        minus_half = const.tile([P, 2, 1], F32)
         nc.vector.memset(minus_half[:], -0.5)
         ln_floor = const.tile([P, 1], F32)
         nc.vector.memset(ln_floor[:], LN_FLOOR)
@@ -82,87 +97,83 @@ def tile_autoencoder_pb_t_kernel(tc, h_dec1, D2, g4, b4, D3, bo, out):
         bo_rows = const.tile([P, K_OUT], BF16)
         gain_bias = const.tile([P, 2 * CHUNKS], F32)
 
-        def load_rows(src, n):
-            raw = raws.tile([P, 2 * K_IN], BF16, name="raw")
-            nc.sync.dma_start(
-                out=raw[:].rearrange("p (a k) -> p a k", a=2),
-                in_=src[PAIR * n : PAIR * (n + 1), :].rearrange("(a p) k -> p a k", p=P),
-            )
-            return raw
+        raw = {}
+        turned = {}
+        grouped = {}
 
-        def turn_rows(raw):
-            words = raw[:].bitcast(F32)
-            turned = psum_o.tile([P, 2, PAIR], F32, tag="bank", name="turned")
-            for u in range(2):
-                for a in range(2):
-                    first = (K_IN // 2) * a + P * u
-                    nc.tensor.transpose(
-                        out=turned[:, u, P * a : P * (a + 1)],
-                        in_=words[:, first : first + P],
-                        identity=ident_f32[:],
-                    )
-            grouped = stage.tile([P, PAIR * PACK], BF16, align_bytes=64, tag="grouped", name="grouped")
-            nc.scalar.copy(
-                out=grouped[:].bitcast(F32).rearrange("p (r u) -> p r u", u=2),
-                in_=turned[:].rearrange("p u r -> p r u"),
-            )
-            return grouped
+        def source(key):
+            kind, n = key
+            return (D2 if kind == "w" else h_dec1)[PAIR * n : PAIR * (n + 1), :]
 
-        def quantise_rows(grouped, words, scales):
-            nc.vector.quantize_mx(out=words.bitcast(FP8X4), scales=scales, in_=grouped[:])
-
-        def load_d3(d):
-            raw = raws.tile([P, HIDDEN], BF16, name="raw")
-            nc.sync.dma_start(out=raw[:], in_=D3[P * d : P * (d + 1), :])
-            return raw
-
-        def turn_d3(raw):
-            turned = psum_o.tile([P, CHUNKS, P], BF16, tag="bank", name="turned3")
-            for c in range(CHUNKS):
-                nc.tensor.transpose(
-                    out=turned[:, c, :], in_=raw[:, P * c : P * (c + 1)], identity=ident_bf16[:]
-                )
-            grouped = stage.tile([P, PASSES, P, PACK], BF16, align_bytes=64, tag="grouped", name="grouped3")
-            nc.scalar.copy(out=grouped[:], in_=turned[:].rearrange("p (g t) r -> p g r t", t=PACK))
-            return grouped
-
-        def quantise_d3(grouped, d):
-            cols = slice(P * d, P * (d + 1))
-            for g in range(PASSES):
-                nc.vector.quantize_mx(
-                    out=d3_words[:, g, cols].bitcast(FP8X4),
-                    scales=d3_scales[:, g, cols],
-                    in_=grouped[:, g].rearrange("p r t -> p (r t)"),
-                )
-
-        piece_raw = {}
-        piece_grouped = {}
-
-        def load_piece(n):
-            piece_raw[n] = load_rows(h_dec1, n) if n < X_PAIRS else load_d3(n - X_PAIRS)
-
-        def turn_piece(n):
-            piece_grouped[n] = turn_rows(piece_raw[n]) if n < X_PAIRS else turn_d3(piece_raw[n])
-
-        def quantise_piece(n):
-            if n < X_PAIRS:
-                cols = slice(PAIR * n, PAIR * (n + 1))
-                quantise_rows(piece_grouped[n], x_words[:, cols], x_scales[:, cols])
+        def load(key):
+            kind, n = key
+            tile = raws.tile([P, 2 * K_IN], BF16, name="raw")
+            if kind == "d3":
+                nc.sync.dma_start(out=tile[:], in_=D3[P * n : P * (n + 1), :])
             else:
-                quantise_d3(piece_grouped[n], n - X_PAIRS)
+                nc.sync.dma_start(
+                    out=tile[:].rearrange("p (a k) -> p a k", a=2),
+                    in_=source(key).rearrange("(a p) k -> p a k", p=P),
+                )
+            raw[key] = tile
 
-        def prepare_inputs(s):
-            first = 1 + PIECES_PER_STEP * s
-            for n in range(max(first - PIECES_PER_STEP, 1), min(first, N_PIECES)):
-                quantise_piece(n)
-            for n in range(first, min(first + PIECES_PER_STEP, N_PIECES)):
-                if n + PIECES_AHEAD < N_PIECES:
-                    load_piece(n + PIECES_AHEAD)
-                turn_piece(n)
+        def turn(key, pool):
+            kind, n = key
+            if kind == "d3":
+                bank = pool.tile([P, CHUNKS, P], BF16, tag="bank", name="turned3")
+                for c in range(CHUNKS):
+                    nc.tensor.transpose(out=bank[:, c, :], in_=raw[key][:, P * c : P * (c + 1)], identity=ident_bf16[:])
+            else:
+                words = raw[key][:].bitcast(F32)
+                bank = pool.tile([P, 2, PAIR], F32, tag="bank", name="turned")
+                for u in range(2):
+                    for a in range(2):
+                        first = (K_IN // 2) * a + P * u
+                        nc.tensor.transpose(
+                            out=bank[:, u, P * a : P * (a + 1)],
+                            in_=words[:, first : first + P],
+                            identity=ident_f32[:],
+                        )
+            turned[key] = bank
+
+        def group(key, engine):
+            kind, n = key
+            if kind == "d3":
+                tile = stage.tile([P, PASSES, P, PACK], BF16, align_bytes=64, tag="grouped", name="grouped3")
+                o, i = tile[:], turned[key][:].rearrange("p (g t) r -> p g r t", t=PACK)
+                if engine == "V":
+                    nc.vector.tensor_copy(out=o, in_=i)
+                else:
+                    nc.scalar.copy(out=o, in_=i)
+            else:
+                tile = stage.tile([P, PAIR * PACK], BF16, align_bytes=64, tag="grouped", name="grouped")
+                o = tile[:].bitcast(F32).rearrange("p (r u) -> p r u", u=2)
+                i = turned[key][:].rearrange("p u r -> p r u")
+                if engine == "V":
+                    nc.vector.tensor_copy(out=o, in_=i)
+                else:
+                    nc.scalar.copy(out=o, in_=i)
+            grouped[key] = tile
+
+        def quantise(key):
+            kind, n = key
+            if kind == "d3":
+                cols = slice(P * n, P * (n + 1))
+                for g in range(PASSES):
+                    nc.vector.quantize_mx(
+                        out=d3_words[:, g, cols].bitcast(FP8X4),
+                        scales=d3_scales[:, g, cols],
+                        in_=grouped[key][:, g].rearrange("p r t -> p (r t)"),
+                    )
+            else:
+                cols = slice(PAIR * n, PAIR * (n + 1))
+                words, scales = (d2_words, d2_scales) if kind == "w" else (x_words, x_scales)
+                nc.vector.quantize_mx(out=words[:, cols].bitcast(FP8X4), scales=scales[:, cols], in_=grouped[key][:])
 
         u_banks = {}
-        bank_stats = {}
-        moments = {}
+        stats = {}
+        mean_var = {}
+        rstd = {}
         z_tiles = {}
         zt_banks = {}
         v_tiles = {}
@@ -187,29 +198,33 @@ def tile_autoencoder_pb_t_kernel(tc, h_dec1, D2, g4, b4, D3, bo, out):
             u_banks[r] = banks
 
         def bank_statistics(r):
-            stats = small.tile([P, 2, 6], F32, name="stats")
+            tile = small.tile([P, 2, 6], F32, name="stats")
             for half in range(2):
-                nc.vector.bn_stats(out=stats[:, half, :], in_=u_banks[r][half][:])
-            bank_stats[r] = stats
+                nc.vector.bn_stats(out=tile[:, half, :], in_=u_banks[r][half][:])
+            stats[r] = tile
 
-        def row_moments(r):
-            mean_var = small.tile([P, 2], F32, name="mean_var")
-            nc.vector.bn_aggr(out=mean_var[:], in_=bank_stats[r][:].rearrange("p a s -> p (a s)"))
-            var_eps = small.tile([P, 1], F32, name="var_eps")
-            nc.gpsimd.tensor_scalar_add(out=var_eps[:], in0=mean_var[:, 1:2], scalar1=EPS)
-            rstd = small.tile([P, 1], F32, name="rstd")
-            nc.gpsimd.tensor_tensor(out=rstd[:], in0=var_eps[:], in1=minus_half[:], op=ALU.pow)
-            moments[r] = (mean_var, rstd)
+        def row_moments(n):
+            tile = small.tile([P, 2, 2], F32, name="mean_var")
+            for a in range(2):
+                nc.vector.bn_aggr(out=tile[:, a, :], in_=stats[2 * n + a][:].rearrange("p a s -> p (a s)"))
+            mean_var[n] = tile
+
+        def reciprocal_deviations(n):
+            var_eps = small.tile([P, 2, 1], F32, name="var_eps")
+            nc.gpsimd.tensor_scalar_add(out=var_eps[:], in0=mean_var[n][:, :, 1:2], scalar1=EPS)
+            tile = small.tile([P, 2, 1], F32, name="rstd")
+            nc.gpsimd.tensor_tensor(out=tile[:], in0=var_eps[:], in1=minus_half[:], op=ALU.pow)
+            rstd[n] = tile
 
         def normalise(r):
-            mean_var, rstd = moments[r]
+            n, a = r // 2, r % 2
             z = zpool.tile([P, HIDDEN], F32, name="z")
             for half in range(2):
                 nc.vector.tensor_scalar(
                     out=z[:, BANK * half : BANK * (half + 1)],
                     in0=u_banks[r][half][:],
-                    scalar1=mean_var[:, 0:1],
-                    scalar2=rstd[:],
+                    scalar1=mean_var[n][:, a, 0:1],
+                    scalar2=rstd[n][:, a, 0:1],
                     op0=ALU.subtract,
                     op1=ALU.mult,
                 )
@@ -218,16 +233,16 @@ def tile_autoencoder_pb_t_kernel(tc, h_dec1, D2, g4, b4, D3, bo, out):
         def turn_hidden(n, g):
             banks = []
             for j in range(2):
-                turned = psum_turn.tile([P, 2, PAIR], F32, tag="bank", name="zt")
+                bank = psum_turn.tile([P, 2, PAIR], F32, tag="bank", name="zt")
                 for e in range(2):
                     c = PACK * g + 2 * j + e
                     for a in range(2):
                         nc.tensor.transpose(
-                            out=turned[:, e, P * a : P * (a + 1)],
+                            out=bank[:, e, P * a : P * (a + 1)],
                             in_=z_tiles[2 * n + a][:, P * c : P * (c + 1)],
                             identity=ident_f32[:],
                         )
-                banks.append(turned)
+                banks.append(bank)
             zt_banks[(n, g)] = banks
 
         def gain_and_bias(n, g):
@@ -237,30 +252,12 @@ def tile_autoencoder_pb_t_kernel(tc, h_dec1, D2, g4, b4, D3, bo, out):
             for j in range(2):
                 for e in range(2):
                     c = PACK * g + 2 * j + e
-                    nc.vector.tensor_scalar(
-                        out=v_tiles[n][:, c, :],
-                        in0=zt_banks[(n, g)][j][:, e, :],
-                        scalar1=gain_bias[:, c : c + 1],
-                        scalar2=gain_bias[:, CHUNKS + c : CHUNKS + c + 1],
-                        op0=ALU.mult,
-                        op1=ALU.add,
-                    )
-
-        def front_step(s):
-            prepare_inputs(s)
-            m = s - TURN_LAG
-            if 0 <= m < ROW_TILES:
-                turn_hidden(m // 2, m % 2)
-            if s < ROW_TILES:
-                bank_statistics(s)
-            if 0 <= s - 1 < ROW_TILES:
-                normalise(s - 1)
-            if s < ROW_TILES:
-                row_moments(s)
-            if s + 1 < ROW_TILES:
-                first_matmul(s + 1)
-            if 0 <= m < ROW_TILES:
-                gain_and_bias(m // 2, m % 2)
+                    gain, bias = gain_bias[:, c : c + 1], gain_bias[:, CHUNKS + c : CHUNKS + c + 1]
+                    o, i = v_tiles[n][:, c, :], zt_banks[(n, g)][j][:, e, :]
+                    if n < S_GAIN:
+                        nc.scalar.activation(out=o, in_=i, func=FUNC.Identity, scale=gain, bias=bias)
+                    else:
+                        nc.vector.tensor_scalar(out=o, in0=i, scalar1=gain, scalar2=bias, op0=ALU.mult, op1=ALU.add)
 
         def sigmoid_pair(n):
             q = qpool.tile([P, CHUNKS, PAIR], F32, name="q")
@@ -278,35 +275,37 @@ def tile_autoencoder_pb_t_kernel(tc, h_dec1, D2, g4, b4, D3, bo, out):
         o_banks = {}
         y_tiles = {}
 
-        def mish_product(r):
-            hb = hpool.tile([P, PASSES, P, PACK], BF16, align_bytes=64, name="hb")
-            rows = slice(P * (r % 2), P * (r % 2) + P)
-            for g in range(PASSES):
-                chunks = slice(PACK * g, PACK * (g + 1))
-                engine = nc.vector if g == 1 and r >= ROW_TILES - BATCH else nc.gpsimd
-                engine.tensor_tensor(
-                    out=hb[:, g].rearrange("p (c i) t -> p c t i", i=4),
-                    in0=v_tiles[r // 2][:, chunks, rows].rearrange("p t (c i) -> p c t i", i=4),
-                    in1=q_tiles[r // 2][:, chunks, rows].rearrange("p t (c i) -> p c t i", i=4),
-                    op=ALU.mult,
-                )
-            h_bf16[r] = hb
+        def mish_product(n):
+            hb = hpool.tile([P, 2, PASSES, P, PACK], BF16, align_bytes=64, name="hb")
+            for a in range(2):
+                rows = slice(P * a, P * (a + 1))
+                for g in range(PASSES):
+                    chunks = slice(PACK * g, PACK * (g + 1))
+                    engine = nc.vector if n >= PAIRS - V_PROD and g == 1 else nc.gpsimd
+                    engine.tensor_tensor(
+                        out=hb[:, a, g].rearrange("p (c i) t -> p c t i", i=4),
+                        in0=v_tiles[n][:, chunks, rows].rearrange("p t (c i) -> p c t i", i=4),
+                        in1=q_tiles[n][:, chunks, rows].rearrange("p t (c i) -> p c t i", i=4),
+                        op=ALU.mult,
+                    )
+            h_bf16[n] = hb
 
-        def quantise_hidden(r):
-            hw = hpool.tile([P, PASSES * P], U32, align_bytes=64, name="hw")
-            hs = hpool.tile([P, PASSES * P], U8, align_bytes=64, name="hs")
+        def quantise_hidden(n):
+            hw = wpool.tile([P, 2 * PASSES * P], U32, align_bytes=64, name="hw")
+            hs = wpool.tile([P, 2 * PASSES * P], U8, align_bytes=64, name="hs")
             nc.vector.quantize_mx(
-                out=hw[:].bitcast(FP8X4), scales=hs[:], in_=h_bf16[r][:].rearrange("p g r t -> p (g r t)"),
+                out=hw[:].bitcast(FP8X4), scales=hs[:], in_=h_bf16[n][:].rearrange("p a g r t -> p (a g r t)"),
             )
-            h_words[r] = (hw, hs)
+            h_words[n] = (hw, hs)
 
         def second_matmul(r):
-            hw, hs = h_words[r]
+            hw, hs = h_words[r // 2]
             wide = psum_o.tile([P, BANK], F32, tag="bank", name="wide")
             narrow = psum_o.tile([P, K_OUT - BANK], F32, tag="bank", name="narrow")
-            for g in range(PASSES):
-                cols = slice(P * g, P * (g + 1))
-                for acc, lo, hi in ((wide, 0, BANK), (narrow, BANK, K_OUT)):
+            for acc, lo, hi in ((wide, 0, BANK), (narrow, BANK, K_OUT)):
+                for g in range(PASSES):
+                    first = P * (PASSES * (r % 2) + g)
+                    cols = slice(first, first + P)
                     nc.tensor.matmul_mx(
                         out=acc[:],
                         lhsT=hw[:, cols].bitcast(FP8X4),
@@ -325,60 +324,248 @@ def tile_autoencoder_pb_t_kernel(tc, h_dec1, D2, g4, b4, D3, bo, out):
             nc.vector.tensor_tensor(out=y[:, BANK:K_OUT], in0=narrow[:], in1=bo_rows[:, BANK:K_OUT], op=ALU.add)
             y_tiles[r] = y
 
-        def back_tick(r):
-            if 0 <= r - QUANT_LAG < ROW_TILES:
-                quantise_hidden(r - QUANT_LAG)
-            if 0 <= r - BIAS_LAG < ROW_TILES:
-                add_bias(r - BIAS_LAG)
-            if 0 <= r - QUANT_LAG < ROW_TILES:
-                second_matmul(r - QUANT_LAG)
-            if 0 <= r < ROW_TILES:
-                mish_product(r)
+        def output_sigmoid(r):
+            y = y_tiles[r]
+            nc.scalar.activation(out=y[:], in_=y[:], func=FUNC.Sigmoid)
+            nc.sync.dma_start(out=out[P * r : P * (r + 1), :], in_=y[:])
 
-        def output_sigmoids(first_tick, end_tick):
-            for r in range(max(first_tick - BIAS_LAG, 0), min(end_tick - BIAS_LAG, ROW_TILES)):
-                y = y_tiles[r]
-                nc.scalar.activation(out=y[:], in_=y[:], func=FUNC.Sigmoid)
-                nc.sync.dma_start(out=out[P * r : P * (r + 1), :], in_=y[:])
+        def turn_gain_and_bias():
+            bank = psum_o.tile([P, P], BF16, tag="bank", name="gb_turned")
+            nc.tensor.transpose(out=bank[:], in_=gb_rows[:], identity=ident_bf16[:])
+            turned["gb"] = bank
 
-        d2_raw = [load_rows(D2, n) for n in range(D2_PAIRS)]
-        load_piece(0)
-        nc.scalar.dma_start(out=gb_rows[0:CHUNKS, :], in_=g4.rearrange("(c p) -> c p", p=P))
-        nc.scalar.dma_start(out=gb_rows[CHUNKS : 2 * CHUNKS, :], in_=b4.rearrange("(c p) -> c p", p=P))
-        nc.scalar.dma_start(out=bo_rows[:], in_=bo.partition_broadcast(P))
-        for n in range(D2_PAIRS):
-            cols = slice(PAIR * n, PAIR * (n + 1))
-            quantise_rows(turn_rows(d2_raw[n]), d2_words[:, cols], d2_scales[:, cols])
-        turn_piece(0)
-        quantise_piece(0)
-        for n in range(1, 1 + PIECES_AHEAD):
-            load_piece(n)
-        first_matmul(0)
-        gb_turned = psum_o.tile([P, P], BF16, tag="bank", name="gb_turned")
-        nc.tensor.transpose(out=gb_turned[:], in_=gb_rows[:], identity=ident_bf16[:])
-        nc.vector.tensor_copy(out=gain_bias[:], in_=gb_turned[:, 0 : 2 * CHUNKS])
+        def keep_gain_and_bias():
+            nc.vector.tensor_copy(out=gain_bias[:], in_=turned["gb"][:, 0 : 2 * CHUNKS])
+
+        streams = {"Q": [], "T": [], "S": [], "V": [], "G": []}
+        done = set()
+        starts = [sum(BATCHES[:n]) for n in range(N_BATCHES + 1)]
+
+        def add(engine, key, fn, *args, needs=()):
+            streams[engine].append((key, fn, args, tuple(needs)))
 
         def pairs(batch):
             if 0 <= batch < N_BATCHES:
-                return range(BATCH * batch // 2, BATCH * (batch + 1) // 2)
+                return range(starts[batch], starts[batch + 1])
             return range(0)
 
-        for s in range(TURN_LAG):
-            front_step(s)
+        W = [("w", n) for n in range(D2_PIECES)]
+        X = [("x", n) for n in range(PAIRS)]
+        Z = [("d3", n) for n in range(D3_TILES)]
+        head = [X[0], W[0], W[1], W[2], W[3]]
+        rest = X[1:XS]
+        early = set(rest)
+        pieces = head + rest
+        later = sorted([(max(n - X_LEAD, 0), 0, key) for n, key in enumerate(X) if n >= XS] + [(D3_FROM + j // 2, 1, key) for j, key in enumerate(Z)])
+        when = {len(pieces) + j: cyc for j, (cyc, kind, key) in enumerate(later)}
+        pieces += [key for cyc, kind, key in later]
+
+        for k, key in enumerate(pieces):
+            add("Q", ("load", key), load, key, needs=[("turn", pieces[k - RAWS])] if k >= RAWS else [])
+            if k == len(head):
+                add("Q", ("gbload",), lambda: (
+                    nc.scalar.dma_start(out=gb_rows[0:CHUNKS, :], in_=g4.rearrange("(c p) -> c p", p=P)),
+                    nc.scalar.dma_start(out=gb_rows[CHUNKS : 2 * CHUNKS, :], in_=b4.rearrange("(c p) -> c p", p=P)),
+                    nc.scalar.dma_start(out=bo_rows[:], in_=bo.partition_broadcast(P))))
+
+        allocs = {"h": [], "o": []}
+
+        def take(pool, reader):
+            allocs[pool].append(reader)
+            return allocs[pool][-3:-2]
+
+        def add_turn(k):
+            key = pieces[k]
+            name, pool = ("h", psum_turn) if k < len(head) and k % 2 else ("o", psum_o)
+            add("T", ("turn", key), turn, key, pool, needs=[("load", key)] + take(name, ("group", key)))
+
+        def add_group(k, engine):
+            key = pieces[k]
+            needs = [("turn", key)] + ([("quant", pieces[k - STAGE])] if k >= STAGE else [])
+            add(engine, ("group", key), group, key, engine, needs=needs)
+
+        def add_quant(key):
+            add("V", ("quant", key), quantise, key, needs=[("group", key)])
+
+        for k in range(len(head)):
+            add_turn(k)
+        for k in range(len(head)):
+            if k % 2 == 0:
+                add_group(k, "S")
+        add_group(1, "V")
+        add_quant(head[0])
+        add_quant(head[1])
+        add_group(3, "V")
+        add_quant(head[2])
+        add_quant(head[3])
+        add_quant(head[4])
+        for r in range(2):
+            add("T", ("mm1", r), first_matmul, r, needs=[("quant", key) for key in head])
+        add("T", ("gbturn",), turn_gain_and_bias, needs=[("gbload",)] + take("o", ("gb",)))
+
+        turn_next = [len(head)]
+
+        def turn_pieces(count, stop=len(head) + len(rest)):
+            for k in range(turn_next[0], min(turn_next[0] + count, stop)):
+                add_turn(k)
+                add_group(k, "S")
+            turn_next[0] = max(turn_next[0], min(turn_next[0] + count, stop))
+
+        def cycle(n, share=0, back=None):
+            live, last = n < PAIRS, 1 <= n <= PAIRS
+            late = [k for k in range(len(pieces)) if when.get(k) == n]
+            for k in late:
+                add_turn(k)
+            for k in late:
+                add_group(k, D3_ON if pieces[k][0] == "d3" else "V")
+            if live:
+                for r in (2 * n, 2 * n + 1):
+                    add("V", ("stats", r), bank_statistics, r, needs=[("mm1", r)])
+                add("V", ("moments", n), row_moments, n)
+                add("G", ("rstd", n), reciprocal_deviations, n, needs=[("moments", n)])
+            if n == 0:
+                add("V", ("gb",), keep_gain_and_bias, needs=[("gbturn",)])
+                turn_pieces(2)
+                add_quant(X[1])
+
+            def gain(g):
+                needs = [("zt", n - 1, g)]
+                if n - 1 >= VBUFS:
+                    needs.append(("prod", n - 1 - VBUFS))
+                add("S" if n - 1 < S_GAIN else "V", ("gain", n - 1, g), gain_and_bias, n - 1, g, needs=needs)
+
+            def norm(r):
+                needs = [("rstd", n)]
+                if n >= 2:
+                    needs.append(("zt", n - 2, 1))
+                add("V", ("norm", r), normalise, r, needs=needs)
+                if r + 2 < ROW_TILES:
+                    add("T", ("mm1", r + 2), first_matmul, r + 2, needs=[("norm", r), ("quant", X[n + 1])])
+
+            if last:
+                gain(0)
+                add("T", ("zt", n - 1, 1), turn_hidden, n - 1, 1, needs=[("gain", n - 1, 0)])
+            if back is not None:
+                quanth(back)
+                multiply(2 * back)
+            turn_pieces(share - 2 * (share // 3))
+            if n == 1 and FIRST_GAIN:
+                gain(1)
+            if live:
+                norm(2 * n)
+            if back is not None:
+                bias(2 * back)
+                multiply(2 * back + 1)
+            if live:
+                norm(2 * n + 1)
+            turn_pieces(share // 3)
+            if last and not (n == 1 and FIRST_GAIN):
+                gain(1)
+            if live:
+                add("T", ("zt", n, 0), turn_hidden, n, 0, needs=[("norm", 2 * n + 1)] + ([("gain", n - 1, 1)] if n else []))
+            if back is not None:
+                bias(2 * back + 1)
+            turn_pieces(share // 3)
+            for key in pieces[len(head) + 1 + QUANTS * n : len(head) + 1 + QUANTS * (n + 1)]:
+                if key in early:
+                    add_quant(key)
+            for k in late:
+                add_quant(pieces[k])
+
+        def product_tick(n):
+            needs = [("tanh", n)]
+            if n >= HBUFS:
+                needs.append(("quanth", n - HBUFS))
+            add("G", ("prod", n), mish_product, n, needs=needs)
+
+        bias_added = [0]
+
+        def bias(r):
+            needs = [("mm2", r)]
+            if r >= YBUFS:
+                needs.append(("outsig", r - YBUFS))
+            add("V", ("bias", r), add_bias, r, needs=needs)
+            bias_added[0] = r + 1
+
+        def quanth(n):
+            needs = [("prod", n)]
+            if n >= 2:
+                needs.append(("mm2", 2 * (n - 2) + 1))
+            add("V", ("quanth", n), quantise_hidden, n, needs=needs)
+
+        def multiply(r):
+            needs = [("quanth", r // 2)] + [("quant", key) for key in Z]
+            needs += take("o", ("bias", r))
+            needs += take("o", ("bias", r))
+            add("T", ("mm2", r), second_matmul, r, needs=needs)
+
+        out_done = 0
+        first_cycle = max(S_GAIN, starts[1]) + 1
+        for n in range(first_cycle):
+            cycle(n, -(-(len(rest) - 2) // COPY_CYCLES))
+        back_done = 0
+        prod_added = 0
         for i in range(N_BATCHES + 2):
-            first_tick = BATCH * (i - 2)
-            load_sigmoid_table()
-            for n in pairs(i - 2):
-                tanh_pair(n)
-            output_sigmoids(first_tick - BATCH, first_tick)
+            add("S", ("table", i), load_sigmoid_table)
             for n in pairs(i - 1):
-                sigmoid_pair(n)
-            for n in pairs(i - 1):
-                log_pair(n)
-            for j in range(BATCH):
-                front_step(TURN_LAG + BATCH * i + j)
-                back_tick(first_tick + j)
-        output_sigmoids(ROW_TILES - BATCH, ROW_TILES)
-        for r in range(ROW_TILES, ROW_TILES + BIAS_LAG):
-            back_tick(r)
-            output_sigmoids(r, r + 1)
+                add("S", ("tanh", n), tanh_pair, n)
+            for n in pairs(i):
+                needs = [("gain", n, 1)]
+                if n >= QBUFS:
+                    needs.append(("prod", n - QBUFS))
+                add("S", ("sig", n), sigmoid_pair, n, needs=needs)
+            out_end = ROW_TILES if i > N_BATCHES else max(out_done, bias_added[0] - OUT_LESS)
+            for r in range(out_done, out_end):
+                add("S", ("outsig", r), output_sigmoid, r, needs=[("bias", r)])
+            out_done = out_end
+            for n in pairs(i):
+                add("S", ("ln", n), log_pair, n)
+            if i > N_BATCHES:
+                continue
+            last_round = i == N_BATCHES
+            fronts = [c for c in range(pairs(i + 1).start + 1, pairs(i + 1).stop + 1) if c >= first_cycle]
+            prods = list(pairs(i - 1))
+            merged = [((j + 0.5) / len(fronts), 0, c) for j, c in enumerate(fronts)]
+            merged += [(OFF + (1 - OFF) * (j + 0.5) / len(prods), 1, n) for j, n in enumerate(prods)]
+            for pos, kind, n in sorted(merged):
+                if kind == 1:
+                    product_tick(n)
+                    prod_added = n + 1
+                    continue
+                due = min(prod_added, int((n + 1 - LAG) * RATE))
+                if back_done < due:
+                    cycle(n, back=back_done)
+                    back_done += 1
+                else:
+                    cycle(n)
+                if back_done < due and RATE > 1:
+                    quanth(back_done)
+                    multiply(2 * back_done)
+                    bias(2 * back_done)
+                    multiply(2 * back_done + 1)
+                    bias(2 * back_done + 1)
+                    back_done += 1
+        for n in range(back_done, PAIRS):
+            quanth(n)
+            multiply(2 * n)
+            if n > back_done:
+                bias(2 * n - 1)
+            bias(2 * n)
+            multiply(2 * n + 1)
+        bias(ROW_TILES - 1)
+
+        heads = {e: 0 for e in streams}
+        moved = True
+        while moved:
+            moved = False
+            for e in streams:
+                while heads[e] < len(streams[e]):
+                    key, fn, args, needs = streams[e][heads[e]]
+                    if not all(k in done for k in needs):
+                        break
+                    fn(*args)
+                    done.add(key)
+                    heads[e] += 1
+                    moved = True
+        stuck = [(e, streams[e][heads[e]][0], [k for k in streams[e][heads[e]][3] if k not in done]) for e in streams if heads[e] < len(streams[e])]
+        assert not stuck, str(stuck)

@@ -25,26 +25,28 @@ PAIRS = ROWS // PAIR
 D2_PIECES = HIDDEN // PAIR
 D3_TILES = K_OUT // P
 
-BATCHES = (3, 2, 2, 2, 2, 2, 2, 1)
-D3_ON = "S"
-LAG = 8
-RATE = 1
+BATCHES = (2, 2, 2, 2, 2, 2, 2, 2)
+D3_ON = "V"
+PROD_LAG = 14
+BACK_LAG = 3
+FLUSH_AHEAD = 2
+LAST_OUT = 0
 OUT_LESS = 0
-OFF = 0.5
-STAGE = 8
+STAGE = 5
 RAWS = 8
-QUANTS = 1
-VBUFS = 6
-QBUFS = 5
-YBUFS = 10
+VBUFS = 7
+QBUFS = 6
+YBUFS = 8
 HBUFS = 4
-V_PROD = 0
-COPY_CYCLES = 3
+V_PROD = 12
+COPY_STEPS = 4
+ZBUFS = 5
+TURN_LAG = 3
 XS = 6
-X_LEAD = 2
-D3_FROM = 1
+X_LEAD = 4
+D3_FROM = 10
 S_GAIN = 2
-FIRST_GAIN = 1
+S_NORM = 0
 N_BATCHES = len(BATCHES)
 LN_FLOOR = 2.0 ** -60
 
@@ -58,7 +60,7 @@ def tile_autoencoder_pb_t_kernel(tc, h_dec1, D2, g4, b4, D3, bo, out):
         raws = stack.enter_context(tc.tile_pool(name="raws", bufs=RAWS))
         stage = stack.enter_context(tc.tile_pool(name="stage", bufs=STAGE))
         small = stack.enter_context(tc.tile_pool(name="small", bufs=4))
-        zpool = stack.enter_context(tc.tile_pool(name="zpool", bufs=4))
+        zpool = stack.enter_context(tc.tile_pool(name="zpool", bufs=ZBUFS))
         vpool = stack.enter_context(tc.tile_pool(name="vpool", bufs=VBUFS))
         qpool = stack.enter_context(tc.tile_pool(name="qpool", bufs=QBUFS))
         hpool = stack.enter_context(tc.tile_pool(name="hpool", bufs=HBUFS))
@@ -73,7 +75,7 @@ def tile_autoencoder_pb_t_kernel(tc, h_dec1, D2, g4, b4, D3, bo, out):
         make_identity(nc, ident_f32[:])
         ident_bf16 = const.tile([P, P], BF16)
         make_identity(nc, ident_bf16[:])
-        minus_half = const.tile([P, 2, 1], F32)
+        minus_half = const.tile([P, 1], F32)
         nc.vector.memset(minus_half[:], -0.5)
         ln_floor = const.tile([P, 1], F32)
         nc.vector.memset(ln_floor[:], LN_FLOOR)
@@ -174,6 +176,7 @@ def tile_autoencoder_pb_t_kernel(tc, h_dec1, D2, g4, b4, D3, bo, out):
         stats = {}
         mean_var = {}
         rstd = {}
+        shift = {}
         z_tiles = {}
         zt_banks = {}
         v_tiles = {}
@@ -184,7 +187,7 @@ def tile_autoencoder_pb_t_kernel(tc, h_dec1, D2, g4, b4, D3, bo, out):
             banks = []
             for half in range(HIDDEN // BANK):
                 hid = slice(BANK * half, BANK * (half + 1))
-                u = psum_u.tile([P, BANK], F32, name="u")
+                u = psum_u.tile([P, BANK], F32, tag="u", name="u")
                 nc.tensor.matmul_mx(
                     out=u[:],
                     lhsT=x_words[:, cols].bitcast(FP8X4),
@@ -203,31 +206,42 @@ def tile_autoencoder_pb_t_kernel(tc, h_dec1, D2, g4, b4, D3, bo, out):
                 nc.vector.bn_stats(out=tile[:, half, :], in_=u_banks[r][half][:])
             stats[r] = tile
 
-        def row_moments(n):
-            tile = small.tile([P, 2, 2], F32, name="mean_var")
-            for a in range(2):
-                nc.vector.bn_aggr(out=tile[:, a, :], in_=stats[2 * n + a][:].rearrange("p a s -> p (a s)"))
-            mean_var[n] = tile
+        def row_moments(r):
+            tile = small.tile([P, 2], F32, name="mean_var")
+            nc.vector.bn_aggr(out=tile[:], in_=stats[r][:].rearrange("p a s -> p (a s)"))
+            mean_var[r] = tile
 
-        def reciprocal_deviations(n):
-            var_eps = small.tile([P, 2, 1], F32, name="var_eps")
-            nc.gpsimd.tensor_scalar_add(out=var_eps[:], in0=mean_var[n][:, :, 1:2], scalar1=EPS)
-            tile = small.tile([P, 2, 1], F32, name="rstd")
+        def reciprocal_deviation(r):
+            var_eps = small.tile([P, 1], F32, name="var_eps")
+            nc.gpsimd.tensor_scalar_add(out=var_eps[:], in0=mean_var[r][:, 1:2], scalar1=EPS)
+            tile = small.tile([P, 1], F32, name="rstd")
             nc.gpsimd.tensor_tensor(out=tile[:], in0=var_eps[:], in1=minus_half[:], op=ALU.pow)
-            rstd[n] = tile
+            rstd[r] = tile
+            if on_scalar(r):
+                product = small.tile([P, 1], F32, name="product")
+                nc.gpsimd.tensor_tensor(out=product[:], in0=mean_var[r][:, 0:1], in1=tile[:], op=ALU.mult)
+                minus = small.tile([P, 1], F32, name="minus")
+                nc.gpsimd.tensor_scalar(out=minus[:], in0=product[:], scalar1=-1.0, scalar2=0.0, op0=ALU.mult, op1=ALU.add)
+                shift[r] = minus
+
+        def on_scalar(r):
+            return r % 2 == 1 and r < 2 * S_NORM
 
         def normalise(r):
-            n, a = r // 2, r % 2
             z = zpool.tile([P, HIDDEN], F32, name="z")
             for half in range(2):
-                nc.vector.tensor_scalar(
-                    out=z[:, BANK * half : BANK * (half + 1)],
-                    in0=u_banks[r][half][:],
-                    scalar1=mean_var[n][:, a, 0:1],
-                    scalar2=rstd[n][:, a, 0:1],
-                    op0=ALU.subtract,
-                    op1=ALU.mult,
-                )
+                cols = slice(BANK * half, BANK * (half + 1))
+                if on_scalar(r):
+                    nc.scalar.activation(
+                        out=z[:, cols], in_=u_banks[r][half][:], func=FUNC.Identity,
+                        scale=rstd[r][:], bias=shift[r][:],
+                    )
+                else:
+                    nc.vector.tensor_scalar(
+                        out=z[:, cols], in0=u_banks[r][half][:],
+                        scalar1=mean_var[r][:, 0:1], scalar2=rstd[r][:],
+                        op0=ALU.subtract, op1=ALU.mult,
+                    )
             z_tiles[r] = z
 
         def turn_hidden(n, g):
@@ -275,20 +289,21 @@ def tile_autoencoder_pb_t_kernel(tc, h_dec1, D2, g4, b4, D3, bo, out):
         o_banks = {}
         y_tiles = {}
 
-        def mish_product(n):
-            hb = hpool.tile([P, 2, PASSES, P, PACK], BF16, align_bytes=64, name="hb")
-            for a in range(2):
-                rows = slice(P * a, P * (a + 1))
-                for g in range(PASSES):
-                    chunks = slice(PACK * g, PACK * (g + 1))
-                    engine = nc.vector if n >= PAIRS - V_PROD and g == 1 else nc.gpsimd
-                    engine.tensor_tensor(
-                        out=hb[:, a, g].rearrange("p (c i) t -> p c t i", i=4),
-                        in0=v_tiles[n][:, chunks, rows].rearrange("p t (c i) -> p c t i", i=4),
-                        in1=q_tiles[n][:, chunks, rows].rearrange("p t (c i) -> p c t i", i=4),
-                        op=ALU.mult,
-                    )
-            h_bf16[n] = hb
+        def mish_product(r):
+            n, a = r // 2, r % 2
+            if a == 0:
+                hb = hpool.tile([P, 2, PASSES, P, PACK], BF16, align_bytes=64, name="hb")
+                h_bf16[n] = hb
+            rows = slice(P * a, P * (a + 1))
+            for g in range(PASSES):
+                chunks = slice(PACK * g, PACK * (g + 1))
+                engine = nc.vector if r >= ROW_TILES - V_PROD and r % 2 else nc.gpsimd
+                engine.tensor_tensor(
+                    out=h_bf16[n][:, a, g].rearrange("p (c i) t -> p c t i", i=4),
+                    in0=v_tiles[n][:, chunks, rows].rearrange("p t (c i) -> p c t i", i=4),
+                    in1=q_tiles[n][:, chunks, rows].rearrange("p t (c i) -> p c t i", i=4),
+                    op=ALU.mult,
+                )
 
         def quantise_hidden(n):
             hw = wpool.tile([P, 2 * PASSES * P], U32, align_bytes=64, name="hw")
@@ -298,10 +313,14 @@ def tile_autoencoder_pb_t_kernel(tc, h_dec1, D2, g4, b4, D3, bo, out):
             )
             h_words[n] = (hw, hs)
 
-        def second_matmul(r):
+        def second_matmul(r, flush):
             hw, hs = h_words[r // 2]
-            wide = psum_o.tile([P, BANK], F32, tag="bank", name="wide")
-            narrow = psum_o.tile([P, K_OUT - BANK], F32, tag="bank", name="narrow")
+            if flush:
+                wide = psum_u.tile([P, BANK], F32, tag="u", name="wide")
+                narrow = psum_u.tile([P, K_OUT - BANK], F32, tag="u", name="narrow")
+            else:
+                wide = psum_o.tile([P, BANK], F32, tag="bank", name="wide")
+                narrow = psum_o.tile([P, K_OUT - BANK], F32, tag="bank", name="narrow")
             for acc, lo, hi in ((wide, 0, BANK), (narrow, BANK, K_OUT)):
                 for g in range(PASSES):
                     first = P * (PASSES * (r % 2) + g)
@@ -356,7 +375,7 @@ def tile_autoencoder_pb_t_kernel(tc, h_dec1, D2, g4, b4, D3, bo, out):
         rest = X[1:XS]
         early = set(rest)
         pieces = head + rest
-        later = sorted([(max(n - X_LEAD, 0), 0, key) for n, key in enumerate(X) if n >= XS] + [(D3_FROM + j // 2, 1, key) for j, key in enumerate(Z)])
+        later = sorted([(max(2 * n - X_LEAD, 0), 0, key) for n, key in enumerate(X) if n >= XS] + [(D3_FROM + j, 1, key) for j, key in enumerate(Z)])
         when = {len(pieces) + j: cyc for j, (cyc, kind, key) in enumerate(later)}
         pieces += [key for cyc, kind, key in later]
 
@@ -411,72 +430,61 @@ def tile_autoencoder_pb_t_kernel(tc, h_dec1, D2, g4, b4, D3, bo, out):
                 add_group(k, "S")
             turn_next[0] = max(turn_next[0], min(turn_next[0] + count, stop))
 
-        def cycle(n, share=0, back=None):
-            live, last = n < PAIRS, 1 <= n <= PAIRS
-            late = [k for k in range(len(pieces)) if when.get(k) == n]
+        def step(s, share=0, back=()):
+            m = s - TURN_LAG
+            n, g = m // 2, m % 2
+            early_m = s - 2
+            late = [k for k in range(len(pieces)) if when.get(k) == s]
+            if 2 * S_GAIN <= m < ROW_TILES:
+                needs = [("norm", 2 * n + 1)] + ([("gain", (m - 1) // 2, (m - 1) % 2)] if m else [])
+                add("T", ("zt", n, g), turn_hidden, n, g, needs=needs)
+            if s < ROW_TILES:
+                add("V", ("stats", s), bank_statistics, s, needs=[("mm1", s)])
+            if 0 <= s - 1 < ROW_TILES:
+                r = s - 1
+                needs = [("rstd", r)]
+                if r >= ZBUFS:
+                    needs.append(("zt", (r - ZBUFS) // 2, 1))
+                add("S" if on_scalar(r) else "V", ("norm", r), normalise, r, needs=needs)
+            if s < ROW_TILES:
+                add("V", ("moments", s), row_moments, s)
+                add("G", ("rstd", s), reciprocal_deviation, s, needs=[("moments", s)])
+            if s == 1:
+                add("V", ("gb",), keep_gain_and_bias, needs=[("gbturn",)])
+            if 1 < s + 1 < ROW_TILES:
+                needs = [("quant", X[(s + 1) // 2])] + ([("norm", s - 1)] if s else [])
+                add("T", ("mm1", s + 1), first_matmul, s + 1, needs=needs)
+            if 0 <= early_m < 2 * S_GAIN:
+                n, g = early_m // 2, early_m % 2
+                needs = [("norm", 2 * n + 1)] + ([("gain", (early_m - 1) // 2, (early_m - 1) % 2)] if early_m else [])
+                add("T", ("zt", n, g), turn_hidden, n, g, needs=needs)
+                add("S", ("gain", n, g), gain_and_bias, n, g, needs=[("zt", n, g)])
+                if g == 1 and n < starts[1]:
+                    add("S", ("sig", n), sigmoid_pair, n)
+                n, g = m // 2, m % 2
             for k in late:
                 add_turn(k)
+            for f, arg in back:
+                f(arg)
+            turn_pieces(share)
+            if 2 * S_GAIN <= m < ROW_TILES:
+                needs = [("zt", n, g)]
+                if n >= VBUFS:
+                    needs.append(("prod", 2 * (n - VBUFS) + 1))
+                add("V", ("gain", n, g), gain_and_bias, n, g, needs=needs)
+            if s % 2 == 0 and 1 <= (s + 2) // 2 < XS:
+                add_quant(X[(s + 2) // 2])
+            for k in range(len(pieces)):
+                if when.get(k) == s - 1:
+                    add_quant(pieces[k])
             for k in late:
                 add_group(k, D3_ON if pieces[k][0] == "d3" else "V")
-            if live:
-                for r in (2 * n, 2 * n + 1):
-                    add("V", ("stats", r), bank_statistics, r, needs=[("mm1", r)])
-                add("V", ("moments", n), row_moments, n)
-                add("G", ("rstd", n), reciprocal_deviations, n, needs=[("moments", n)])
-            if n == 0:
-                add("V", ("gb",), keep_gain_and_bias, needs=[("gbturn",)])
-                turn_pieces(2)
-                add_quant(X[1])
 
-            def gain(g):
-                needs = [("zt", n - 1, g)]
-                if n - 1 >= VBUFS:
-                    needs.append(("prod", n - 1 - VBUFS))
-                add("S" if n - 1 < S_GAIN else "V", ("gain", n - 1, g), gain_and_bias, n - 1, g, needs=needs)
-
-            def norm(r):
-                needs = [("rstd", n)]
-                if n >= 2:
-                    needs.append(("zt", n - 2, 1))
-                add("V", ("norm", r), normalise, r, needs=needs)
-                if r + 2 < ROW_TILES:
-                    add("T", ("mm1", r + 2), first_matmul, r + 2, needs=[("norm", r), ("quant", X[n + 1])])
-
-            if last:
-                gain(0)
-                add("T", ("zt", n - 1, 1), turn_hidden, n - 1, 1, needs=[("gain", n - 1, 0)])
-            if back is not None:
-                quanth(back)
-                multiply(2 * back)
-            turn_pieces(share - 2 * (share // 3))
-            if n == 1 and FIRST_GAIN:
-                gain(1)
-            if live:
-                norm(2 * n)
-            if back is not None:
-                bias(2 * back)
-                multiply(2 * back + 1)
-            if live:
-                norm(2 * n + 1)
-            turn_pieces(share // 3)
-            if last and not (n == 1 and FIRST_GAIN):
-                gain(1)
-            if live:
-                add("T", ("zt", n, 0), turn_hidden, n, 0, needs=[("norm", 2 * n + 1)] + ([("gain", n - 1, 1)] if n else []))
-            if back is not None:
-                bias(2 * back + 1)
-            turn_pieces(share // 3)
-            for key in pieces[len(head) + 1 + QUANTS * n : len(head) + 1 + QUANTS * (n + 1)]:
-                if key in early:
-                    add_quant(key)
-            for k in late:
-                add_quant(pieces[k])
-
-        def product_tick(n):
-            needs = [("tanh", n)]
-            if n >= HBUFS:
-                needs.append(("quanth", n - HBUFS))
-            add("G", ("prod", n), mish_product, n, needs=needs)
+        def product_tick(r):
+            needs = [("tanh", r // 2)]
+            if r // 2 >= HBUFS:
+                needs.append(("quanth", r // 2 - HBUFS))
+            add("V" if r >= ROW_TILES - V_PROD and r % 2 else "G", ("prod", r), mish_product, r, needs=needs)
 
         bias_added = [0]
 
@@ -487,72 +495,90 @@ def tile_autoencoder_pb_t_kernel(tc, h_dec1, D2, g4, b4, D3, bo, out):
             add("V", ("bias", r), add_bias, r, needs=needs)
             bias_added[0] = r + 1
 
+        flushing = []
+
         def quanth(n):
-            needs = [("prod", n)]
+            needs = [("prod", 2 * n + 1)]
             if n >= 2:
                 needs.append(("mm2", 2 * (n - 2) + 1))
             add("V", ("quanth", n), quantise_hidden, n, needs=needs)
 
         def multiply(r):
             needs = [("quanth", r // 2)] + [("quant", key) for key in Z]
-            needs += take("o", ("bias", r))
-            needs += take("o", ("bias", r))
-            add("T", ("mm2", r), second_matmul, r, needs=needs)
+            if flushing:
+                needs += [("norm", ROW_TILES - 1)]
+                if len(flushing) > 2:
+                    needs.append(("bias", flushing[-3]))
+            else:
+                needs += take("o", ("bias", r))
+                needs += take("o", ("bias", r))
+            add("T", ("mm2", r), second_matmul, r, bool(flushing), needs=needs)
 
+        def back_calls(s):
+            nonlocal_back = state["back"]
+            calls = []
+            t = nonlocal_back
+            ready = t > 2 * PAIRS - 1 or 2 * (t // 2) + 2 <= state["prods"]
+            if t <= 2 * PAIRS and ready and s >= t + PROD_LAG + BACK_LAG:
+                if t >= 1:
+                    calls.append((bias, t - 1))
+                if t < 2 * PAIRS:
+                    if t % 2 == 0:
+                        calls.append((quanth, t // 2))
+                    calls.append((multiply, t))
+                state["back"] = t + 1
+            return calls
+
+        state = {"back": 0, "prods": 0}
+        for s in range(TURN_LAG + ROW_TILES):
+            r = s - PROD_LAG
+            if 0 <= r < ROW_TILES:
+                product_tick(r)
+                state["prods"] = r + 1
+            step(s, share=-(-len(rest) // COPY_STEPS), back=back_calls(s))
+        first = state["back"]
+        pending = [first - 1] if first >= 1 else []
+        for t in range(first, 2 * PAIRS):
+            if t % 2 == 0:
+                for r in range(state["prods"], min(t + 2 + FLUSH_AHEAD, ROW_TILES)):
+                    product_tick(r)
+                    state["prods"] = r + 1
+                quanth(t // 2)
+            flushing.append(t)
+            multiply(t)
+            if len(pending) == 2:
+                bias(pending.pop(0))
+            pending.append(t)
+        for t in pending:
+            bias(t)
         out_done = 0
-        first_cycle = max(S_GAIN, starts[1]) + 1
-        for n in range(first_cycle):
-            cycle(n, -(-(len(rest) - 2) // COPY_CYCLES))
-        back_done = 0
-        prod_added = 0
         for i in range(N_BATCHES + 2):
             add("S", ("table", i), load_sigmoid_table)
             for n in pairs(i - 1):
                 add("S", ("tanh", n), tanh_pair, n)
-            for n in pairs(i):
-                needs = [("gain", n, 1)]
-                if n >= QBUFS:
-                    needs.append(("prod", n - QBUFS))
-                add("S", ("sig", n), sigmoid_pair, n, needs=needs)
-            out_end = ROW_TILES if i > N_BATCHES else max(out_done, bias_added[0] - OUT_LESS)
-            for r in range(out_done, out_end):
-                add("S", ("outsig", r), output_sigmoid, r, needs=[("bias", r)])
+            if i < N_BATCHES:
+                last_step = TURN_LAG + 2 * pairs(i).stop - 1
+                out_end = max(out_done, min(ROW_TILES, last_step - PROD_LAG - BACK_LAG - OUT_LESS))
+            elif i == N_BATCHES:
+                out_end = max(out_done, starts[i - 1] * 2 - LAST_OUT)
+            else:
+                out_end = ROW_TILES
+            outs = list(range(out_done, out_end))
             out_done = out_end
             for n in pairs(i):
+                if n == pairs(i).stop - 1:
+                    for r in outs:
+                        add("S", ("outsig", r), output_sigmoid, r, needs=[("bias", r)])
+                    outs = []
+                needs = [("gain", n, 1)]
+                if n >= QBUFS:
+                    needs.append(("prod", 2 * (n - QBUFS) + 1))
+                if n >= min(S_GAIN, starts[1]):
+                    add("S", ("sig", n), sigmoid_pair, n, needs=needs)
+            for r in outs:
+                add("S", ("outsig", r), output_sigmoid, r, needs=[("bias", r)])
+            for n in pairs(i):
                 add("S", ("ln", n), log_pair, n)
-            if i > N_BATCHES:
-                continue
-            last_round = i == N_BATCHES
-            fronts = [c for c in range(pairs(i + 1).start + 1, pairs(i + 1).stop + 1) if c >= first_cycle]
-            prods = list(pairs(i - 1))
-            merged = [((j + 0.5) / len(fronts), 0, c) for j, c in enumerate(fronts)]
-            merged += [(OFF + (1 - OFF) * (j + 0.5) / len(prods), 1, n) for j, n in enumerate(prods)]
-            for pos, kind, n in sorted(merged):
-                if kind == 1:
-                    product_tick(n)
-                    prod_added = n + 1
-                    continue
-                due = min(prod_added, int((n + 1 - LAG) * RATE))
-                if back_done < due:
-                    cycle(n, back=back_done)
-                    back_done += 1
-                else:
-                    cycle(n)
-                if back_done < due and RATE > 1:
-                    quanth(back_done)
-                    multiply(2 * back_done)
-                    bias(2 * back_done)
-                    multiply(2 * back_done + 1)
-                    bias(2 * back_done + 1)
-                    back_done += 1
-        for n in range(back_done, PAIRS):
-            quanth(n)
-            multiply(2 * n)
-            if n > back_done:
-                bias(2 * n - 1)
-            bias(2 * n)
-            multiply(2 * n + 1)
-        bias(ROW_TILES - 1)
 
         heads = {e: 0 for e in streams}
         moved = True

@@ -25,27 +25,30 @@ PAIRS = ROWS // PAIR
 D2_PIECES = HIDDEN // PAIR
 D3_TILES = K_OUT // P
 
-BATCHES = (2, 2, 2, 2, 2, 2, 2, 2)
+BATCHES = (4, 3, 3, 3, 3)
 D3_ON = "V"
-PROD_LAG = 14
-BACK_LAG = 3
-FLUSH_AHEAD = 2
+PROD_LAG = 15
+BACK_LAG = 6
+RATE = 1
+FLUSH_AHEAD = 5
+FLUSH_DEPTH = 4
+FLUSH_HOLD = 3
 LAST_OUT = 0
 OUT_LESS = 0
-STAGE = 5
+STAGE = 7
 RAWS = 8
 VBUFS = 7
 QBUFS = 6
 YBUFS = 8
 HBUFS = 4
-V_PROD = 12
-COPY_STEPS = 4
+V_PROD = 6
+COPY_STEPS = 5
 ZBUFS = 5
 TURN_LAG = 3
-XS = 6
-X_LEAD = 4
-D3_FROM = 10
-S_GAIN = 2
+XS = 10
+X_LEAD = 8
+D3_FROM = 14
+S_GAIN = 4
 S_NORM = 0
 N_BATCHES = len(BATCHES)
 LN_FLOOR = 2.0 ** -60
@@ -315,12 +318,10 @@ def tile_autoencoder_pb_t_kernel(tc, h_dec1, D2, g4, b4, D3, bo, out):
 
         def second_matmul(r, flush):
             hw, hs = h_words[r // 2]
-            if flush:
-                wide = psum_u.tile([P, BANK], F32, tag="u", name="wide")
-                narrow = psum_u.tile([P, K_OUT - BANK], F32, tag="u", name="narrow")
-            else:
-                wide = psum_o.tile([P, BANK], F32, tag="bank", name="wide")
-                narrow = psum_o.tile([P, K_OUT - BANK], F32, tag="bank", name="narrow")
+            pool = {0: psum_o, 1: psum_u, 2: psum_u, 3: psum_turn}[flush]
+            tag = "u" if pool is psum_u else "bank"
+            wide = pool.tile([P, BANK], F32, tag=tag, name="wide")
+            narrow = pool.tile([P, K_OUT - BANK], F32, tag=tag, name="narrow")
             for acc, lo, hi in ((wide, 0, BANK), (narrow, BANK, K_OUT)):
                 for g in range(PASSES):
                     first = P * (PASSES * (r % 2) + g)
@@ -486,14 +487,12 @@ def tile_autoencoder_pb_t_kernel(tc, h_dec1, D2, g4, b4, D3, bo, out):
                 needs.append(("quanth", r // 2 - HBUFS))
             add("V" if r >= ROW_TILES - V_PROD and r % 2 else "G", ("prod", r), mish_product, r, needs=needs)
 
-        bias_added = [0]
-
         def bias(r):
             needs = [("mm2", r)]
             if r >= YBUFS:
                 needs.append(("outsig", r - YBUFS))
             add("V", ("bias", r), add_bias, r, needs=needs)
-            bias_added[0] = r + 1
+            bias_step[r] = state["step"]
 
         flushing = []
 
@@ -506,20 +505,26 @@ def tile_autoencoder_pb_t_kernel(tc, h_dec1, D2, g4, b4, D3, bo, out):
         def multiply(r):
             needs = [("quanth", r // 2)] + [("quant", key) for key in Z]
             if flushing:
-                needs += [("norm", ROW_TILES - 1)]
-                if len(flushing) > 2:
-                    needs.append(("bias", flushing[-3]))
+                needs += [("norm", ROW_TILES - 1), ("gain", PAIRS - 1, 1)]
+                if len(flushing) > FLUSH_DEPTH:
+                    needs.append(("bias", flushing[-1 - FLUSH_DEPTH]))
+                way = (len(flushing) - 1) % FLUSH_DEPTH + 1
+                if way == 4:
+                    way = 0
+                    if len(flushing) == 4 and r > 3:
+                        needs.append(("bias", r - 4))
             else:
+                way = 0
                 needs += take("o", ("bias", r))
                 needs += take("o", ("bias", r))
-            add("T", ("mm2", r), second_matmul, r, bool(flushing), needs=needs)
+            add("T", ("mm2", r), second_matmul, r, way, needs=needs)
 
         def back_calls(s):
             nonlocal_back = state["back"]
             calls = []
             t = nonlocal_back
             ready = t > 2 * PAIRS - 1 or 2 * (t // 2) + 2 <= state["prods"]
-            if t <= 2 * PAIRS and ready and s >= t + PROD_LAG + BACK_LAG:
+            if t <= 2 * PAIRS and ready and (s + 1 - PROD_LAG - BACK_LAG) * RATE > t:
                 if t >= 1:
                     calls.append((bias, t - 1))
                 if t < 2 * PAIRS:
@@ -529,13 +534,18 @@ def tile_autoencoder_pb_t_kernel(tc, h_dec1, D2, g4, b4, D3, bo, out):
                 state["back"] = t + 1
             return calls
 
-        state = {"back": 0, "prods": 0}
+        state = {"back": 0, "prods": 0, "step": 0}
+        bias_step = {}
         for s in range(TURN_LAG + ROW_TILES):
-            r = s - PROD_LAG
-            if 0 <= r < ROW_TILES:
+            due = min(ROW_TILES, max(0, int((s + 1 - PROD_LAG) * RATE)))
+            for r in range(state["prods"], due):
                 product_tick(r)
                 state["prods"] = r + 1
-            step(s, share=-(-len(rest) // COPY_STEPS), back=back_calls(s))
+            calls = back_calls(s)
+            if len(calls) and s not in when.values() and (s + 1 - PROD_LAG - BACK_LAG) * RATE > state["back"] + 1:
+                calls += back_calls(s)
+            step(s, share=-(-len(rest) // COPY_STEPS), back=calls)
+            state["step"] = s + 1
         first = state["back"]
         pending = [first - 1] if first >= 1 else []
         for t in range(first, 2 * PAIRS):
@@ -546,7 +556,7 @@ def tile_autoencoder_pb_t_kernel(tc, h_dec1, D2, g4, b4, D3, bo, out):
                 quanth(t // 2)
             flushing.append(t)
             multiply(t)
-            if len(pending) == 2:
+            if len(pending) == FLUSH_HOLD:
                 bias(pending.pop(0))
             pending.append(t)
         for t in pending:
@@ -558,9 +568,7 @@ def tile_autoencoder_pb_t_kernel(tc, h_dec1, D2, g4, b4, D3, bo, out):
                 add("S", ("tanh", n), tanh_pair, n)
             if i < N_BATCHES:
                 last_step = TURN_LAG + 2 * pairs(i).stop - 1
-                out_end = max(out_done, min(ROW_TILES, last_step - PROD_LAG - BACK_LAG - OUT_LESS))
-            elif i == N_BATCHES:
-                out_end = max(out_done, starts[i - 1] * 2 - LAST_OUT)
+                out_end = sum(1 for r in bias_step if bias_step[r] < last_step - OUT_LESS)
             else:
                 out_end = ROW_TILES
             outs = list(range(out_done, out_end))

@@ -30,20 +30,21 @@ D3_ON = "V"
 PROD_LAG = 15
 BACK_LAG = 6
 RATE = 1
-FLUSH_AHEAD = 5
+FLUSH_AHEAD = 2
 FLUSH_DEPTH = 4
 FLUSH_HOLD = 3
-LAST_OUT = 0
+LAST_OUT = 40
+TAIL_OUT = 3
 OUT_LESS = 0
-STAGE = 7
-RAWS = 8
+STAGE = 6
+RAWS = 6
 VBUFS = 7
 QBUFS = 6
-YBUFS = 8
+YBUFS = 11
 HBUFS = 4
 V_PROD = 6
 COPY_STEPS = 5
-ZBUFS = 5
+ZBUFS = 4
 TURN_LAG = 3
 XS = 10
 X_LEAD = 8
@@ -294,7 +295,7 @@ def tile_autoencoder_pb_t_kernel(tc, h_dec1, D2, g4, b4, D3, bo, out):
 
         def mish_product(r):
             n, a = r // 2, r % 2
-            if a == 0:
+            if n not in h_bf16:
                 hb = hpool.tile([P, 2, PASSES, P, PACK], BF16, align_bytes=64, name="hb")
                 h_bf16[n] = hb
             rows = slice(P * a, P * (a + 1))
@@ -548,9 +549,15 @@ def tile_autoencoder_pb_t_kernel(tc, h_dec1, D2, g4, b4, D3, bo, out):
             state["step"] = s + 1
         first = state["back"]
         pending = [first - 1] if first >= 1 else []
+        last_tile = 2 * starts[N_BATCHES - 1]
         for t in range(first, 2 * PAIRS):
+            if t == last_tile:
+                for r in pending:
+                    bias(r)
+                pending = []
             if t % 2 == 0:
-                for r in range(state["prods"], min(t + 2 + FLUSH_AHEAD, ROW_TILES)):
+                stop = last_tile if t < last_tile else ROW_TILES
+                for r in range(state["prods"], min(t + 2 + FLUSH_AHEAD, stop)):
                     product_tick(r)
                     state["prods"] = r + 1
                 quanth(t // 2)
@@ -564,11 +571,18 @@ def tile_autoencoder_pb_t_kernel(tc, h_dec1, D2, g4, b4, D3, bo, out):
         out_done = 0
         for i in range(N_BATCHES + 2):
             add("S", ("table", i), load_sigmoid_table)
+            if i == N_BATCHES:
+                for r in range(out_done, max(out_done, 2 * starts[i - 1] - LAST_OUT)):
+                    add("S", ("outsig", r), output_sigmoid, r, needs=[("bias", r)])
+                    out_done = r + 1
             for n in pairs(i - 1):
                 add("S", ("tanh", n), tanh_pair, n)
             if i < N_BATCHES:
                 last_step = TURN_LAG + 2 * pairs(i).stop - 1
                 out_end = sum(1 for r in bias_step if bias_step[r] < last_step - OUT_LESS)
+                if i == N_BATCHES - 1:
+                    out_end = max(out_end, 2 * starts[i - 1] - TAIL_OUT)
+                out_end = max(out_end, out_done)
             else:
                 out_end = ROW_TILES
             outs = list(range(out_done, out_end))

@@ -35,6 +35,7 @@ FLUSH_DEPTH = 4
 FLUSH_HOLD = 3
 LAST_OUT = 40
 TAIL_OUT = 3
+WARM_BANKS = (0,)
 OUT_LESS = 0
 STAGE = 6
 RAWS = 6
@@ -83,6 +84,8 @@ def tile_autoencoder_pb_t_kernel(tc, h_dec1, D2, g4, b4, D3, bo, out):
         nc.vector.memset(minus_half[:], -0.5)
         ln_floor = const.tile([P, 1], F32)
         nc.vector.memset(ln_floor[:], LN_FLOOR)
+        warm_rows = const.tile([P, PAIR], F32)
+        nc.vector.memset(warm_rows[:], 1.0)
         warm_in = const.tile([P, 1], F32)
         nc.vector.memset(warm_in[:], 0.0)
         warm_out = const.tile([P, 1], F32)
@@ -110,6 +113,14 @@ def tile_autoencoder_pb_t_kernel(tc, h_dec1, D2, g4, b4, D3, bo, out):
         def source(key):
             kind, n = key
             return (D2 if kind == "w" else h_dec1)[PAIR * n : PAIR * (n + 1), :]
+
+        def keep_warm(out):
+            nc.tensor.matmul(out=out, lhsT=ident_f32[:], rhs=warm_rows[:], start=True, stop=True)
+
+        def warm_up():
+            bank = psum_turn.tile([P, 2, PAIR], F32, tag="bank", name="warm")
+            for e in range(2):
+                keep_warm(bank[:, e, :])
 
         def load(key):
             kind, n = key
@@ -252,6 +263,8 @@ def tile_autoencoder_pb_t_kernel(tc, h_dec1, D2, g4, b4, D3, bo, out):
             banks = []
             for j in range(2):
                 bank = psum_turn.tile([P, 2, PAIR], F32, tag="bank", name="zt")
+                if j in WARM_BANKS:
+                    keep_warm(bank[:, 0, :])
                 for e in range(2):
                     c = PACK * g + 2 * j + e
                     for a in range(2):
@@ -389,7 +402,7 @@ def tile_autoencoder_pb_t_kernel(tc, h_dec1, D2, g4, b4, D3, bo, out):
                     nc.scalar.dma_start(out=gb_rows[CHUNKS : 2 * CHUNKS, :], in_=b4.rearrange("(c p) -> c p", p=P)),
                     nc.scalar.dma_start(out=bo_rows[:], in_=bo.partition_broadcast(P))))
 
-        allocs = {"h": [], "o": []}
+        allocs = {"h": [("warm",)], "o": []}
 
         def take(pool, reader):
             allocs[pool].append(reader)
@@ -408,6 +421,7 @@ def tile_autoencoder_pb_t_kernel(tc, h_dec1, D2, g4, b4, D3, bo, out):
         def add_quant(key):
             add("V", ("quant", key), quantise, key, needs=[("group", key)])
 
+        add("T", ("warm",), warm_up)
         for k in range(len(head)):
             add_turn(k)
         for k in range(len(head)):

@@ -364,7 +364,7 @@ def tile_autoencoder_pb_t_kernel(tc, h_dec1, D2, g4, b4, D3, bo, out):
             nc.sync.dma_start(out=out[P * r : P * (r + 1), :], in_=y[:])
 
         def turn_gain_and_bias():
-            bank = psum_o.tile([P, P], BF16, tag="bank", name="gb_turned")
+            bank = psum_turn.tile([P, P], BF16, tag="bank", name="gb_turned")
             nc.tensor.transpose(out=bank[:], in_=gb_rows[:], identity=ident_bf16[:])
             turned["gb"] = bank
 
@@ -396,11 +396,12 @@ def tile_autoencoder_pb_t_kernel(tc, h_dec1, D2, g4, b4, D3, bo, out):
 
         for k, key in enumerate(pieces):
             add("Q", ("load", key), load, key, needs=[("turn", pieces[k - RAWS])] if k >= RAWS else [])
-            if k == len(head):
+            if k == len(head) + 1:
                 add("Q", ("gbload",), lambda: (
-                    nc.scalar.dma_start(out=gb_rows[0:CHUNKS, :], in_=g4.rearrange("(c p) -> c p", p=P)),
-                    nc.scalar.dma_start(out=gb_rows[CHUNKS : 2 * CHUNKS, :], in_=b4.rearrange("(c p) -> c p", p=P)),
-                    nc.scalar.dma_start(out=bo_rows[:], in_=bo.partition_broadcast(P))))
+                    nc.sync.dma_start(out=gb_rows[0:CHUNKS, :], in_=g4.rearrange("(c p) -> c p", p=P)),
+                    nc.sync.dma_start(out=gb_rows[CHUNKS : 2 * CHUNKS, :], in_=b4.rearrange("(c p) -> c p", p=P))))
+            if k == len(head) + len(rest) - 1:
+                add("Q", ("boload",), lambda: nc.sync.dma_start(out=bo_rows[:], in_=bo.partition_broadcast(P)))
 
         allocs = {"h": [("warm",)], "o": []}
 
@@ -434,11 +435,13 @@ def tile_autoencoder_pb_t_kernel(tc, h_dec1, D2, g4, b4, D3, bo, out):
         add_quant(head[2])
         add_quant(head[3])
         add_quant(head[4])
+        add_turn(len(head))
+        add_group(len(head), "S")
         for r in range(2):
             add("T", ("mm1", r), first_matmul, r, needs=[("quant", key) for key in head])
-        add("T", ("gbturn",), turn_gain_and_bias, needs=[("gbload",)] + take("o", ("gb",)))
+        add("T", ("gbturn",), turn_gain_and_bias, needs=[("gbload",)] + take("h", ("gb",)))
 
-        turn_next = [len(head)]
+        turn_next = [len(head) + 1]
 
         def turn_pieces(count, stop=len(head) + len(rest)):
             for k in range(turn_next[0], min(turn_next[0] + count, stop)):
@@ -472,7 +475,7 @@ def tile_autoencoder_pb_t_kernel(tc, h_dec1, D2, g4, b4, D3, bo, out):
                 add("T", ("mm1", s + 1), first_matmul, s + 1, needs=needs)
             if 0 <= early_m < 2 * S_GAIN:
                 n, g = early_m // 2, early_m % 2
-                needs = [("norm", 2 * n + 1)] + ([("gain", (early_m - 1) // 2, (early_m - 1) % 2)] if early_m else [])
+                needs = [("norm", 2 * n + 1), ("gb",)] + ([("gain", (early_m - 1) // 2, (early_m - 1) % 2)] if early_m else [])
                 add("T", ("zt", n, g), turn_hidden, n, g, needs=needs)
                 add("S", ("gain", n, g), gain_and_bias, n, g, needs=[("zt", n, g)])
                 if g == 1 and n < starts[1]:
@@ -503,7 +506,7 @@ def tile_autoencoder_pb_t_kernel(tc, h_dec1, D2, g4, b4, D3, bo, out):
             add("V" if r >= ROW_TILES - V_PROD and r % 2 else "G", ("prod", r), mish_product, r, needs=needs)
 
         def bias(r):
-            needs = [("mm2", r)]
+            needs = [("mm2", r), ("boload",)]
             if r >= YBUFS:
                 needs.append(("outsig", r - YBUFS))
             add("V", ("bias", r), add_bias, r, needs=needs)

@@ -25,35 +25,32 @@ PAIRS = ROWS // PAIR
 D2_PIECES = HIDDEN // PAIR
 D3_TILES = K_OUT // P
 
-BATCHES = (4, 3, 3, 3, 3)
-D3_ON = "V"
-PROD_LAG = 15
-BACK_LAG = 6
-RATE = 1
-FLUSH_AHEAD = 2
-FLUSH_DEPTH = 4
-FLUSH_HOLD = 3
-LAST_OUT = 40
-TAIL_OUT = 3
-WARM_BANKS = (0,)
-OUT_LESS = 0
-STAGE = 6
-RAWS = 6
-VBUFS = 7
-QBUFS = 6
-YBUFS = 11
-HBUFS = 4
-V_PROD = 6
-COPY_STEPS = 5
-ZBUFS = 4
-TURN_LAG = 3
-XS = 10
-X_LEAD = 8
-D3_FROM = 14
-S_GAIN = 4
-S_NORM = 0
+FIRST_BATCH, BATCH = 4, 3
+BATCHES = (FIRST_BATCH,) + (BATCH,) * ((PAIRS - FIRST_BATCH) // BATCH)
 N_BATCHES = len(BATCHES)
-LN_FLOOR = 2.0 ** -60
+START = [sum(BATCHES[:i]) for i in range(N_BATCHES + 1)]
+
+V_BUFS = FIRST_BATCH + BATCH
+Q_BUFS = 2 * BATCH
+Z_BUFS = 4
+RAW_BUFS = 6
+EARLY_BUFS = 6
+LATE_BUFS = 2
+Y_BUFS = 11
+
+TURN_LAG = 3
+PRODUCT_LAG = 2 * V_BUFS + 1
+BACK_LAG = PRODUCT_LAG + D3_TILES
+H_BUFS = (BACK_LAG - PRODUCT_LAG) // 2 + 1
+
+COPIES_A_STEP = 2
+EARLY_PIECES = 2 + COPIES_A_STEP * FIRST_BATCH
+LATE_LEAD = 2 * FIRST_BATCH
+D3_STEP = PRODUCT_LAG - 1
+
+DUMMIES = BACK_LAG - TURN_LAG
+
+LN_FLOOR = 2.0**-60
 
 FLOPS = 2 * ROWS * K_IN * HIDDEN + 2 * ROWS * HIDDEN * K_OUT
 
@@ -62,18 +59,19 @@ def tile_autoencoder_pb_t_kernel(tc, h_dec1, D2, g4, b4, D3, bo, out):
     nc = tc.nc
     with ExitStack() as stack:
         const = stack.enter_context(tc.tile_pool(name="const", bufs=1))
-        raws = stack.enter_context(tc.tile_pool(name="raws", bufs=RAWS))
-        stage = stack.enter_context(tc.tile_pool(name="stage", bufs=STAGE))
+        raw_pool = stack.enter_context(tc.tile_pool(name="raw", bufs=RAW_BUFS))
+        early_pool = stack.enter_context(tc.tile_pool(name="early", bufs=EARLY_BUFS))
+        late_pool = stack.enter_context(tc.tile_pool(name="late", bufs=LATE_BUFS))
         small = stack.enter_context(tc.tile_pool(name="small", bufs=4))
-        zpool = stack.enter_context(tc.tile_pool(name="zpool", bufs=ZBUFS))
-        vpool = stack.enter_context(tc.tile_pool(name="vpool", bufs=VBUFS))
-        qpool = stack.enter_context(tc.tile_pool(name="qpool", bufs=QBUFS))
-        hpool = stack.enter_context(tc.tile_pool(name="hpool", bufs=HBUFS))
-        wpool = stack.enter_context(tc.tile_pool(name="wpool", bufs=2))
-        ypool = stack.enter_context(tc.tile_pool(name="ypool", bufs=YBUFS))
+        z_pool = stack.enter_context(tc.tile_pool(name="z", bufs=Z_BUFS))
+        v_pool = stack.enter_context(tc.tile_pool(name="v", bufs=V_BUFS))
+        q_pool = stack.enter_context(tc.tile_pool(name="q", bufs=Q_BUFS))
+        h_pool = stack.enter_context(tc.tile_pool(name="h", bufs=H_BUFS))
+        word_pool = stack.enter_context(tc.tile_pool(name="words", bufs=2))
+        y_pool = stack.enter_context(tc.tile_pool(name="y", bufs=Y_BUFS))
         psum_u = stack.enter_context(tc.psum_pool(name="psum_u", bufs=4))
         psum_turn = stack.enter_context(tc.psum_pool(name="psum_turn", bufs=2))
-        psum_o = stack.enter_context(tc.psum_pool(name="psum_o", bufs=2))
+        psum_out = stack.enter_context(tc.psum_pool(name="psum_out", bufs=2))
         stack.enter_context(tc.manual_schedule())
 
         ident_f32 = const.tile([P, P], F32)
@@ -84,131 +82,140 @@ def tile_autoencoder_pb_t_kernel(tc, h_dec1, D2, g4, b4, D3, bo, out):
         nc.vector.memset(minus_half[:], -0.5)
         ln_floor = const.tile([P, 1], F32)
         nc.vector.memset(ln_floor[:], LN_FLOOR)
-        warm_rows = const.tile([P, PAIR], F32)
-        nc.vector.memset(warm_rows[:], 1.0)
-        warm_in = const.tile([P, 1], F32)
-        nc.vector.memset(warm_in[:], 0.0)
-        warm_out = const.tile([P, 1], F32)
+        ones = const.tile([P, PAIR], F32)
+        nc.vector.memset(ones[:], 1.0)
+        table_in = const.tile([P, 1], F32)
+        nc.vector.memset(table_in[:], 0.0)
+        table_out = const.tile([P, 1], F32)
         gb_rows = const.tile([P, P], BF16)
         nc.vector.memset(gb_rows[:], 0.0)
-
-        def load_sigmoid_table():
-            nc.scalar.activation(out=warm_out[:], in_=warm_in[:], func=FUNC.Sigmoid)
-
-        load_sigmoid_table()
-
+        gain_bias = const.tile([P, 2 * CHUNKS], F32)
+        bo_rows = const.tile([P, K_OUT], BF16)
         x_words = const.tile([P, ROWS], U32, align_bytes=64)
         x_scales = const.tile([P, ROWS], U8, align_bytes=64)
         d2_words = const.tile([P, HIDDEN], U32, align_bytes=64)
         d2_scales = const.tile([P, HIDDEN], U8, align_bytes=64)
         d3_words = const.tile([P, PASSES, K_OUT], U32, align_bytes=64)
         d3_scales = const.tile([P, PASSES, K_OUT], U8, align_bytes=64)
-        bo_rows = const.tile([P, K_OUT], BF16)
-        gain_bias = const.tile([P, 2 * CHUNKS], F32)
+
+        def load_sigmoid_table():
+            nc.scalar.activation(out=table_out[:], in_=table_in[:], func=FUNC.Sigmoid)
+
+        load_sigmoid_table()
 
         raw = {}
         turned = {}
         grouped = {}
 
-        def source(key):
-            kind, n = key
-            return (D2 if kind == "w" else h_dec1)[PAIR * n : PAIR * (n + 1), :]
-
-        def keep_warm(out):
-            nc.tensor.matmul(out=out, lhsT=ident_f32[:], rhs=warm_rows[:], start=True, stop=True)
-
-        def warm_up():
-            bank = psum_turn.tile([P, 2, PAIR], F32, tag="bank", name="warm")
-            for e in range(2):
-                keep_warm(bank[:, e, :])
-
-        def load(key):
-            kind, n = key
-            tile = raws.tile([P, 2 * K_IN], BF16, name="raw")
+        def load(piece):
+            kind, n = piece
+            tile = raw_pool.tile([P, 2 * K_IN], BF16, name="raw")
             if kind == "d3":
                 nc.sync.dma_start(out=tile[:], in_=D3[P * n : P * (n + 1), :])
             else:
+                rows = slice(PAIR * n, PAIR * (n + 1))
+                source = h_dec1[rows, :] if kind == "x" else D2[rows, :]
                 nc.sync.dma_start(
                     out=tile[:].rearrange("p (a k) -> p a k", a=2),
-                    in_=source(key).rearrange("(a p) k -> p a k", p=P),
+                    in_=source.rearrange("(a p) k -> p a k", p=P),
                 )
-            raw[key] = tile
+            raw[piece] = tile
 
-        def turn(key, pool):
-            kind, n = key
+        def load_gain_and_bias():
+            for vector, first in ((g4, 0), (b4, CHUNKS)):
+                nc.sync.dma_start(out=gb_rows[first : first + CHUNKS, :], in_=vector.rearrange("(c p) -> c p", p=P))
+
+        def load_output_bias():
+            nc.sync.dma_start(out=bo_rows[:], in_=bo.partition_broadcast(P))
+
+        def turn(piece, pool):
+            kind, n = piece
             if kind == "d3":
                 bank = pool.tile([P, CHUNKS, P], BF16, tag="bank", name="turned3")
                 for c in range(CHUNKS):
-                    nc.tensor.transpose(out=bank[:, c, :], in_=raw[key][:, P * c : P * (c + 1)], identity=ident_bf16[:])
+                    nc.tensor.transpose(
+                        out=bank[:, c, :], in_=raw[piece][:, P * c : P * (c + 1)], identity=ident_bf16[:]
+                    )
             else:
-                words = raw[key][:].bitcast(F32)
+                twos = raw[piece][:].bitcast(F32)
                 bank = pool.tile([P, 2, PAIR], F32, tag="bank", name="turned")
                 for u in range(2):
                     for a in range(2):
                         first = (K_IN // 2) * a + P * u
                         nc.tensor.transpose(
                             out=bank[:, u, P * a : P * (a + 1)],
-                            in_=words[:, first : first + P],
+                            in_=twos[:, first : first + P],
                             identity=ident_f32[:],
                         )
-            turned[key] = bank
+            turned[piece] = bank
 
-        def group(key, engine):
-            kind, n = key
+        def group(piece, engine):
+            kind, n = piece
+            pool = early_pool if piece in early else late_pool
             if kind == "d3":
-                tile = stage.tile([P, PASSES, P, PACK], BF16, align_bytes=64, tag="grouped", name="grouped3")
-                o, i = tile[:], turned[key][:].rearrange("p (g t) r -> p g r t", t=PACK)
-                if engine == "V":
-                    nc.vector.tensor_copy(out=o, in_=i)
-                else:
-                    nc.scalar.copy(out=o, in_=i)
+                tile = pool.tile([P, PASSES, P, PACK], BF16, align_bytes=64, tag="grouped", name="grouped3")
+                to, source = tile[:], turned[piece][:].rearrange("p (g t) r -> p g r t", t=PACK)
             else:
-                tile = stage.tile([P, PAIR * PACK], BF16, align_bytes=64, tag="grouped", name="grouped")
-                o = tile[:].bitcast(F32).rearrange("p (r u) -> p r u", u=2)
-                i = turned[key][:].rearrange("p u r -> p r u")
-                if engine == "V":
-                    nc.vector.tensor_copy(out=o, in_=i)
-                else:
-                    nc.scalar.copy(out=o, in_=i)
-            grouped[key] = tile
+                tile = pool.tile([P, PAIR * PACK], BF16, align_bytes=64, tag="grouped", name="grouped")
+                to = tile[:].bitcast(F32).rearrange("p (r u) -> p r u", u=2)
+                source = turned[piece][:].rearrange("p u r -> p r u")
+            if engine == "scalar":
+                nc.scalar.copy(out=to, in_=source)
+            else:
+                nc.vector.tensor_copy(out=to, in_=source)
+            grouped[piece] = tile
 
-        def quantise(key):
-            kind, n = key
+        def quantise(piece):
+            kind, n = piece
             if kind == "d3":
                 cols = slice(P * n, P * (n + 1))
                 for g in range(PASSES):
                     nc.vector.quantize_mx(
                         out=d3_words[:, g, cols].bitcast(FP8X4),
                         scales=d3_scales[:, g, cols],
-                        in_=grouped[key][:, g].rearrange("p r t -> p (r t)"),
+                        in_=grouped[piece][:, g].rearrange("p r t -> p (r t)"),
                     )
             else:
                 cols = slice(PAIR * n, PAIR * (n + 1))
-                words, scales = (d2_words, d2_scales) if kind == "w" else (x_words, x_scales)
-                nc.vector.quantize_mx(out=words[:, cols].bitcast(FP8X4), scales=scales[:, cols], in_=grouped[key][:])
+                words, scales = (x_words, x_scales) if kind == "x" else (d2_words, d2_scales)
+                nc.vector.quantize_mx(out=words[:, cols].bitcast(FP8X4), scales=scales[:, cols], in_=grouped[piece][:])
+
+        def turn_gain_and_bias():
+            bank = psum_turn.tile([P, P], BF16, tag="bank", name="turned_gb")
+            nc.tensor.transpose(out=bank[:], in_=gb_rows[:], identity=ident_bf16[:])
+            turned["gb"] = bank
+
+        def keep_gain_and_bias():
+            nc.vector.tensor_copy(out=gain_bias[:], in_=turned["gb"][:, 0 : 2 * CHUNKS])
 
         u_banks = {}
         stats = {}
         mean_var = {}
         rstd = {}
-        shift = {}
         z_tiles = {}
-        zt_banks = {}
+        z_turned = {}
         v_tiles = {}
-        q_tiles = {}
 
-        def first_matmul(r):
-            cols = slice(P * r, P * (r + 1))
+        def dummy_product(columns):
+            nc.tensor.matmul(out=columns, lhsT=ident_f32[:], rhs=ones[:], start=True, stop=True)
+
+        def warm_up():
+            bank = psum_turn.tile([P, 2, PAIR], F32, tag="bank", name="warm")
+            for e in range(2):
+                dummy_product(bank[:, e, :])
+
+        def first_product(r):
+            rows = slice(P * r, P * (r + 1))
             banks = []
             for half in range(HIDDEN // BANK):
-                hid = slice(BANK * half, BANK * (half + 1))
+                hidden = slice(BANK * half, BANK * (half + 1))
                 u = psum_u.tile([P, BANK], F32, tag="u", name="u")
                 nc.tensor.matmul_mx(
                     out=u[:],
-                    lhsT=x_words[:, cols].bitcast(FP8X4),
-                    lhsT_scale=x_scales[:, cols],
-                    rhs=d2_words[:, hid].bitcast(FP8X4),
-                    rhs_scale=d2_scales[:, hid],
+                    lhsT=x_words[:, rows].bitcast(FP8X4),
+                    lhsT_scale=x_scales[:, rows],
+                    rhs=d2_words[:, hidden].bitcast(FP8X4),
+                    rhs_scale=d2_scales[:, hidden],
                     start=True,
                     stop=True,
                 )
@@ -232,39 +239,26 @@ def tile_autoencoder_pb_t_kernel(tc, h_dec1, D2, g4, b4, D3, bo, out):
             tile = small.tile([P, 1], F32, name="rstd")
             nc.gpsimd.tensor_tensor(out=tile[:], in0=var_eps[:], in1=minus_half[:], op=ALU.pow)
             rstd[r] = tile
-            if on_scalar(r):
-                product = small.tile([P, 1], F32, name="product")
-                nc.gpsimd.tensor_tensor(out=product[:], in0=mean_var[r][:, 0:1], in1=tile[:], op=ALU.mult)
-                minus = small.tile([P, 1], F32, name="minus")
-                nc.gpsimd.tensor_scalar(out=minus[:], in0=product[:], scalar1=-1.0, scalar2=0.0, op0=ALU.mult, op1=ALU.add)
-                shift[r] = minus
-
-        def on_scalar(r):
-            return r % 2 == 1 and r < 2 * S_NORM
 
         def normalise(r):
-            z = zpool.tile([P, HIDDEN], F32, name="z")
+            z = z_pool.tile([P, HIDDEN], F32, name="z")
             for half in range(2):
-                cols = slice(BANK * half, BANK * (half + 1))
-                if on_scalar(r):
-                    nc.scalar.activation(
-                        out=z[:, cols], in_=u_banks[r][half][:], func=FUNC.Identity,
-                        scale=rstd[r][:], bias=shift[r][:],
-                    )
-                else:
-                    nc.vector.tensor_scalar(
-                        out=z[:, cols], in0=u_banks[r][half][:],
-                        scalar1=mean_var[r][:, 0:1], scalar2=rstd[r][:],
-                        op0=ALU.subtract, op1=ALU.mult,
-                    )
+                nc.vector.tensor_scalar(
+                    out=z[:, BANK * half : BANK * (half + 1)],
+                    in0=u_banks[r][half][:],
+                    scalar1=mean_var[r][:, 0:1],
+                    scalar2=rstd[r][:],
+                    op0=ALU.subtract,
+                    op1=ALU.mult,
+                )
             z_tiles[r] = z
 
         def turn_hidden(n, g):
             banks = []
             for j in range(2):
                 bank = psum_turn.tile([P, 2, PAIR], F32, tag="bank", name="zt")
-                if j in WARM_BANKS:
-                    keep_warm(bank[:, 0, :])
+                if j == 0 and 2 * n + g < DUMMIES:
+                    dummy_product(bank[:, 0, :])
                 for e in range(2):
                     c = PACK * g + 2 * j + e
                     for a in range(2):
@@ -274,86 +268,91 @@ def tile_autoencoder_pb_t_kernel(tc, h_dec1, D2, g4, b4, D3, bo, out):
                             identity=ident_f32[:],
                         )
                 banks.append(bank)
-            zt_banks[(n, g)] = banks
+            z_turned[(n, g)] = banks
 
         def gain_and_bias(n, g):
             if g == 0:
-                v = vpool.tile([P, CHUNKS, PAIR], F32, name="v")
+                v = v_pool.tile([P, CHUNKS, PAIR], F32, name="v")
                 v_tiles[n] = v
             for j in range(2):
                 for e in range(2):
                     c = PACK * g + 2 * j + e
                     gain, bias = gain_bias[:, c : c + 1], gain_bias[:, CHUNKS + c : CHUNKS + c + 1]
-                    o, i = v_tiles[n][:, c, :], zt_banks[(n, g)][j][:, e, :]
-                    if n < S_GAIN:
-                        nc.scalar.activation(out=o, in_=i, func=FUNC.Identity, scale=gain, bias=bias)
+                    to, source = v_tiles[n][:, c, :], z_turned[(n, g)][j][:, e, :]
+                    if n < FIRST_BATCH:
+                        nc.scalar.activation(out=to, in_=source, func=FUNC.Identity, scale=gain, bias=bias)
                     else:
-                        nc.vector.tensor_scalar(out=o, in0=i, scalar1=gain, scalar2=bias, op0=ALU.mult, op1=ALU.add)
+                        nc.vector.tensor_scalar(
+                            out=to, in0=source, scalar1=gain, scalar2=bias, op0=ALU.mult, op1=ALU.add
+                        )
 
-        def sigmoid_pair(n):
-            q = qpool.tile([P, CHUNKS, PAIR], F32, name="q")
+        q_tiles = {}
+        h_tiles = {}
+
+        def sigmoid_of_minus(n):
+            q = q_pool.tile([P, CHUNKS, PAIR], F32, name="q")
             nc.scalar.activation(out=q[:], in_=v_tiles[n][:], func=FUNC.Sigmoid, scale=-1.0)
             q_tiles[n] = q
 
-        def log_pair(n):
+        def logarithm(n):
             nc.scalar.activation(out=q_tiles[n][:], in_=q_tiles[n][:], func=FUNC.Ln, bias=ln_floor[:])
 
-        def tanh_pair(n):
+        def tanh_of_minus(n):
             nc.scalar.activation(out=q_tiles[n][:], in_=q_tiles[n][:], func=FUNC.Tanh, scale=-1.0)
 
-        h_bf16 = {}
-        h_words = {}
-        o_banks = {}
-        y_tiles = {}
+        def product_on_vector(r):
+            return r >= 2 * START[N_BATCHES - 1] and r % 2 == 1
 
         def mish_product(r):
             n, a = r // 2, r % 2
-            if n not in h_bf16:
-                hb = hpool.tile([P, 2, PASSES, P, PACK], BF16, align_bytes=64, name="hb")
-                h_bf16[n] = hb
+            if n not in h_tiles:
+                h = h_pool.tile([P, 2, PASSES, P, PACK], BF16, align_bytes=64, name="h")
+                h_tiles[n] = h
             rows = slice(P * a, P * (a + 1))
+            engine = nc.vector if product_on_vector(r) else nc.gpsimd
             for g in range(PASSES):
                 chunks = slice(PACK * g, PACK * (g + 1))
-                engine = nc.vector if r >= ROW_TILES - V_PROD and r % 2 else nc.gpsimd
                 engine.tensor_tensor(
-                    out=h_bf16[n][:, a, g].rearrange("p (c i) t -> p c t i", i=4),
+                    out=h_tiles[n][:, a, g].rearrange("p (c i) t -> p c t i", i=4),
                     in0=v_tiles[n][:, chunks, rows].rearrange("p t (c i) -> p c t i", i=4),
                     in1=q_tiles[n][:, chunks, rows].rearrange("p t (c i) -> p c t i", i=4),
                     op=ALU.mult,
                 )
 
-        def quantise_hidden(n):
-            hw = wpool.tile([P, 2 * PASSES * P], U32, align_bytes=64, name="hw")
-            hs = wpool.tile([P, 2 * PASSES * P], U8, align_bytes=64, name="hs")
-            nc.vector.quantize_mx(
-                out=hw[:].bitcast(FP8X4), scales=hs[:], in_=h_bf16[n][:].rearrange("p a g r t -> p (a g r t)"),
-            )
-            h_words[n] = (hw, hs)
+        h_operands = {}
+        out_banks = {}
+        y_tiles = {}
 
-        def second_matmul(r, flush):
-            hw, hs = h_words[r // 2]
-            pool = {0: psum_o, 1: psum_u, 2: psum_u, 3: psum_turn}[flush]
-            tag = "u" if pool is psum_u else "bank"
+        def quantise_hidden(n):
+            words = word_pool.tile([P, 2 * PASSES * P], U32, align_bytes=64, name="h_words")
+            scales = word_pool.tile([P, 2 * PASSES * P], U8, align_bytes=64, name="h_scales")
+            nc.vector.quantize_mx(
+                out=words[:].bitcast(FP8X4), scales=scales[:], in_=h_tiles[n][:].rearrange("p a g r t -> p (a g r t)")
+            )
+            h_operands[n] = (words, scales)
+
+        def second_product(r, pool, tag):
+            words, scales = h_operands[r // 2]
             wide = pool.tile([P, BANK], F32, tag=tag, name="wide")
             narrow = pool.tile([P, K_OUT - BANK], F32, tag=tag, name="narrow")
-            for acc, lo, hi in ((wide, 0, BANK), (narrow, BANK, K_OUT)):
+            for bank, lo, hi in ((wide, 0, BANK), (narrow, BANK, K_OUT)):
                 for g in range(PASSES):
                     first = P * (PASSES * (r % 2) + g)
-                    cols = slice(first, first + P)
+                    rows = slice(first, first + P)
                     nc.tensor.matmul_mx(
-                        out=acc[:],
-                        lhsT=hw[:, cols].bitcast(FP8X4),
-                        lhsT_scale=hs[:, cols],
+                        out=bank[:],
+                        lhsT=words[:, rows].bitcast(FP8X4),
+                        lhsT_scale=scales[:, rows],
                         rhs=d3_words[:, g, lo:hi].bitcast(FP8X4),
                         rhs_scale=d3_scales[:, g, lo:hi],
                         start=(g == 0),
                         stop=(g == PASSES - 1),
                     )
-            o_banks[r] = (wide, narrow)
+            out_banks[r] = (wide, narrow)
 
-        def add_bias(r):
-            wide, narrow = o_banks[r]
-            y = ypool.tile([P, K_OUT], F32, name="y")
+        def add_output_bias(r):
+            wide, narrow = out_banks[r]
+            y = y_pool.tile([P, K_OUT], F32, name="y")
             nc.vector.tensor_tensor(out=y[:, 0:BANK], in0=wide[:], in1=bo_rows[:, 0:BANK], op=ALU.add)
             nc.vector.tensor_tensor(out=y[:, BANK:K_OUT], in0=narrow[:], in1=bo_rows[:, BANK:K_OUT], op=ALU.add)
             y_tiles[r] = y
@@ -363,274 +362,217 @@ def tile_autoencoder_pb_t_kernel(tc, h_dec1, D2, g4, b4, D3, bo, out):
             nc.scalar.activation(out=y[:], in_=y[:], func=FUNC.Sigmoid)
             nc.sync.dma_start(out=out[P * r : P * (r + 1), :], in_=y[:])
 
-        def turn_gain_and_bias():
-            bank = psum_turn.tile([P, P], BF16, tag="bank", name="gb_turned")
-            nc.tensor.transpose(out=bank[:], in_=gb_rows[:], identity=ident_bf16[:])
-            turned["gb"] = bank
+        lists = {"sync": [], "tensor": [], "scalar": [], "vector": [], "gpsimd": []}
 
-        def keep_gain_and_bias():
-            nc.vector.tensor_copy(out=gain_bias[:], in_=turned["gb"][:, 0 : 2 * CHUNKS])
+        def add(engine, name, call, *arguments, after=()):
+            lists[engine].append((name, call, arguments, tuple(after)))
 
-        streams = {"Q": [], "T": [], "S": [], "V": [], "G": []}
-        done = set()
-        starts = [sum(BATCHES[:n]) for n in range(N_BATCHES + 1)]
+        bank_readers = {"turn": [], "out": []}
 
-        def add(engine, key, fn, *args, needs=()):
-            streams[engine].append((key, fn, args, tuple(needs)))
+        def bank_free(pool, reader):
+            bank_readers[pool].append(reader)
+            return bank_readers[pool][-3:-2]
 
-        def pairs(batch):
-            if 0 <= batch < N_BATCHES:
-                return range(starts[batch], starts[batch + 1])
-            return range(0)
+        x_pieces = [("x", n) for n in range(PAIRS)]
+        d2_pieces = [("d2", n) for n in range(D2_PIECES)]
+        d3_pieces = [("d3", n) for n in range(D3_TILES)]
+        head = x_pieces[:1] + d2_pieces
+        early = head + x_pieces[1:EARLY_PIECES]
+        late_step = {("x", n): 2 * n - LATE_LEAD for n in range(EARLY_PIECES, PAIRS)}
+        late_step.update({("d3", n): D3_STEP + n for n in range(D3_TILES)})
+        late = [piece for s in range(ROW_TILES) for piece in x_pieces + d3_pieces if late_step.get(piece) == s]
+        pieces = early + late
 
-        W = [("w", n) for n in range(D2_PIECES)]
-        X = [("x", n) for n in range(PAIRS)]
-        Z = [("d3", n) for n in range(D3_TILES)]
-        head = [X[0], W[0], W[1], W[2], W[3]]
-        rest = X[1:XS]
-        early = set(rest)
-        pieces = head + rest
-        later = sorted([(max(2 * n - X_LEAD, 0), 0, key) for n, key in enumerate(X) if n >= XS] + [(D3_FROM + j, 1, key) for j, key in enumerate(Z)])
-        when = {len(pieces) + j: cyc for j, (cyc, kind, key) in enumerate(later)}
-        pieces += [key for cyc, kind, key in later]
+        def add_turn(piece):
+            k = pieces.index(piece)
+            if k < len(head) and k % 2 == 1:
+                free = bank_free("turn", ("group", piece))
+                add("tensor", ("turn", piece), turn, piece, psum_turn, after=[("load", piece)] + free)
+            else:
+                free = bank_free("out", ("group", piece))
+                add("tensor", ("turn", piece), turn, piece, psum_out, after=[("load", piece)] + free)
 
-        for k, key in enumerate(pieces):
-            add("Q", ("load", key), load, key, needs=[("turn", pieces[k - RAWS])] if k >= RAWS else [])
-            if k == len(head) + 1:
-                add("Q", ("gbload",), lambda: (
-                    nc.sync.dma_start(out=gb_rows[0:CHUNKS, :], in_=g4.rearrange("(c p) -> c p", p=P)),
-                    nc.sync.dma_start(out=gb_rows[CHUNKS : 2 * CHUNKS, :], in_=b4.rearrange("(c p) -> c p", p=P))))
-            if k == len(head) + len(rest) - 1:
-                add("Q", ("boload",), lambda: nc.sync.dma_start(out=bo_rows[:], in_=bo.partition_broadcast(P)))
+        def add_group(piece, engine):
+            line, bufs = (early, EARLY_BUFS) if piece in early else (late, LATE_BUFS)
+            k = line.index(piece)
+            free = [("quantise", line[k - bufs])] if k >= bufs else []
+            add(engine, ("group", piece), group, piece, engine, after=[("turn", piece)] + free)
 
-        allocs = {"h": [("warm",)], "o": []}
+        def add_quantise(piece):
+            add("vector", ("quantise", piece), quantise, piece, after=[("group", piece)])
 
-        def take(pool, reader):
-            allocs[pool].append(reader)
-            return allocs[pool][-3:-2]
+        for k, piece in enumerate(pieces):
+            free = [("turn", pieces[k - RAW_BUFS])] if k >= RAW_BUFS else []
+            add("sync", ("load", piece), load, piece, after=free)
+            if piece == x_pieces[2]:
+                add("sync", ("load", "gb"), load_gain_and_bias)
+            if piece == early[-1]:
+                add("sync", ("load", "bo"), load_output_bias)
 
-        def add_turn(k):
-            key = pieces[k]
-            name, pool = ("h", psum_turn) if k < len(head) and k % 2 else ("o", psum_o)
-            add("T", ("turn", key), turn, key, pool, needs=[("load", key)] + take(name, ("group", key)))
-
-        def add_group(k, engine):
-            key = pieces[k]
-            needs = [("turn", key)] + ([("quant", pieces[k - STAGE])] if k >= STAGE else [])
-            add(engine, ("group", key), group, key, engine, needs=needs)
-
-        def add_quant(key):
-            add("V", ("quant", key), quantise, key, needs=[("group", key)])
-
-        add("T", ("warm",), warm_up)
-        for k in range(len(head)):
-            add_turn(k)
-        for k in range(len(head)):
-            if k % 2 == 0:
-                add_group(k, "S")
-        add_group(1, "V")
-        add_quant(head[0])
-        add_quant(head[1])
-        add_group(3, "V")
-        add_quant(head[2])
-        add_quant(head[3])
-        add_quant(head[4])
-        add_turn(len(head))
-        add_group(len(head), "S")
+        add("tensor", ("warm up",), warm_up)
+        bank_readers["turn"].append(("warm up",))
+        for piece in head:
+            add_turn(piece)
+        for k in range(0, len(head), 2):
+            add_group(head[k], "scalar")
+        add_group(head[1], "vector")
+        add_quantise(head[0])
+        add_quantise(head[1])
+        add_group(head[3], "vector")
+        for piece in head[2:]:
+            add_quantise(piece)
+        add_turn(x_pieces[1])
+        add_group(x_pieces[1], "scalar")
         for r in range(2):
-            add("T", ("mm1", r), first_matmul, r, needs=[("quant", key) for key in head])
-        add("T", ("gbturn",), turn_gain_and_bias, needs=[("gbload",)] + take("h", ("gb",)))
+            add("tensor", ("first", r), first_product, r, after=[("quantise", piece) for piece in head])
+        free = bank_free("turn", ("keep", "gb"))
+        add("tensor", ("turn", "gb"), turn_gain_and_bias, after=[("load", "gb")] + free)
 
-        turn_next = [len(head) + 1]
+        def add_turn_hidden(half):
+            n, g = half // 2, half % 2
+            free = [("gain", half - 1)] if half else [("keep", "gb")]
+            add("tensor", ("turn z", half), turn_hidden, n, g, after=[("normalise", 2 * n + 1)] + free)
 
-        def turn_pieces(count, stop=len(head) + len(rest)):
-            for k in range(turn_next[0], min(turn_next[0] + count, stop)):
-                add_turn(k)
-                add_group(k, "S")
-            turn_next[0] = max(turn_next[0], min(turn_next[0] + count, stop))
+        def add_gain_and_bias(half, engine):
+            n, g = half // 2, half % 2
+            free = [("product", 2 * (n - V_BUFS) + 1)] if n >= V_BUFS else []
+            add(engine, ("gain", half), gain_and_bias, n, g, after=[("turn z", half)] + free)
 
-        def step(s, share=0, back=()):
-            m = s - TURN_LAG
-            n, g = m // 2, m % 2
-            early_m = s - 2
-            late = [k for k in range(len(pieces)) if when.get(k) == s]
-            if 2 * S_GAIN <= m < ROW_TILES:
-                needs = [("norm", 2 * n + 1)] + ([("gain", (m - 1) // 2, (m - 1) % 2)] if m else [])
-                add("T", ("zt", n, g), turn_hidden, n, g, needs=needs)
+        def add_sigmoid(n):
+            free = [("product", 2 * (n - Q_BUFS) + 1)] if n >= Q_BUFS else []
+            add("scalar", ("sigmoid", n), sigmoid_of_minus, n, after=[("gain", 2 * n + 1)] + free)
+
+        def add_product(r):
+            n = r // 2
+            free = [("quantise h", n - H_BUFS)] if n >= H_BUFS else []
+            engine = "vector" if product_on_vector(r) else "gpsimd"
+            add(engine, ("product", r), mish_product, r, after=[("tanh", n)] + free)
+
+        def add_quantise_hidden(n):
+            free = [("second", 2 * n - 3)] if n >= 2 else []
+            add("vector", ("quantise h", n), quantise_hidden, n, after=[("product", 2 * n + 1)] + free)
+
+        def add_second_product(r, pool, tag, free):
+            needs = [("quantise h", r // 2)] + [("quantise", piece) for piece in d3_pieces]
+            add("tensor", ("second", r), second_product, r, pool, tag, after=needs + free)
+
+        def add_bias(r):
+            free = [("output", r - Y_BUFS)] if r >= Y_BUFS else []
+            add("vector", ("bias", r), add_output_bias, r, after=[("second", r), ("load", "bo")] + free)
+
+        for s in range(ROW_TILES + TURN_LAG):
+            if 0 <= s - PRODUCT_LAG < ROW_TILES:
+                add_product(s - PRODUCT_LAG)
+            half = s - TURN_LAG
+            by_vector = 2 * FIRST_BATCH <= half
+            if by_vector:
+                add_turn_hidden(half)
             if s < ROW_TILES:
-                add("V", ("stats", s), bank_statistics, s, needs=[("mm1", s)])
-            if 0 <= s - 1 < ROW_TILES:
-                r = s - 1
-                needs = [("rstd", r)]
-                if r >= ZBUFS:
-                    needs.append(("zt", (r - ZBUFS) // 2, 1))
-                add("S" if on_scalar(r) else "V", ("norm", r), normalise, r, needs=needs)
+                add("vector", ("statistics", s), bank_statistics, s, after=[("first", s)])
+            if 1 <= s <= ROW_TILES:
+                free = [("turn z", s - 1 - Z_BUFS + (s % 2))] if s > Z_BUFS else []
+                add("vector", ("normalise", s - 1), normalise, s - 1, after=[("deviation", s - 1)] + free)
             if s < ROW_TILES:
-                add("V", ("moments", s), row_moments, s)
-                add("G", ("rstd", s), reciprocal_deviation, s, needs=[("moments", s)])
+                add("vector", ("moments", s), row_moments, s)
+                add("gpsimd", ("deviation", s), reciprocal_deviation, s, after=[("moments", s)])
             if s == 1:
-                add("V", ("gb",), keep_gain_and_bias, needs=[("gbturn",)])
-            if 1 < s + 1 < ROW_TILES:
-                needs = [("quant", X[(s + 1) // 2])] + ([("norm", s - 1)] if s else [])
-                add("T", ("mm1", s + 1), first_matmul, s + 1, needs=needs)
-            if 0 <= early_m < 2 * S_GAIN:
-                n, g = early_m // 2, early_m % 2
-                needs = [("norm", 2 * n + 1), ("gb",)] + ([("gain", (early_m - 1) // 2, (early_m - 1) % 2)] if early_m else [])
-                add("T", ("zt", n, g), turn_hidden, n, g, needs=needs)
-                add("S", ("gain", n, g), gain_and_bias, n, g, needs=[("zt", n, g)])
-                if g == 1 and n < starts[1]:
-                    add("S", ("sig", n), sigmoid_pair, n)
-                n, g = m // 2, m % 2
-            for k in late:
-                add_turn(k)
-            for f, arg in back:
-                f(arg)
-            turn_pieces(share)
-            if 2 * S_GAIN <= m < ROW_TILES:
-                needs = [("zt", n, g)]
-                if n >= VBUFS:
-                    needs.append(("prod", 2 * (n - VBUFS) + 1))
-                add("V", ("gain", n, g), gain_and_bias, n, g, needs=needs)
-            if s % 2 == 0 and 1 <= (s + 2) // 2 < XS:
-                add_quant(X[(s + 2) // 2])
-            for k in range(len(pieces)):
-                if when.get(k) == s - 1:
-                    add_quant(pieces[k])
-            for k in late:
-                add_group(k, D3_ON if pieces[k][0] == "d3" else "V")
+                add("vector", ("keep", "gb"), keep_gain_and_bias, after=[("turn", "gb")])
+            if 1 <= s < ROW_TILES - 1:
+                needs = [("quantise", x_pieces[(s + 1) // 2]), ("normalise", s - 1)]
+                add("tensor", ("first", s + 1), first_product, s + 1, after=needs)
+            if 0 <= half + 1 < 2 * FIRST_BATCH:
+                add_turn_hidden(half + 1)
+                add_gain_and_bias(half + 1, "scalar")
+                if (half + 1) % 2 == 1:
+                    add_sigmoid((half + 1) // 2)
+            now = [piece for piece in late if late_step[piece] == s]
+            for piece in now:
+                add_turn(piece)
+            r = s - BACK_LAG
+            if r >= 0:
+                if r >= 1:
+                    add_bias(r - 1)
+                if r % 2 == 0:
+                    add_quantise_hidden(r // 2)
+                free = bank_free("out", ("bias", r)) + bank_free("out", ("bias", r))
+                add_second_product(r, psum_out, "bank", free)
+            first = 2 + COPIES_A_STEP * s
+            for piece in x_pieces[first : min(first + COPIES_A_STEP, EARLY_PIECES)]:
+                add_turn(piece)
+                add_group(piece, "scalar")
+            if by_vector:
+                add_gain_and_bias(half, "vector")
+            if s % 2 == 0 and (s + 2) // 2 < EARLY_PIECES:
+                add_quantise(x_pieces[(s + 2) // 2])
+            for piece in late:
+                if late_step[piece] == s - 1:
+                    add_quantise(piece)
+            for piece in now:
+                add_group(piece, "vector")
 
-        def product_tick(r):
-            needs = [("tanh", r // 2)]
-            if r // 2 >= HBUFS:
-                needs.append(("quanth", r // 2 - HBUFS))
-            add("V" if r >= ROW_TILES - V_PROD and r % 2 else "G", ("prod", r), mish_product, r, needs=needs)
+        places = ((psum_u, "u"), (psum_u, "u"), (psum_turn, "bank"), (psum_out, "bank"))
+        rest = ROW_TILES + TURN_LAG - BACK_LAG
+        last = 2 * START[N_BATCHES - 1]
+        products = ROW_TILES + TURN_LAG - PRODUCT_LAG
+        held = [rest - 1]
+        for r in range(rest, ROW_TILES):
+            if r == last:
+                for earlier in held:
+                    add_bias(earlier)
+                held = []
+            if r % 2 == 0:
+                stop = min(r + 4, last if r < last else ROW_TILES)
+                for product in range(products, stop):
+                    add_product(product)
+                products = max(products, stop)
+                add_quantise_hidden(r // 2)
+            pool, tag = places[(r - rest) % 4]
+            needs = [("normalise", ROW_TILES - 1), ("gain", 2 * PAIRS - 1)]
+            free = [("bias", r - 4)] if r - rest >= 3 else []
+            add_second_product(r, pool, tag, needs + free)
+            if len(held) == 3:
+                add_bias(held.pop(0))
+            held.append(r)
+        for r in held:
+            add_bias(r)
 
-        def bias(r):
-            needs = [("mm2", r), ("boload",)]
-            if r >= YBUFS:
-                needs.append(("outsig", r - YBUFS))
-            add("V", ("bias", r), add_bias, r, needs=needs)
-            bias_step[r] = state["step"]
-
-        flushing = []
-
-        def quanth(n):
-            needs = [("prod", 2 * n + 1)]
-            if n >= 2:
-                needs.append(("mm2", 2 * (n - 2) + 1))
-            add("V", ("quanth", n), quantise_hidden, n, needs=needs)
-
-        def multiply(r):
-            needs = [("quanth", r // 2)] + [("quant", key) for key in Z]
-            if flushing:
-                needs += [("norm", ROW_TILES - 1), ("gain", PAIRS - 1, 1)]
-                if len(flushing) > FLUSH_DEPTH:
-                    needs.append(("bias", flushing[-1 - FLUSH_DEPTH]))
-                way = (len(flushing) - 1) % FLUSH_DEPTH + 1
-                if way == 4:
-                    way = 0
-                    if len(flushing) == 4 and r > 3:
-                        needs.append(("bias", r - 4))
-            else:
-                way = 0
-                needs += take("o", ("bias", r))
-                needs += take("o", ("bias", r))
-            add("T", ("mm2", r), second_matmul, r, way, needs=needs)
-
-        def back_calls(s):
-            nonlocal_back = state["back"]
-            calls = []
-            t = nonlocal_back
-            ready = t > 2 * PAIRS - 1 or 2 * (t // 2) + 2 <= state["prods"]
-            if t <= 2 * PAIRS and ready and (s + 1 - PROD_LAG - BACK_LAG) * RATE > t:
-                if t >= 1:
-                    calls.append((bias, t - 1))
-                if t < 2 * PAIRS:
-                    if t % 2 == 0:
-                        calls.append((quanth, t // 2))
-                    calls.append((multiply, t))
-                state["back"] = t + 1
-            return calls
-
-        state = {"back": 0, "prods": 0, "step": 0}
-        bias_step = {}
-        for s in range(TURN_LAG + ROW_TILES):
-            due = min(ROW_TILES, max(0, int((s + 1 - PROD_LAG) * RATE)))
-            for r in range(state["prods"], due):
-                product_tick(r)
-                state["prods"] = r + 1
-            calls = back_calls(s)
-            if len(calls) and s not in when.values() and (s + 1 - PROD_LAG - BACK_LAG) * RATE > state["back"] + 1:
-                calls += back_calls(s)
-            step(s, share=-(-len(rest) // COPY_STEPS), back=calls)
-            state["step"] = s + 1
-        first = state["back"]
-        pending = [first - 1] if first >= 1 else []
-        last_tile = 2 * starts[N_BATCHES - 1]
-        for t in range(first, 2 * PAIRS):
-            if t == last_tile:
-                for r in pending:
-                    bias(r)
-                pending = []
-            if t % 2 == 0:
-                stop = last_tile if t < last_tile else ROW_TILES
-                for r in range(state["prods"], min(t + 2 + FLUSH_AHEAD, stop)):
-                    product_tick(r)
-                    state["prods"] = r + 1
-                quanth(t // 2)
-            flushing.append(t)
-            multiply(t)
-            if len(pending) == FLUSH_HOLD:
-                bias(pending.pop(0))
-            pending.append(t)
-        for t in pending:
-            bias(t)
-        out_done = 0
+        outputs = 0
         for i in range(N_BATCHES + 2):
-            add("S", ("table", i), load_sigmoid_table)
-            if i == N_BATCHES:
-                for r in range(out_done, max(out_done, 2 * starts[i - 1] - LAST_OUT)):
-                    add("S", ("outsig", r), output_sigmoid, r, needs=[("bias", r)])
-                    out_done = r + 1
-            for n in pairs(i - 1):
-                add("S", ("tanh", n), tanh_pair, n)
+            add("scalar", ("table", i), load_sigmoid_table)
+            if 1 <= i <= N_BATCHES:
+                for n in range(START[i - 1], START[i]):
+                    add("scalar", ("tanh", n), tanh_of_minus, n)
+            due = ROW_TILES
             if i < N_BATCHES:
-                last_step = TURN_LAG + 2 * pairs(i).stop - 1
-                out_end = sum(1 for r in bias_step if bias_step[r] < last_step - OUT_LESS)
+                last_step = 2 * START[i + 1] - 1 + TURN_LAG
+                due = max(0, last_step - BACK_LAG - 1)
                 if i == N_BATCHES - 1:
-                    out_end = max(out_end, 2 * starts[i - 1] - TAIL_OUT)
-                out_end = max(out_end, out_done)
-            else:
-                out_end = ROW_TILES
-            outs = list(range(out_done, out_end))
-            out_done = out_end
-            for n in pairs(i):
-                if n == pairs(i).stop - 1:
-                    for r in outs:
-                        add("S", ("outsig", r), output_sigmoid, r, needs=[("bias", r)])
-                    outs = []
-                needs = [("gain", n, 1)]
-                if n >= QBUFS:
-                    needs.append(("prod", 2 * (n - QBUFS) + 1))
-                if n >= min(S_GAIN, starts[1]):
-                    add("S", ("sig", n), sigmoid_pair, n, needs=needs)
-            for r in outs:
-                add("S", ("outsig", r), output_sigmoid, r, needs=[("bias", r)])
-            for n in pairs(i):
-                add("S", ("ln", n), log_pair, n)
+                    due = rest + 2
+            batch = list(range(START[i], START[i + 1])) if i < N_BATCHES else []
+            if i > 0:
+                for n in batch[:-1]:
+                    add_sigmoid(n)
+            for r in range(outputs, due):
+                add("scalar", ("output", r), output_sigmoid, r, after=[("bias", r)])
+            outputs = due
+            if i > 0:
+                for n in batch[-1:]:
+                    add_sigmoid(n)
+            for n in batch:
+                add("scalar", ("logarithm", n), logarithm, n)
 
-        heads = {e: 0 for e in streams}
+        written = set()
+        position = {engine: 0 for engine in lists}
         moved = True
         while moved:
             moved = False
-            for e in streams:
-                while heads[e] < len(streams[e]):
-                    key, fn, args, needs = streams[e][heads[e]]
-                    if not all(k in done for k in needs):
+            for engine, entries in lists.items():
+                while position[engine] < len(entries):
+                    name, call, arguments, after = entries[position[engine]]
+                    if not all(needed in written for needed in after):
                         break
-                    fn(*args)
-                    done.add(key)
-                    heads[e] += 1
+                    call(*arguments)
+                    written.add(name)
+                    position[engine] += 1
                     moved = True
-        stuck = [(e, streams[e][heads[e]][0], [k for k in streams[e][heads[e]][3] if k not in done]) for e in streams if heads[e] < len(streams[e])]
-        assert not stuck, str(stuck)
+        assert all(position[engine] == len(lists[engine]) for engine in lists), "a list waits for itself"

@@ -48,7 +48,7 @@ EARLY_PIECES = 2 + COPIES_A_STEP * FIRST_BATCH
 LATE_LEAD = 2 * FIRST_BATCH
 D3_STEP = PRODUCT_LAG - 1
 
-DUMMIES = BACK_LAG - TURN_LAG
+DUMMY_PAIRS = (BACK_LAG - TURN_LAG) // 2
 
 LN_FLOOR = 2.0**-60
 
@@ -257,7 +257,7 @@ def tile_autoencoder_pb_t_kernel(tc, h_dec1, D2, g4, b4, D3, bo, out):
             banks = []
             for j in range(2):
                 bank = psum_turn.tile([P, 2, PAIR], F32, tag="bank", name="zt")
-                if j == 0 and 2 * n + g < DUMMIES:
+                if j == 0 and 1 <= n < DUMMY_PAIRS:
                     dummy_product(bank[:, 0, :])
                 for e in range(2):
                     c = PACK * g + 2 * j + e
@@ -423,8 +423,10 @@ def tile_autoencoder_pb_t_kernel(tc, h_dec1, D2, g4, b4, D3, bo, out):
             add_quantise(piece)
         add_turn(x_pieces[1])
         add_group(x_pieces[1], "scalar")
-        for r in range(2):
-            add("tensor", ("first", r), first_product, r, after=[("quantise", piece) for piece in head])
+        add("tensor", ("first", 0), first_product, 0, after=[("quantise", piece) for piece in head])
+        add_turn(x_pieces[2])
+        add_group(x_pieces[2], "scalar")
+        add("tensor", ("first", 1), first_product, 1)
         free = bank_free("turn", ("keep", "gb"))
         add("tensor", ("turn", "gb"), turn_gain_and_bias, after=[("load", "gb")] + free)
 
@@ -496,7 +498,7 @@ def tile_autoencoder_pb_t_kernel(tc, h_dec1, D2, g4, b4, D3, bo, out):
                     add_quantise_hidden(r // 2)
                 free = bank_free("out", ("bias", r)) + bank_free("out", ("bias", r))
                 add_second_product(r, psum_out, "bank", free)
-            first = 2 + COPIES_A_STEP * s
+            first = 3 + COPIES_A_STEP * s
             for piece in x_pieces[first : min(first + COPIES_A_STEP, EARLY_PIECES)]:
                 add_turn(piece)
                 add_group(piece, "scalar")
@@ -521,10 +523,8 @@ def tile_autoencoder_pb_t_kernel(tc, h_dec1, D2, g4, b4, D3, bo, out):
                     add_bias(earlier)
                 held = []
             if r % 2 == 0:
-                stop = min(r + 4, last if r < last else ROW_TILES)
-                for product in range(products, stop):
+                for product in range(max(products, r), r + 2):
                     add_product(product)
-                products = max(products, stop)
                 add_quantise_hidden(r // 2)
             pool, tag = places[(r - rest) % 4]
             needs = [("normalise", ROW_TILES - 1), ("gain", 2 * PAIRS - 1)]

from contextlib import ExitStack

import concourse.mybir as mybir
from concourse.masks import make_identity

F32 = mybir.dt.float32
BF16 = mybir.dt.bfloat16
U32 = mybir.dt.uint32
U8 = mybir.dt.uint8
FP8X4 = mybir.dt.float8_e4m3fn_x4
ALU = mybir.AluOpType
FUNC = mybir.ActivationFunctionType

P = 128
PACK = 4
ROWS, K_IN, HIDDEN, K_OUT = 4096, 512, 1024, 768
EPS = 1e-5
BANK = 512

ROW_TILES = ROWS // P
CHUNKS = HIDDEN // P
PASSES = HIDDEN // (P * PACK)
PAIR = 2 * P
PAIRS = ROWS // PAIR
D2_PIECES = HIDDEN // PAIR
D3_TILES = K_OUT // P

FIRST_BATCH, BATCH = 4, 3
BATCHES = (FIRST_BATCH,) + (BATCH,) * ((PAIRS - FIRST_BATCH) // BATCH)
N_BATCHES = len(BATCHES)
START = [sum(BATCHES[:i]) for i in range(N_BATCHES + 1)]

V_BUFS = FIRST_BATCH + BATCH
Q_BUFS = 2 * BATCH
Z_BUFS = 4
RAW_BUFS = 6
EARLY_BUFS = 6
LATE_BUFS = 2
Y_BUFS = 11

TURN_LAG = 3
PRODUCT_LAG = 2 * V_BUFS + 1
BACK_LAG = PRODUCT_LAG + D3_TILES
H_BUFS = (BACK_LAG - PRODUCT_LAG) // 2 + 1

COPIES_A_STEP = 2
EARLY_PIECES = 2 + COPIES_A_STEP * FIRST_BATCH
LATE_LEAD = 2 * FIRST_BATCH
D3_STEP = PRODUCT_LAG - 1

DUMMY_PAIRS = (BACK_LAG - TURN_LAG) // 2

LN_FLOOR = 2.0**-60

FLOPS = 2 * ROWS * K_IN * HIDDEN + 2 * ROWS * HIDDEN * K_OUT


def tile_autoencoder_pb_t_kernel(tc, h_dec1, D2, g4, b4, D3, bo, out):
    nc = tc.nc
    with ExitStack() as stack:
        const = stack.enter_context(tc.tile_pool(name="const", bufs=1))
        raw_pool = stack.enter_context(tc.tile_pool(name="raw", bufs=RAW_BUFS))
        early_pool = stack.enter_context(tc.tile_pool(name="early", bufs=EARLY_BUFS))
        late_pool = stack.enter_context(tc.tile_pool(name="late", bufs=LATE_BUFS))
        small = stack.enter_context(tc.tile_pool(name="small", bufs=4))
        z_pool = stack.enter_context(tc.tile_pool(name="z", bufs=Z_BUFS))
        v_pool = stack.enter_context(tc.tile_pool(name="v", bufs=V_BUFS))
        q_pool = stack.enter_context(tc.tile_pool(name="q", bufs=Q_BUFS))
        h_pool = stack.enter_context(tc.tile_pool(name="h", bufs=H_BUFS))
        word_pool = stack.enter_context(tc.tile_pool(name="words", bufs=2))
        y_pool = stack.enter_context(tc.tile_pool(name="y", bufs=Y_BUFS))
        psum_u = stack.enter_context(tc.psum_pool(name="psum_u", bufs=4))
        psum_turn = stack.enter_context(tc.psum_pool(name="psum_turn", bufs=2))
        psum_out = stack.enter_context(tc.psum_pool(name="psum_out", bufs=2))
        stack.enter_context(tc.manual_schedule())

        ident_f32 = const.tile([P, P], F32)
        make_identity(nc, ident_f32[:])
        ident_bf16 = const.tile([P, P], BF16)
        make_identity(nc, ident_bf16[:])
        minus_half = const.tile([P, 1], F32)
        nc.vector.memset(minus_half[:], -0.5)
        ln_floor = const.tile([P, 1], F32)
        nc.vector.memset(ln_floor[:], LN_FLOOR)
        ones = const.tile([P, PAIR], F32)
        nc.vector.memset(ones[:], 1.0)
        table_in = const.tile([P, 1], F32)
        nc.vector.memset(table_in[:], 0.0)
        table_out = const.tile([P, 1], F32)
        gb_rows = const.tile([P, P], BF16)
        nc.vector.memset(gb_rows[:], 0.0)
        gain_bias = const.tile([P, 2 * CHUNKS], F32)
        bo_rows = const.tile([P, K_OUT], BF16)
        x_words = const.tile([P, ROWS], U32, align_bytes=64)
        x_scales = const.tile([P, ROWS], U8, align_bytes=64)
        d2_words = const.tile([P, HIDDEN], U32, align_bytes=64)
        d2_scales = const.tile([P, HIDDEN], U8, align_bytes=64)
        d3_words = const.tile([P, PASSES, K_OUT], U32, align_bytes=64)
        d3_scales = const.tile([P, PASSES, K_OUT], U8, align_bytes=64)

        def load_sigmoid_table():
            nc.scalar.activation(out=table_out[:], in_=table_in[:], func=FUNC.Sigmoid)

        load_sigmoid_table()

        raw = {}
        turned = {}
        grouped = {}

        def load(piece):
            kind, n = piece
            tile = raw_pool.tile([P, 2 * K_IN], BF16, name="raw")
            if kind == "d3":
                nc.sync.dma_start(out=tile[:], in_=D3[P * n : P * (n + 1), :])
            else:
                rows = slice(PAIR * n, PAIR * (n + 1))
                source = h_dec1[rows, :] if kind == "x" else D2[rows, :]
                nc.sync.dma_start(
                    out=tile[:].rearrange("p (a k) -> p a k", a=2),
                    in_=source.rearrange("(a p) k -> p a k", p=P),
                )
            raw[piece] = tile

        def load_gain_and_bias():
            for vector, first in ((g4, 0), (b4, CHUNKS)):
                nc.sync.dma_start(out=gb_rows[first : first + CHUNKS, :], in_=vector.rearrange("(c p) -> c p", p=P))

        def load_output_bias():
            nc.sync.dma_start(out=bo_rows[:], in_=bo.partition_broadcast(P))

        def turn(piece, pool):
            kind, n = piece
            if kind == "d3":
                bank = pool.tile([P, CHUNKS, P], BF16, tag="bank", name="turned3")
                for c in range(CHUNKS):
                    nc.tensor.transpose(
                        out=bank[:, c, :], in_=raw[piece][:, P * c : P * (c + 1)], identity=ident_bf16[:]
                    )
            else:
                twos = raw[piece][:].bitcast(F32)
                bank = pool.tile([P, 2, PAIR], F32, tag="bank", name="turned")
                for u in range(2):
                    for a in range(2):
                        first = (K_IN // 2) * a + P * u
                        nc.tensor.transpose(
                            out=bank[:, u, P * a : P * (a + 1)],
                            in_=twos[:, first : first + P],
                            identity=ident_f32[:],
                        )
            turned[piece] = bank

        def group(piece, engine):
            kind, n = piece
            pool = early_pool if piece in early else late_pool
            if kind == "d3":
                tile = pool.tile([P, PASSES, P, PACK], BF16, align_bytes=64, tag="grouped", name="grouped3")
                to, source = tile[:], turned[piece][:].rearrange("p (g t) r -> p g r t", t=PACK)
            else:
                tile = pool.tile([P, PAIR * PACK], BF16, align_bytes=64, tag="grouped", name="grouped")
                to = tile[:].bitcast(F32).rearrange("p (r u) -> p r u", u=2)
                source = turned[piece][:].rearrange("p u r -> p r u")
            if engine == "scalar":
                nc.scalar.copy(out=to, in_=source)
            else:
                nc.vector.tensor_copy(out=to, in_=source)
            grouped[piece] = tile

        def quantise(piece):
            kind, n = piece
            if kind == "d3":
                cols = slice(P * n, P * (n + 1))
                for g in range(PASSES):
                    nc.vector.quantize_mx(
                        out=d3_words[:, g, cols].bitcast(FP8X4),
                        scales=d3_scales[:, g, cols],
                        in_=grouped[piece][:, g].rearrange("p r t -> p (r t)"),
                    )
            else:
                cols = slice(PAIR * n, PAIR * (n + 1))
                words, scales = (x_words, x_scales) if kind == "x" else (d2_words, d2_scales)
                nc.vector.quantize_mx(out=words[:, cols].bitcast(FP8X4), scales=scales[:, cols], in_=grouped[piece][:])

        def turn_gain_and_bias():
            bank = psum_turn.tile([P, P], BF16, tag="bank", name="turned_gb")
            nc.tensor.transpose(out=bank[:], in_=gb_rows[:], identity=ident_bf16[:])
            turned["gb"] = bank

        def keep_gain_and_bias():
            nc.vector.tensor_copy(out=gain_bias[:], in_=turned["gb"][:, 0 : 2 * CHUNKS])

        u_banks = {}
        stats = {}
        mean_var = {}
        rstd = {}
        z_tiles = {}
        z_turned = {}
        v_tiles = {}

        def dummy_product(columns):
            nc.tensor.matmul(out=columns, lhsT=ident_f32[:], rhs=ones[:], start=True, stop=True)

        def warm_up():
            bank = psum_turn.tile([P, 2, PAIR], F32, tag="bank", name="warm")
            for e in range(2):
                dummy_product(bank[:, e, :])

        def first_product(r):
            rows = slice(P * r, P * (r + 1))
            banks = []
            for half in range(HIDDEN // BANK):
                hidden = slice(BANK * half, BANK * (half + 1))
                u = psum_u.tile([P, BANK], F32, tag="u", name="u")
                nc.tensor.matmul_mx(
                    out=u[:],
                    lhsT=x_words[:, rows].bitcast(FP8X4),
                    lhsT_scale=x_scales[:, rows],
                    rhs=d2_words[:, hidden].bitcast(FP8X4),
                    rhs_scale=d2_scales[:, hidden],
                    start=True,
                    stop=True,
                )
                banks.append(u)
            u_banks[r] = banks

        def bank_statistics(r):
            tile = small.tile([P, 2, 6], F32, name="stats")
            for half in range(2):
                nc.vector.bn_stats(out=tile[:, half, :], in_=u_banks[r][half][:])
            stats[r] = tile

        def row_moments(r):
            tile = small.tile([P, 2], F32, name="mean_var")
            nc.vector.bn_aggr(out=tile[:], in_=stats[r][:].rearrange("p a s -> p (a s)"))
            mean_var[r] = tile

        def reciprocal_deviation(r):
            var_eps = small.tile([P, 1], F32, name="var_eps")
            nc.gpsimd.tensor_scalar_add(out=var_eps[:], in0=mean_var[r][:, 1:2], scalar1=EPS)
            tile = small.tile([P, 1], F32, name="rstd")
            nc.gpsimd.tensor_tensor(out=tile[:], in0=var_eps[:], in1=minus_half[:], op=ALU.pow)
            rstd[r] = tile

        def normalise(r):
            z = z_pool.tile([P, HIDDEN], F32, name="z")
            for half in range(2):
                nc.vector.tensor_scalar(
                    out=z[:, BANK * half : BANK * (half + 1)],
                    in0=u_banks[r][half][:],
                    scalar1=mean_var[r][:, 0:1],
                    scalar2=rstd[r][:],
                    op0=ALU.subtract,
                    op1=ALU.mult,
                )
            z_tiles[r] = z

        def turn_hidden(n, g):
            banks = []
            for j in range(2):
                bank = psum_turn.tile([P, 2, PAIR], F32, tag="bank", name="zt")
                if j == 0 and 1 <= n < DUMMY_PAIRS:
                    dummy_product(bank[:, 0, :])
                for e in range(2):
                    c = PACK * g + 2 * j + e
                    for a in range(2):
                        nc.tensor.transpose(
                            out=bank[:, e, P * a : P * (a + 1)],
                            in_=z_tiles[2 * n + a][:, P * c : P * (c + 1)],
                            identity=ident_f32[:],
                        )
                banks.append(bank)
            z_turned[(n, g)] = banks

        def gain_and_bias(n, g):
            if g == 0:
                v = v_pool.tile([P, CHUNKS, PAIR], F32, name="v")
                v_tiles[n] = v
            for j in range(2):
                for e in range(2):
                    c = PACK * g + 2 * j + e
                    gain, bias = gain_bias[:, c : c + 1], gain_bias[:, CHUNKS + c : CHUNKS + c + 1]
                    to, source = v_tiles[n][:, c, :], z_turned[(n, g)][j][:, e, :]
                    if n < FIRST_BATCH:
                        nc.scalar.activation(out=to, in_=source, func=FUNC.Identity, scale=gain, bias=bias)
                    else:
                        nc.vector.tensor_scalar(
                            out=to, in0=source, scalar1=gain, scalar2=bias, op0=ALU.mult, op1=ALU.add
                        )

        q_tiles = {}
        h_tiles = {}

        def sigmoid_of_minus(n):
            q = q_pool.tile([P, CHUNKS, PAIR], F32, name="q")
            nc.scalar.activation(out=q[:], in_=v_tiles[n][:], func=FUNC.Sigmoid, scale=-1.0)
            q_tiles[n] = q

        def logarithm(n):
            nc.scalar.activation(out=q_tiles[n][:], in_=q_tiles[n][:], func=FUNC.Ln, bias=ln_floor[:])

        def tanh_of_minus(n):
            nc.scalar.activation(out=q_tiles[n][:], in_=q_tiles[n][:], func=FUNC.Tanh, scale=-1.0)

        def product_on_vector(r):
            return r >= 2 * START[N_BATCHES - 1] and r % 2 == 1

        def mish_product(r):
            n, a = r // 2, r % 2
            if n not in h_tiles:
                h = h_pool.tile([P, 2, PASSES, P, PACK], BF16, align_bytes=64, name="h")
                h_tiles[n] = h
            rows = slice(P * a, P * (a + 1))
            engine = nc.vector if product_on_vector(r) else nc.gpsimd
            for g in range(PASSES):
                chunks = slice(PACK * g, PACK * (g + 1))
                engine.tensor_tensor(
                    out=h_tiles[n][:, a, g].rearrange("p (c i) t -> p c t i", i=4),
                    in0=v_tiles[n][:, chunks, rows].rearrange("p t (c i) -> p c t i", i=4),
                    in1=q_tiles[n][:, chunks, rows].rearrange("p t (c i) -> p c t i", i=4),
                    op=ALU.mult,
                )

        h_operands = {}
        out_banks = {}
        y_tiles = {}

        def quantise_hidden(n):
            words = word_pool.tile([P, 2 * PASSES * P], U32, align_bytes=64, name="h_words")
            scales = word_pool.tile([P, 2 * PASSES * P], U8, align_bytes=64, name="h_scales")
            nc.vector.quantize_mx(
                out=words[:].bitcast(FP8X4), scales=scales[:], in_=h_tiles[n][:].rearrange("p a g r t -> p (a g r t)")
            )
            h_operands[n] = (words, scales)

        def second_product(r, pool, tag):
            words, scales = h_operands[r // 2]
            wide = pool.tile([P, BANK], F32, tag=tag, name="wide")
            narrow = pool.tile([P, K_OUT - BANK], F32, tag=tag, name="narrow")
            for bank, lo, hi in ((wide, 0, BANK), (narrow, BANK, K_OUT)):
                for g in range(PASSES):
                    first = P * (PASSES * (r % 2) + g)
                    rows = slice(first, first + P)
                    nc.tensor.matmul_mx(
                        out=bank[:],
                        lhsT=words[:, rows].bitcast(FP8X4),
                        lhsT_scale=scales[:, rows],
                        rhs=d3_words[:, g, lo:hi].bitcast(FP8X4),
                        rhs_scale=d3_scales[:, g, lo:hi],
                        start=(g == 0),
                        stop=(g == PASSES - 1),
                    )
            out_banks[r] = (wide, narrow)

        def add_output_bias(r):
            wide, narrow = out_banks[r]
            y = y_pool.tile([P, K_OUT], F32, name="y")
            nc.vector.tensor_tensor(out=y[:, 0:BANK], in0=wide[:], in1=bo_rows[:, 0:BANK], op=ALU.add)
            nc.vector.tensor_tensor(out=y[:, BANK:K_OUT], in0=narrow[:], in1=bo_rows[:, BANK:K_OUT], op=ALU.add)
            y_tiles[r] = y

        def output_sigmoid(r):
            y = y_tiles[r]
            nc.scalar.activation(out=y[:], in_=y[:], func=FUNC.Sigmoid)
            nc.sync.dma_start(out=out[P * r : P * (r + 1), :], in_=y[:])

        lists = {"sync": [], "tensor": [], "scalar": [], "vector": [], "gpsimd": []}

        def add(engine, name, call, *arguments, after=()):
            lists[engine].append((name, call, arguments, tuple(after)))

        bank_readers = {"turn": [], "out": []}

        def bank_free(pool, reader):
            bank_readers[pool].append(reader)
            return bank_readers[pool][-3:-2]

        x_pieces = [("x", n) for n in range(PAIRS)]
        d2_pieces = [("d2", n) for n in range(D2_PIECES)]
        d3_pieces = [("d3", n) for n in range(D3_TILES)]
        head = x_pieces[:1] + d2_pieces
        early = head + x_pieces[1:EARLY_PIECES]
        late_step = {("x", n): 2 * n - LATE_LEAD for n in range(EARLY_PIECES, PAIRS)}
        late_step.update({("d3", n): D3_STEP + n for n in range(D3_TILES)})
        late = [piece for s in range(ROW_TILES) for piece in x_pieces + d3_pieces if late_step.get(piece) == s]
        pieces = early + late

        def add_turn(piece):
            k = pieces.index(piece)
            if k < len(head) and k % 2 == 1:
                free = bank_free("turn", ("group", piece))
                add("tensor", ("turn", piece), turn, piece, psum_turn, after=[("load", piece)] + free)
            else:
                free = bank_free("out", ("group", piece))
                add("tensor", ("turn", piece), turn, piece, psum_out, after=[("load", piece)] + free)

        def add_group(piece, engine):
            line, bufs = (early, EARLY_BUFS) if piece in early else (late, LATE_BUFS)
            k = line.index(piece)
            free = [("quantise", line[k - bufs])] if k >= bufs else []
            add(engine, ("group", piece), group, piece, engine, after=[("turn", piece)] + free)

        def add_quantise(piece):
            add("vector", ("quantise", piece), quantise, piece, after=[("group", piece)])

        for k, piece in enumerate(pieces):
            free = [("turn", pieces[k - RAW_BUFS])] if k >= RAW_BUFS else []
            add("sync", ("load", piece), load, piece, after=free)
            if piece == x_pieces[2]:
                add("sync", ("load", "gb"), load_gain_and_bias)
            if piece == early[-1]:
                add("sync", ("load", "bo"), load_output_bias)

        add("tensor", ("warm up",), warm_up)
        bank_readers["turn"].append(("warm up",))
        for piece in head:
            add_turn(piece)
        for k in range(0, len(head), 2):
            add_group(head[k], "scalar")
        add_group(head[1], "vector")
        add_quantise(head[0])
        add_quantise(head[1])
        add_group(head[3], "vector")
        for piece in head[2:]:
            add_quantise(piece)
        add_turn(x_pieces[1])
        add_group(x_pieces[1], "scalar")
        add("tensor", ("first", 0), first_product, 0, after=[("quantise", piece) for piece in head])
        add_turn(x_pieces[2])
        add_group(x_pieces[2], "scalar")
        add("tensor", ("first", 1), first_product, 1)
        free = bank_free("turn", ("keep", "gb"))
        add("tensor", ("turn", "gb"), turn_gain_and_bias, after=[("load", "gb")] + free)

        def add_turn_hidden(half):
            n, g = half // 2, half % 2
            free = [("gain", half - 1)] if half else [("keep", "gb")]
            add("tensor", ("turn z", half), turn_hidden, n, g, after=[("normalise", 2 * n + 1)] + free)

        def add_gain_and_bias(half, engine):
            n, g = half // 2, half % 2
            free = [("product", 2 * (n - V_BUFS) + 1)] if n >= V_BUFS else []
            add(engine, ("gain", half), gain_and_bias, n, g, after=[("turn z", half)] + free)

        def add_sigmoid(n):
            free = [("product", 2 * (n - Q_BUFS) + 1)] if n >= Q_BUFS else []
            add("scalar", ("sigmoid", n), sigmoid_of_minus, n, after=[("gain", 2 * n + 1)] + free)

        def add_product(r):
            n = r // 2
            free = [("quantise h", n - H_BUFS)] if n >= H_BUFS else []
            engine = "vector" if product_on_vector(r) else "gpsimd"
            add(engine, ("product", r), mish_product, r, after=[("tanh", n)] + free)

        def add_quantise_hidden(n):
            free = [("second", 2 * n - 3)] if n >= 2 else []
            add("vector", ("quantise h", n), quantise_hidden, n, after=[("product", 2 * n + 1)] + free)

        def add_second_product(r, pool, tag, free):
            needs = [("quantise h", r // 2)] + [("quantise", piece) for piece in d3_pieces]
            add("tensor", ("second", r), second_product, r, pool, tag, after=needs + free)

        def add_bias(r):
            free = [("output", r - Y_BUFS)] if r >= Y_BUFS else []
            add("vector", ("bias", r), add_output_bias, r, after=[("second", r), ("load", "bo")] + free)

        for s in range(ROW_TILES + TURN_LAG):
            if 0 <= s - PRODUCT_LAG < ROW_TILES:
                add_product(s - PRODUCT_LAG)
            half = s - TURN_LAG
            by_vector = 2 * FIRST_BATCH <= half
            if by_vector:
                add_turn_hidden(half)
            if s < ROW_TILES:
                add("vector", ("statistics", s), bank_statistics, s, after=[("first", s)])
            if 1 <= s <= ROW_TILES:
                free = [("turn z", s - 1 - Z_BUFS + (s % 2))] if s > Z_BUFS else []
                add("vector", ("normalise", s - 1), normalise, s - 1, after=[("deviation", s - 1)] + free)
            if s < ROW_TILES:
                add("vector", ("moments", s), row_moments, s)
                add("gpsimd", ("deviation", s), reciprocal_deviation, s, after=[("moments", s)])
            if s == 1:
                add("vector", ("keep", "gb"), keep_gain_and_bias, after=[("turn", "gb")])
            if 1 <= s < ROW_TILES - 1:
                needs = [("quantise", x_pieces[(s + 1) // 2]), ("normalise", s - 1)]
                add("tensor", ("first", s + 1), first_product, s + 1, after=needs)
            if 0 <= half + 1 < 2 * FIRST_BATCH:
                add_turn_hidden(half + 1)
                add_gain_and_bias(half + 1, "scalar")
                if (half + 1) % 2 == 1:
                    add_sigmoid((half + 1) // 2)
            now = [piece for piece in late if late_step[piece] == s]
            for piece in now:
                add_turn(piece)
            r = s - BACK_LAG
            if r >= 0:
                if r >= 1:
                    add_bias(r - 1)
                if r % 2 == 0:
                    add_quantise_hidden(r // 2)
                free = bank_free("out", ("bias", r)) + bank_free("out", ("bias", r))
                add_second_product(r, psum_out, "bank", free)
            first = 3 + COPIES_A_STEP * s
            for piece in x_pieces[first : min(first + COPIES_A_STEP, EARLY_PIECES)]:
                add_turn(piece)
                add_group(piece, "scalar")
            if by_vector:
                add_gain_and_bias(half, "vector")
            if s % 2 == 0 and (s + 2) // 2 < EARLY_PIECES:
                add_quantise(x_pieces[(s + 2) // 2])
            for piece in late:
                if late_step[piece] == s - 1:
                    add_quantise(piece)
            for piece in now:
                add_group(piece, "vector")

        places = ((psum_u, "u"), (psum_u, "u"), (psum_turn, "bank"), (psum_out, "bank"))
        rest = ROW_TILES + TURN_LAG - BACK_LAG
        last = 2 * START[N_BATCHES - 1]
        products = ROW_TILES + TURN_LAG - PRODUCT_LAG
        held = [rest - 1]
        for r in range(rest, ROW_TILES):
            if r == last:
                for earlier in held:
                    add_bias(earlier)
                held = []
            if r % 2 == 0:
                for product in range(max(products, r), r + 2):
                    add_product(product)
                add_quantise_hidden(r // 2)
            pool, tag = places[(r - rest) % 4]
            needs = [("normalise", ROW_TILES - 1), ("gain", 2 * PAIRS - 1)]
            free = [("bias", r - 4)] if r - rest >= 3 else []
            add_second_product(r, pool, tag, needs + free)
            if len(held) == 3:
                add_bias(held.pop(0))
            held.append(r)
        for r in held:
            add_bias(r)

        outputs = 0
        for i in range(N_BATCHES + 2):
            add("scalar", ("table", i), load_sigmoid_table)
            if 1 <= i <= N_BATCHES:
                for n in range(START[i - 1], START[i]):
                    add("scalar", ("tanh", n), tanh_of_minus, n)
            due = ROW_TILES
            if i < N_BATCHES:
                last_step = 2 * START[i + 1] - 1 + TURN_LAG
                due = max(0, last_step - BACK_LAG - 1)
                if i == N_BATCHES - 1:
                    due = rest + 2
            batch = list(range(START[i], START[i + 1])) if i < N_BATCHES else []
            if i > 0:
                for n in batch[:-1]:
                    add_sigmoid(n)
            for r in range(outputs, due):
                add("scalar", ("output", r), output_sigmoid, r, after=[("bias", r)])
            outputs = due
            if i > 0:
                for n in batch[-1:]:
                    add_sigmoid(n)
            for n in batch:
                add("scalar", ("logarithm", n), logarithm, n)

        written = set()
        position = {engine: 0 for engine in lists}
        moved = True
        while moved:
            moved = False
            for engine, entries in lists.items():
                while position[engine] < len(entries):
                    name, call, arguments, after = entries[position[engine]]
                    if not all(needed in written for needed in after):
                        break
                    call(*arguments)
                    written.add(name)
                    position[engine] += 1
                    moved = True
        assert all(position[engine] == len(lists[engine]) for engine in lists), "a list waits for itself"
